import numpy as np
import ml_dtypes


def mxq(x, axis, fmt="e4m3"):
    dtype, down = {"e4m3": (ml_dtypes.float8_e4m3fn, 7), "e5m2": (ml_dtypes.float8_e5m2, 14)}[fmt]
    v = np.moveaxis(np.asarray(x, np.float32).astype(ml_dtypes.bfloat16).astype(np.float64), axis, -1)
    blocks = v.reshape(v.shape[:-1] + (-1, 32))
    amax = np.abs(blocks).max(-1, keepdims=True)
    byte = np.maximum(np.where(amax > 0, np.frexp(amax)[1] - 1 + 127, 0) - down, 1)
    scale = np.exp2(byte - 127.0)
    codes = (blocks / scale).astype(np.float32).astype(dtype).astype(np.float64)
    return np.moveaxis((codes * scale).reshape(v.shape), -1, axis)


WIDE = False


def mx_kscale(k):
    if not WIDE:
        return np.ones(k)
    levels = np.array([10, -10, 5, -5, 0])
    a = np.random.permutation(np.resize(levels, k // 512 * 4)).reshape(k // 512, 4)
    idx = np.arange(k)
    return np.exp2(a[idx // 512, idx % 128 // 32])


BF16 = ml_dtypes.bfloat16


def bf(x):
    return np.asarray(x, np.float32).astype(BF16)


def f64(x):
    return np.asarray(x).astype(np.float64)


B, S, D, H, C = 1, 1024, 1024, 8, 512
DH = D // H
NB = S // C
NEG_INF = -1.0e9


def setup_inputs():
    s = mx_kscale(D)
    return {"q_proj": bf(np.random.standard_normal((B, S, D)) * np.sqrt(2.0)),
            "k_proj": bf(np.random.standard_normal((B, S, D)) * np.sqrt(2.0)),
            "x": bf(np.random.standard_normal((B, S, D)) * s),
            "w_v": bf(np.random.standard_normal((D, D)) * np.sqrt(2.0 / D) / s[:, None])}


def reference(q_proj, k_proj, x, w_v):
    q = f64(q_proj).reshape(B, S, H, DH).transpose(0, 2, 1, 3).reshape(B * H, S, DH)
    k = f64(k_proj).reshape(B, S, H, DH).transpose(0, 2, 3, 1).reshape(B * H, S, DH)
    v = mxq(f64(x), 2, "e4m3") @ mxq(f64(w_v), 0, "e4m3")
    v = v.reshape(B, S, H, DH).transpose(0, 2, 1, 3).reshape(B * H, S, DH)
    vq = mxq(v, 1, "e4m3")
    heads = np.zeros((B * H, S, DH))
    for r in range(NB):
        n = (r + 1) * C
        a = q[:, r * C:n] @ k[:, :n].transpose(0, 2, 1) / np.sqrt(DH)
        tril = (np.arange(n)[None, :] <= np.arange(r * C, n)[:, None]) * 1.0
        a = tril * a + NEG_INF * (1.0 - tril)
        e = np.exp(a - a.max(-1, keepdims=True))
        heads[:, r * C:n] = (mxq(e, 2, "e4m3") @ vq[:, :n]) / e.sum(-1, keepdims=True)
    return heads.reshape(B, H, S, DH).transpose(0, 2, 1, 3).reshape(B, S, D)

@@ -1,0 +1,271 @@
+from contextlib import ExitStack
+
+import concourse.mybir as mybir
+from concourse.masks import make_identity
+
+F32 = mybir.dt.float32
+BF16 = mybir.dt.bfloat16
+U32 = mybir.dt.uint32
+U8 = mybir.dt.uint8
+I32 = mybir.dt.int32
+FP8X4 = mybir.dt.float8_e4m3fn_x4
+ALU = mybir.AluOpType
+ACT = mybir.ActivationFunctionType
+AX = mybir.AxisListType
+
+P = 128
+S = 1024
+D = 1024
+H = 8
+SCALE = 128.0 ** -0.5
+NEG = -(2.0 ** 40)
+FLOPS = 2 * S * D * D + 2 * (2 * H * (512 * 512 + 512 * 1024) * 128)
+
+N_GE = 3
+V_EXIT_HEADS = (1, 4, 6)
+
+
+def tile_multiheadselfattention_pa_kernel(tc, q_proj, k_proj, x, w_v, out):
+    nc = tc.nc
+    q2 = q_proj.rearrange("b s d -> (b s) d")
+    k2 = k_proj.rearrange("b s d -> (b s) d")
+    x2 = x.rearrange("b s d -> (b s) d")
+    o2 = out.rearrange("b s d -> (b s) d")
+
+    with ExitStack() as ctx:
+        const = ctx.enter_context(tc.tile_pool(name="const", bufs=1))
+        keep = ctx.enter_context(tc.tile_pool(name="keep", bufs=1))
+        stage = ctx.enter_context(tc.tile_pool(name="stage", bufs=3))
+        work = ctx.enter_context(tc.tile_pool(name="work", bufs=4))
+        small = ctx.enter_context(tc.tile_pool(name="small", bufs=6))
+        ps_sc = ctx.enter_context(tc.psum_pool(name="ps_sc", bufs=4))
+        ps_et = ctx.enter_context(tc.psum_pool(name="ps_et", bufs=2))
+        ps_pv = ctx.enter_context(tc.psum_pool(name="ps_pv", bufs=2))
+
+        x4 = []
+        for j in range(4):
+            xt_sb = keep.tile([P, 2048], BF16, name="x4_%d" % j)
+            nc.sync.dma_start(
+                out=xt_sb[:].rearrange("p (b k) -> p b k", b=2),
+                in_=x2[256 * j:256 * j + 256, :].rearrange("(b p) k -> p b k", p=P),
+            )
+            x4.append(xt_sb)
+        w_raw = keep.tile([P, 8, D], BF16, name="w_raw")
+        for cu in range(4):
+            nc.sync.dma_start(
+                out=w_raw[:, 2 * cu:2 * cu + 2, :],
+                in_=w_v[256 * cu:256 * cu + 256, :].rearrange("(p e) n -> p e n", e=2),
+            )
+        k_sb = keep.tile([P, 8, D], BF16, name="k_sb")
+        for j in range(4):
+            nc.sync.dma_start(
+                out=k_sb[:, 2 * j:2 * j + 2, :],
+                in_=k2[256 * j:256 * j + 256, :].rearrange("(m p) d -> p m d", p=P),
+            )
+        q_sb = {}
+        for ib in range(7, -1, -1):
+            q_t = keep.tile([P, D], BF16, name="q_sb_%d" % ib)
+            nc.sync.dma_start(out=q_t[:], in_=q2[P * ib:P * ib + P, :])
+            q_sb[ib] = q_t
+
+        ident_f = const.tile([P, P], F32, name="ident_f")
+        make_identity(nc, ident_f[:])
+        ident_b = const.tile([P, P], BF16, name="ident_b")
+        make_identity(nc, ident_b[:])
+        mask_f = const.tile([P, P], F32, name="mask_f")
+        nc.gpsimd.memset(mask_f[:], 0.0)
+        nc.gpsimd.affine_select(
+            out=mask_f[:], in_=mask_f[:], compare_op=ALU.is_ge, fill=NEG,
+            base=0, pattern=[[-1, P]], channel_multiplier=1,
+        )
+        mask_b = const.tile([P, P], BF16, name="mask_b")
+        nc.vector.tensor_copy(out=mask_b[:], in_=mask_f[:])
+        warm = const.tile([P, 2], F32, name="warm")
+        nc.vector.memset(warm[:], 0.0)
+        warm2 = const.tile([P, 2], F32, name="warm2")
+        nc.scalar.activation(out=warm2[:], in_=warm[:], func=ACT.Exp)
+        junk = const.tile([P, 512], BF16, name="junk")
+
+        ge_ring = {}
+        for kind in ("big", "small"):
+            for ibl in range(3):
+                ring = []
+                for r in range(N_GE):
+                    g_t = keep.tile([P, 1024], BF16, name="ge_%s%d_%d" % (kind, ibl, r), align_bytes=64)
+                    nc.vector.memset(g_t[:].bitcast(I32), 0)
+                    ring.append(g_t)
+                ge_ring[(kind, ibl)] = ring
+        ring = []
+        for r in range(N_GE):
+            g_t = keep.tile([P, 1024], BF16, name="ge_full_%d" % r, align_bytes=64)
+            ring.append(g_t)
+        ge_ring[("big", 3)] = ring
+        ge_ring[("small", 3)] = ring
+
+        x_codes = keep.tile([P, 8, 256], U32, name="x_codes", align_bytes=64)
+        x_scales = keep.tile([P, 8, 256], U8, name="x_scales", align_bytes=64)
+        for sb in range(8):
+            xw = x4[sb // 2][:].bitcast(F32)
+            xt = ps_sc.tile([P, 4, P], F32, name="xt", tag="sc")
+            for kw in range(4):
+                c0 = 512 * (sb % 2) + P * kw
+                nc.tensor.transpose(xt[:, kw, :], xw[:, c0:c0 + P], ident_f[:])
+            gx = stage.tile([P, 1024], BF16, name="gx", tag="gx", align_bytes=64)
+            nc.scalar.copy(
+                out=gx[:].bitcast(F32).rearrange("p (c s u) -> p c s u", c=2, u=2),
+                in_=xt[:].rearrange("p (c u) s -> p c s u", u=2),
+            )
+            nc.vector.quantize_mx(
+                out=x_codes[:, sb, :].bitcast(FP8X4), scales=x_scales[:, sb, :], in_=gx[:],
+            )
+
+        w_codes = keep.tile([P, 2, D], U32, name="w_codes", align_bytes=64)
+        w_scales = keep.tile([P, 2, D], U8, name="w_scales", align_bytes=64)
+        for half in range(2):
+            for c in range(2):
+                gw = stage.tile([P, 2048], BF16, name="gw", tag="gw", align_bytes=64)
+                n0 = 512 * half
+                nc.vector.tensor_copy(
+                    out=gw[:].rearrange("p (c i t) -> p c t i", i=4, t=4),
+                    in_=w_raw[:, 4 * c:4 * c + 4, n0:n0 + 512].rearrange("p t (c i) -> p c t i", i=4),
+                )
+                nc.vector.quantize_mx(
+                    out=w_codes[:, c, n0:n0 + 512].bitcast(FP8X4),
+                    scales=w_scales[:, c, n0:n0 + 512], in_=gw[:],
+                )
+
+        v_codes = keep.tile([P, H, 2, P], U32, name="v_codes", align_bytes=64)
+        v_scales = keep.tile([P, H, 2, P], U8, name="v_scales", align_bytes=64)
+        for h in range(H):
+            gv = stage.tile([P, 1024], BF16, name="gv", tag="gv", align_bytes=64)
+            for g in range(2):
+                vp = ps_sc.tile([P, 4, P], F32, name="vp", tag="sc")
+                for t in range(4):
+                    for c in range(2):
+                        nc.tensor.matmul_mx(
+                            out=vp[:, t, :],
+                            lhsT=x_codes[:, 4 * g + t, P * c:P * c + P].bitcast(FP8X4),
+                            lhsT_scale=x_scales[:, 4 * g + t, P * c:P * c + P],
+                            rhs=w_codes[:, c, P * h:P * h + P].bitcast(FP8X4),
+                            rhs_scale=w_scales[:, c, P * h:P * h + P],
+                            start=(c == 0), stop=(c == 1),
+                        )
+                nc.scalar.copy(
+                    out=gv[:, 512 * g:512 * g + 512].rearrange("p (c t) -> p c t", t=4),
+                    in_=vp[:].rearrange("p t c -> p c t"),
+                )
+            nc.vector.quantize_mx(
+                out=v_codes[:, h, :, :].rearrange("p g c -> p (g c)").bitcast(FP8X4),
+                scales=v_scales[:, h, :, :].rearrange("p g c -> p (g c)"), in_=gv[:],
+            )
+
+        def q_transposes(ib):
+            qt = ps_et.tile([P, H, P], BF16, name="qt", tag="et")
+            for h in range(H):
+                nc.tensor.transpose(qt[:, h, :], q_sb[ib][:, P * h:P * h + P], ident_b[:])
+            q_T = work.tile([P, D], BF16, name="q_T", tag="q_T", bufs=2)
+            nc.scalar.copy(out=q_T[:], in_=qt[:].rearrange("p h i -> p (h i)"))
+            return q_T
+
+        q_T_next = q_transposes(7)
+        duo_count = 0
+        for ib in range(7, -1, -1):
+            q_T = q_T_next
+            big = ib >= 4
+            ibl = ib % 4
+            kind = "big" if big else "small"
+            if big:
+                duos = [[(h, 0), (h, 1)] for h in range(H)]
+            else:
+                duos = [[(2 * d, 0), (2 * d + 1, 0)] for d in range(4)]
+            pv = None
+            rs_q = None
+            for di, duo in enumerate(duos):
+                if duo[0][0] % 4 == 0:
+                    pv = ps_pv.tile([P, 4, P], F32, name="pv", tag="pv")
+                    rs_q = small.tile([P, 4, 2], F32, name="rs_q", tag="rs_q")
+                banks = []
+                nms = []
+                nm = None
+                for si, (h, g) in enumerate(duo):
+                    diag = (g == ib // 4)
+                    nblk = (ibl + 1) if diag else 4
+                    ncol = P * nblk
+                    sc = ps_sc.tile([P, 512], F32, name="sc", tag="sc")
+                    nc.tensor.matmul(
+                        out=sc[:, 0:ncol].rearrange("p (d m) -> p m d", m=8),
+                        lhsT=q_T[:, P * h:P * h + P],
+                        rhs=k_sb[:, :, P * h + 64 * g:P * h + 64 * g + ncol // 8],
+                        start=True, stop=(not diag),
+                    )
+                    if diag:
+                        nc.tensor.matmul(
+                            out=sc[:, P * ibl:P * ibl + P], lhsT=ident_b[:], rhs=mask_b[:],
+                            start=False, stop=True,
+                        )
+                    chained = big and si == 1
+                    if not chained:
+                        nm = small.tile([P, 2], F32, name="nm", tag="nm")
+                    nc.vector.tensor_scalar(
+                        out=junk[:, 0:ncol], in0=sc[:, 0:ncol], scalar1=-SCALE,
+                        scalar2=(nm[:, 0:1] if chained else None),
+                        op0=ALU.mult, op1=ALU.min,
+                        accum_out=(nm[:, 1:2] if chained else nm[:, 0:1]),
+                    )
+                    banks.append((sc, ncol, nblk))
+                    nms.append(nm)
+                e_t = work.tile([P, 1024], BF16, name="e_t", tag="e_t")
+                for si, (h, g) in enumerate(duo):
+                    sc, ncol, nblk = banks[si]
+                    bias = nms[si][:, 1:2] if big else nms[si][:, 0:1]
+                    nc.scalar.activation(
+                        out=e_t[:, 512 * si:512 * si + ncol], in_=sc[:, 0:ncol], func=ACT.Exp,
+                        bias=bias, scale=SCALE, accum_out=rs_q[:, h % 4, g:g + 1],
+                    )
+                et = ps_et.tile([P, 8, P], BF16, name="et", tag="et")
+                ge = ge_ring[(kind, ibl)][duo_count % N_GE]
+                ge4 = ge[:].rearrange("p (s i t) -> p s i t", s=2, t=4)
+                for si, (h, g) in enumerate(duo):
+                    sc, ncol, nblk = banks[si]
+                    for t in range(nblk):
+                        c0 = 512 * si + P * t
+                        nc.tensor.transpose(et[:, 4 * si + t, :], e_t[:, c0:c0 + P], ident_b[:])
+                for si, (h, g) in enumerate(duo):
+                    sc, ncol, nblk = banks[si]
+                    src = et[:, 4 * si:4 * si + nblk, :].rearrange("p t i -> p i t")
+                    dst = ge4[:, si, :, 0:nblk]
+                    if g == ib // 4 and h in V_EXIT_HEADS:
+                        nc.vector.tensor_copy(out=dst, in_=src)
+                    else:
+                        nc.scalar.copy(out=dst, in_=src)
+                e_codes = work.tile([P, 256], U32, name="e_codes", tag="e_codes", align_bytes=64)
+                e_scales = work.tile([P, 256], U8, name="e_scales", tag="e_scales", align_bytes=64)
+                nc.vector.quantize_mx(out=e_codes[:].bitcast(FP8X4), scales=e_scales[:], in_=ge[:])
+                for si, (h, g) in enumerate(duo):
+                    nc.tensor.matmul_mx(
+                        out=pv[:, h % 4, :],
+                        lhsT=e_codes[:, P * si:P * si + P].bitcast(FP8X4),
+                        lhsT_scale=e_scales[:, P * si:P * si + P],
+                        rhs=v_codes[:, h, g, :].bitcast(FP8X4),
+                        rhs_scale=v_scales[:, h, g, :],
+                        start=(g == 0), stop=(g == ib // 4),
+                    )
+                duo_count += 1
+                last_h = duo[-1][0]
+                if last_h % 4 == 3:
+                    hq = last_h // 4
+                    rinv = small.tile([P, 4], F32, name="rinv", tag="rinv")
+                    if big:
+                        rsum = small.tile([P, 4], F32, name="rsum", tag="rsum")
+                        nc.vector.tensor_reduce(out=rsum[:], in_=rs_q[:], axis=AX.X, op=ALU.add)
+                        nc.vector.reciprocal(out=rinv[:], in_=rsum[:])
+                    else:
+                        nc.vector.reciprocal(out=rinv[:], in_=rs_q[:, :, 0])
+                    o_sb = work.tile([P, 512], F32, name="o_sb", tag="o_sb", bufs=3)
+                    nc.vector.tensor_tensor(
+                        out=o_sb[:].rearrange("p (h c) -> p h c", h=4), in0=pv[:],
+                        in1=rinv[:].unsqueeze(2).to_broadcast([P, 4, P]), op=ALU.mult,
+                    )
+                    nc.sync.dma_start(out=o2[P * ib:P * ib + P, 512 * hq:512 * hq + 512], in_=o_sb[:])
+                if di == len(duos) // 2 and ib > 0:
+                    q_T_next = q_transposes(ib - 1)

@@ -21,8 +21,7 @@ SCALE = 128.0 ** -0.5
 NEG = -(2.0 ** 40)
 FLOPS = 2 * S * D * D + 2 * (2 * H * (512 * 512 + 512 * 1024) * 128)
 
-N_GE = 3
-V_EXIT_HEADS = (1, 4, 6)
+N_GE = 2
 
 
 def tile_multiheadselfattention_pa_kernel(tc, q_proj, k_proj, x, w_v, out):
@@ -56,17 +55,17 @@ def tile_multiheadselfattention_pa_kernel(tc, q_proj, k_proj, x, w_v, out):
                 out=w_raw[:, 2 * cu:2 * cu + 2, :],
                 in_=w_v[256 * cu:256 * cu + 256, :].rearrange("(p e) n -> p e n", e=2),
             )
+        q_sb = {}
+        for ib in range(7, -1, -1):
+            q_t = keep.tile([P, D], BF16, name="q_sb_%d" % ib)
+            nc.sync.dma_start(out=q_t[:], in_=q2[P * ib:P * ib + P, :])
+            q_sb[ib] = q_t
         k_sb = keep.tile([P, 8, D], BF16, name="k_sb")
         for j in range(4):
             nc.sync.dma_start(
                 out=k_sb[:, 2 * j:2 * j + 2, :],
                 in_=k2[256 * j:256 * j + 256, :].rearrange("(m p) d -> p m d", p=P),
             )
-        q_sb = {}
-        for ib in range(7, -1, -1):
-            q_t = keep.tile([P, D], BF16, name="q_sb_%d" % ib)
-            nc.sync.dma_start(out=q_t[:], in_=q2[P * ib:P * ib + P, :])
-            q_sb[ib] = q_t
 
         ident_f = const.tile([P, P], F32, name="ident_f")
         make_identity(nc, ident_f[:])
@@ -84,7 +83,6 @@ def tile_multiheadselfattention_pa_kernel(tc, q_proj, k_proj, x, w_v, out):
         nc.vector.memset(warm[:], 0.0)
         warm2 = const.tile([P, 2], F32, name="warm2")
         nc.scalar.activation(out=warm2[:], in_=warm[:], func=ACT.Exp)
-        junk = const.tile([P, 512], BF16, name="junk")
 
         ge_ring = {}
         for kind in ("big", "small"):
@@ -92,7 +90,8 @@ def tile_multiheadselfattention_pa_kernel(tc, q_proj, k_proj, x, w_v, out):
                 ring = []
                 for r in range(N_GE):
                     g_t = keep.tile([P, 1024], BF16, name="ge_%s%d_%d" % (kind, ibl, r), align_bytes=64)
-                    nc.vector.memset(g_t[:].bitcast(I32), 0)
+                    first = 512 if kind == "big" else 0
+                    nc.vector.memset(g_t[:, first:1024].bitcast(I32), 0)
                     ring.append(g_t)
                 ge_ring[(kind, ibl)] = ring
         ring = []
@@ -123,12 +122,14 @@ def tile_multiheadselfattention_pa_kernel(tc, q_proj, k_proj, x, w_v, out):
         w_scales = keep.tile([P, 2, D], U8, name="w_scales", align_bytes=64)
         for half in range(2):
             for c in range(2):
-                gw = stage.tile([P, 2048], BF16, name="gw", tag="gw", align_bytes=64)
+                gw = stage.tile([P, 2048], BF16, name="gw", tag="gw", align_bytes=64, bufs=4)
                 n0 = 512 * half
-                nc.vector.tensor_copy(
-                    out=gw[:].rearrange("p (c i t) -> p c t i", i=4, t=4),
-                    in_=w_raw[:, 4 * c:4 * c + 4, n0:n0 + 512].rearrange("p t (c i) -> p c t i", i=4),
-                )
+                dst = gw[:].rearrange("p (c i t) -> p c t i", i=4, t=4)
+                src = w_raw[:, 4 * c:4 * c + 4, n0:n0 + 512].rearrange("p t (c i) -> p c t i", i=4)
+                if c == 0:
+                    nc.vector.tensor_copy(out=dst, in_=src)
+                else:
+                    nc.scalar.copy(out=dst, in_=src)
                 nc.vector.quantize_mx(
                     out=w_codes[:, c, n0:n0 + 512].bitcast(FP8X4),
                     scales=w_scales[:, c, n0:n0 + 512], in_=gw[:],
@@ -136,10 +137,13 @@ def tile_multiheadselfattention_pa_kernel(tc, q_proj, k_proj, x, w_v, out):
 
         v_codes = keep.tile([P, H, 2, P], U32, name="v_codes", align_bytes=64)
         v_scales = keep.tile([P, H, 2, P], U8, name="v_scales", align_bytes=64)
-        for h in range(H):
+        gvs = {}
+
+        def v_passes(h):
             gv = stage.tile([P, 1024], BF16, name="gv", tag="gv", align_bytes=64)
+            gvs[h] = gv
             for g in range(2):
-                vp = ps_sc.tile([P, 4, P], F32, name="vp", tag="sc")
+                vp = ps_pv.tile([P, 4, P], F32, name="vp", tag="pv")
                 for t in range(4):
                     for c in range(2):
                         nc.tensor.matmul_mx(
@@ -154,94 +158,145 @@ def tile_multiheadselfattention_pa_kernel(tc, q_proj, k_proj, x, w_v, out):
                     out=gv[:, 512 * g:512 * g + 512].rearrange("p (c t) -> p c t", t=4),
                     in_=vp[:].rearrange("p t c -> p c t"),
                 )
+
+        def v_quantise(h):
             nc.vector.quantize_mx(
                 out=v_codes[:, h, :, :].rearrange("p g c -> p (g c)").bitcast(FP8X4),
-                scales=v_scales[:, h, :, :].rearrange("p g c -> p (g c)"), in_=gv[:],
+                scales=v_scales[:, h, :, :].rearrange("p g c -> p (g c)"), in_=gvs[h][:],
             )
 
-        def q_transposes(ib):
+        for h in range(4):
+            v_passes(h)
+            v_quantise(h)
+
+        q_T = {}
+        for ib in range(7, -1, -1):
             qt = ps_et.tile([P, H, P], BF16, name="qt", tag="et")
             for h in range(H):
                 nc.tensor.transpose(qt[:, h, :], q_sb[ib][:, P * h:P * h + P], ident_b[:])
-            q_T = work.tile([P, D], BF16, name="q_T", tag="q_T", bufs=2)
-            nc.scalar.copy(out=q_T[:], in_=qt[:].rearrange("p h i -> p (h i)"))
-            return q_T
-
-        q_T_next = q_transposes(7)
-        duo_count = 0
-        for ib in range(7, -1, -1):
-            q_T = q_T_next
-            big = ib >= 4
-            ibl = ib % 4
-            kind = "big" if big else "small"
-            if big:
-                duos = [[(h, 0), (h, 1)] for h in range(H)]
+            q_Tt = keep.tile([P, D], BF16, name="q_T_%d" % ib)
+            if ib % 2:
+                nc.scalar.copy(out=q_Tt[:], in_=qt[:].rearrange("p h i -> p (h i)"))
             else:
-                duos = [[(2 * d, 0), (2 * d + 1, 0)] for d in range(4)]
-            pv = None
-            rs_q = None
-            for di, duo in enumerate(duos):
-                if duo[0][0] % 4 == 0:
-                    pv = ps_pv.tile([P, 4, P], F32, name="pv", tag="pv")
-                    rs_q = small.tile([P, 4, 2], F32, name="rs_q", tag="rs_q")
-                banks = []
-                nms = []
-                nm = None
-                for si, (h, g) in enumerate(duo):
-                    diag = (g == ib // 4)
-                    nblk = (ibl + 1) if diag else 4
-                    ncol = P * nblk
-                    sc = ps_sc.tile([P, 512], F32, name="sc", tag="sc")
+                nc.vector.tensor_copy(out=q_Tt[:], in_=qt[:].rearrange("p h i -> p (h i)"))
+            q_T[ib] = q_Tt
+
+        duos = []
+        for ib in range(7, -1, -1):
+            if ib >= 4:
+                for h in range(H):
+                    duos.append((ib, [(h, 0), (h, 1)]))
+            else:
+                for d in range(4):
+                    duos.append((ib, [(2 * d, 0), (2 * d + 1, 0)]))
+        n_duos = len(duos)
+        st = [dict() for n in range(n_duos)]
+        quad = {}
+
+        def blocks(ib, g):
+            return (ib % 4 + 1) if g == ib // 4 else 4
+
+        def on_vector(ib, h, g):
+            return ib >= 4 and g == 1 and h % 2 == 1
+
+        def qk(n):
+            ib, slots = duos[n]
+            st[n]["sc"] = []
+            for h, g in slots:
+                diag = (g == ib // 4)
+                ncol = P * blocks(ib, g)
+                sc = ps_sc.tile([P, 512], F32, name="sc", tag="sc")
+                nc.tensor.matmul(
+                    out=sc[:, 0:ncol].rearrange("p (d m) -> p m d", m=8),
+                    lhsT=q_T[ib][:, P * h:P * h + P],
+                    rhs=k_sb[:, :, P * h + 64 * g:P * h + 64 * g + ncol // 8],
+                    start=True, stop=(not diag),
+                )
+                if diag:
+                    c0 = P * (ib % 4)
                     nc.tensor.matmul(
-                        out=sc[:, 0:ncol].rearrange("p (d m) -> p m d", m=8),
-                        lhsT=q_T[:, P * h:P * h + P],
-                        rhs=k_sb[:, :, P * h + 64 * g:P * h + 64 * g + ncol // 8],
-                        start=True, stop=(not diag),
+                        out=sc[:, c0:c0 + P], lhsT=ident_b[:], rhs=mask_b[:], start=False, stop=True,
                     )
-                    if diag:
-                        nc.tensor.matmul(
-                            out=sc[:, P * ibl:P * ibl + P], lhsT=ident_b[:], rhs=mask_b[:],
-                            start=False, stop=True,
-                        )
-                    chained = big and si == 1
-                    if not chained:
-                        nm = small.tile([P, 2], F32, name="nm", tag="nm")
-                    nc.vector.tensor_scalar(
-                        out=junk[:, 0:ncol], in0=sc[:, 0:ncol], scalar1=-SCALE,
-                        scalar2=(nm[:, 0:1] if chained else None),
-                        op0=ALU.mult, op1=ALU.min,
-                        accum_out=(nm[:, 1:2] if chained else nm[:, 0:1]),
-                    )
-                    banks.append((sc, ncol, nblk))
-                    nms.append(nm)
-                e_t = work.tile([P, 1024], BF16, name="e_t", tag="e_t")
-                for si, (h, g) in enumerate(duo):
-                    sc, ncol, nblk = banks[si]
-                    bias = nms[si][:, 1:2] if big else nms[si][:, 0:1]
-                    nc.scalar.activation(
-                        out=e_t[:, 512 * si:512 * si + ncol], in_=sc[:, 0:ncol], func=ACT.Exp,
-                        bias=bias, scale=SCALE, accum_out=rs_q[:, h % 4, g:g + 1],
-                    )
-                et = ps_et.tile([P, 8, P], BF16, name="et", tag="et")
-                ge = ge_ring[(kind, ibl)][duo_count % N_GE]
-                ge4 = ge[:].rearrange("p (s i t) -> p s i t", s=2, t=4)
-                for si, (h, g) in enumerate(duo):
-                    sc, ncol, nblk = banks[si]
-                    for t in range(nblk):
-                        c0 = 512 * si + P * t
-                        nc.tensor.transpose(et[:, 4 * si + t, :], e_t[:, c0:c0 + P], ident_b[:])
-                for si, (h, g) in enumerate(duo):
-                    sc, ncol, nblk = banks[si]
-                    src = et[:, 4 * si:4 * si + nblk, :].rearrange("p t i -> p i t")
-                    dst = ge4[:, si, :, 0:nblk]
-                    if g == ib // 4 and h in V_EXIT_HEADS:
-                        nc.vector.tensor_copy(out=dst, in_=src)
-                    else:
-                        nc.scalar.copy(out=dst, in_=src)
-                e_codes = work.tile([P, 256], U32, name="e_codes", tag="e_codes", align_bytes=64)
-                e_scales = work.tile([P, 256], U8, name="e_scales", tag="e_scales", align_bytes=64)
-                nc.vector.quantize_mx(out=e_codes[:].bitcast(FP8X4), scales=e_scales[:], in_=ge[:])
-                for si, (h, g) in enumerate(duo):
+                st[n]["sc"].append(sc)
+
+        def row_max(n):
+            ib, slots = duos[n]
+            m2 = small.tile([P, 2], F32, name="m2", tag="m2")
+            nm = small.tile([P, 2], F32, name="nm", tag="nm")
+            for si, (h, g) in enumerate(slots):
+                ncol = P * blocks(ib, g)
+                nc.vector.tensor_reduce(out=m2[:, si:si + 1], in_=st[n]["sc"][si][:, 0:ncol], axis=AX.X, op=ALU.max)
+            if ib >= 4:
+                nc.vector.tensor_scalar(
+                    out=nm[:, 0:1], in0=m2[:, 0:1], scalar1=m2[:, 1:2], scalar2=-SCALE, op0=ALU.max, op1=ALU.mult,
+                )
+            else:
+                nc.vector.tensor_scalar(out=nm[:], in0=m2[:], scalar1=-SCALE, scalar2=None, op0=ALU.mult)
+            st[n]["nm"] = nm
+
+        def exps(n):
+            ib, slots = duos[n]
+            if slots[0][0] % 4 == 0:
+                quad[(ib, slots[0][0] // 4, "rs")] = small.tile([P, 4, 2], F32, name="rs_q", tag="rs_q")
+            e_t = work.tile([P, 1024], BF16, name="e_t", tag="e_t")
+            for si, (h, g) in enumerate(slots):
+                ncol = P * blocks(ib, g)
+                col = 0 if ib >= 4 else si
+                nc.scalar.activation(
+                    out=e_t[:, 512 * si:512 * si + ncol], in_=st[n]["sc"][si][:, 0:ncol], func=ACT.Exp,
+                    bias=st[n]["nm"][:, col:col + 1], scale=SCALE,
+                    accum_out=quad[(ib, h // 4, "rs")][:, h % 4, g:g + 1],
+                )
+            st[n]["e"] = e_t
+
+        def transposes(n):
+            ib, slots = duos[n]
+            et = ps_et.tile([P, 8, P], BF16, name="et", tag="et")
+            for si, (h, g) in enumerate(slots):
+                for t in range(blocks(ib, g)):
+                    c0 = 512 * si + P * t
+                    nc.tensor.transpose(et[:, 4 * si + t, :], st[n]["e"][:, c0:c0 + P], ident_b[:])
+            st[n]["et"] = et
+
+        def exits(n, vector_share):
+            ib, slots = duos[n]
+            ge = ge_ring[("big" if ib >= 4 else "small", ib % 4)][n % N_GE]
+            st[n]["ge"] = ge
+            ge4 = ge[:].rearrange("p (s i t) -> p s i t", s=2, t=4)
+            et = st[n]["et"]
+            if ib % 4 == 3 and not on_vector(ib, slots[1][0], slots[1][1]):
+                if not vector_share:
+                    nc.scalar.copy(out=ge4, in_=et[:].rearrange("p (s t) i -> p s i t", t=4))
+                return
+            for si, (h, g) in enumerate(slots):
+                if on_vector(ib, h, g) != vector_share:
+                    continue
+                nblk = blocks(ib, g)
+                src = et[:, 4 * si:4 * si + nblk, :].rearrange("p t i -> p i t")
+                dst = ge4[:, si, :, 0:nblk]
+                if vector_share:
+                    nc.vector.tensor_copy(out=dst, in_=src)
+                else:
+                    nc.scalar.copy(out=dst, in_=src)
+
+        def quantise(n):
+            e_codes = work.tile([P, 256], U32, name="e_codes", tag="e_codes", align_bytes=64, bufs=8)
+            e_scales = work.tile([P, 256], U8, name="e_scales", tag="e_scales", align_bytes=64, bufs=8)
+            nc.vector.quantize_mx(out=e_codes[:].bitcast(FP8X4), scales=e_scales[:], in_=st[n]["ge"][:])
+            st[n]["codes"] = (e_codes, e_scales)
+
+        def quad_end(n):
+            return 0 <= n < n_duos and duos[n][1][-1][0] % 4 == 3
+
+        def pv_passes(n_last):
+            ib, slots = duos[n_last]
+            hq = slots[-1][0] // 4
+            pv = ps_pv.tile([P, 4, P], F32, name="pv", tag="pv")
+            quad[(ib, hq, "pv")] = pv
+            n_first = n_last - (3 if ib >= 4 else 1)
+            for n in range(n_first, n_last + 1):
+                e_codes, e_scales = st[n]["codes"]
+                for si, (h, g) in enumerate(duos[n][1]):
                     nc.tensor.matmul_mx(
                         out=pv[:, h % 4, :],
                         lhsT=e_codes[:, P * si:P * si + P].bitcast(FP8X4),
@@ -250,22 +305,43 @@ def tile_multiheadselfattention_pa_kernel(tc, q_proj, k_proj, x, w_v, out):
                         rhs_scale=v_scales[:, h, g, :],
                         start=(g == 0), stop=(g == ib // 4),
                     )
-                duo_count += 1
-                last_h = duo[-1][0]
-                if last_h % 4 == 3:
-                    hq = last_h // 4
-                    rinv = small.tile([P, 4], F32, name="rinv", tag="rinv")
-                    if big:
-                        rsum = small.tile([P, 4], F32, name="rsum", tag="rsum")
-                        nc.vector.tensor_reduce(out=rsum[:], in_=rs_q[:], axis=AX.X, op=ALU.add)
-                        nc.vector.reciprocal(out=rinv[:], in_=rsum[:])
-                    else:
-                        nc.vector.reciprocal(out=rinv[:], in_=rs_q[:, :, 0])
-                    o_sb = work.tile([P, 512], F32, name="o_sb", tag="o_sb", bufs=3)
-                    nc.vector.tensor_tensor(
-                        out=o_sb[:].rearrange("p (h c) -> p h c", h=4), in0=pv[:],
-                        in1=rinv[:].unsqueeze(2).to_broadcast([P, 4, P]), op=ALU.mult,
-                    )
-                    nc.sync.dma_start(out=o2[P * ib:P * ib + P, 512 * hq:512 * hq + 512], in_=o_sb[:])
-                if di == len(duos) // 2 and ib > 0:
-                    q_T_next = q_transposes(ib - 1)
+
+        def finish(n):
+            ib, slots = duos[n]
+            hq = slots[-1][0] // 4
+            rs_q = quad[(ib, hq, "rs")]
+            rinv = small.tile([P, 4], F32, name="rinv", tag="rinv")
+            if ib >= 4:
+                rsum = small.tile([P, 4], F32, name="rsum", tag="rsum")
+                nc.vector.tensor_reduce(out=rsum[:], in_=rs_q[:], axis=AX.X, op=ALU.add)
+                nc.vector.reciprocal(out=rinv[:], in_=rsum[:])
+            else:
+                nc.vector.reciprocal(out=rinv[:], in_=rs_q[:, :, 0])
+            o_sb = work.tile([P, 512], F32, name="o_sb", tag="o_sb", bufs=3)
+            nc.vector.tensor_tensor(
+                out=o_sb[:].rearrange("p (h c) -> p h c", h=4), in0=quad[(ib, hq, "pv")][:],
+                in1=rinv[:].unsqueeze(2).to_broadcast([P, 4, P]), op=ALU.mult,
+            )
+            nc.sync.dma_start(out=o2[P * ib:P * ib + P, 512 * hq:512 * hq + 512], in_=o_sb[:])
+
+        def run(stage_fn, n, *more):
+            if 0 <= n < n_duos:
+                stage_fn(n, *more)
+
+        with tc.manual_schedule():
+            for k in range(-2, n_duos + 4):
+                run(exps, k)
+                run(exits, k - 2, True)
+                run(row_max, k + 1)
+                run(qk, k + 2)
+                run(transposes, k)
+                run(exits, k - 1, False)
+                if 0 <= k < 4:
+                    v_passes(4 + k)
+                run(quantise, k - 2)
+                if 1 <= k < 5:
+                    v_quantise(3 + k)
+                if quad_end(k - 2):
+                    pv_passes(k - 2)
+                if quad_end(k - 3):
+                    finish(k - 3)

@@ -89,14 +89,17 @@ def tile_multiheadselfattention_pa_kernel(tc, q_proj, k_proj, x, w_v, out):
             for ibl in range(3):
                 ring = []
                 for r in range(N_GE):
-                    g_t = keep.tile([P, 1024], BF16, name="ge_%s%d_%d" % (kind, ibl, r), align_bytes=64)
-                    first = 512 if kind == "big" else 0
-                    nc.vector.memset(g_t[:, first:1024].bitcast(I32), 0)
+                    g_t = keep.tile([P, 2048], BF16, name="ge_%s%d_%d" % (kind, ibl, r), align_bytes=64)
+                    words = g_t[:].bitcast(I32).rearrange("p (d s w) -> p d s w", d=2, s=2)
+                    if kind == "big":
+                        nc.vector.memset(words[:, :, 1, :], 0)
+                    else:
+                        nc.vector.memset(g_t[:].bitcast(I32), 0)
                     ring.append(g_t)
                 ge_ring[(kind, ibl)] = ring
         ring = []
         for r in range(N_GE):
-            g_t = keep.tile([P, 1024], BF16, name="ge_full_%d" % r, align_bytes=64)
+            g_t = keep.tile([P, 2048], BF16, name="ge_full_%d" % r, align_bytes=64)
             ring.append(g_t)
         ge_ring[("big", 3)] = ring
         ge_ring[("small", 3)] = ring
@@ -122,7 +125,7 @@ def tile_multiheadselfattention_pa_kernel(tc, q_proj, k_proj, x, w_v, out):
         w_scales = keep.tile([P, 2, D], U8, name="w_scales", align_bytes=64)
         for half in range(2):
             for c in range(2):
-                gw = stage.tile([P, 2048], BF16, name="gw", tag="gw", align_bytes=64, bufs=4)
+                gw = stage.tile([P, 2048], BF16, name="gw", tag="gw", align_bytes=64, bufs=2)
                 n0 = 512 * half
                 dst = gw[:].rearrange("p (c i t) -> p c t i", i=4, t=4)
                 src = w_raw[:, 4 * c:4 * c + 4, n0:n0 + 512].rearrange("p t (c i) -> p c t i", i=4)
@@ -175,10 +178,7 @@ def tile_multiheadselfattention_pa_kernel(tc, q_proj, k_proj, x, w_v, out):
             for h in range(H):
                 nc.tensor.transpose(qt[:, h, :], q_sb[ib][:, P * h:P * h + P], ident_b[:])
             q_Tt = keep.tile([P, D], BF16, name="q_T_%d" % ib)
-            if ib % 2:
-                nc.scalar.copy(out=q_Tt[:], in_=qt[:].rearrange("p h i -> p (h i)"))
-            else:
-                nc.vector.tensor_copy(out=q_Tt[:], in_=qt[:].rearrange("p h i -> p (h i)"))
+            nc.vector.tensor_copy(out=q_Tt[:], in_=qt[:].rearrange("p h i -> p (h i)"))
             q_T[ib] = q_Tt
 
         duos = []
@@ -195,9 +195,6 @@ def tile_multiheadselfattention_pa_kernel(tc, q_proj, k_proj, x, w_v, out):
 
         def blocks(ib, g):
             return (ib % 4 + 1) if g == ib // 4 else 4
-
-        def on_vector(ib, h, g):
-            return ib >= 4 and g == 1 and h % 2 == 1
 
         def qk(n):
             ib, slots = duos[n]
@@ -227,11 +224,11 @@ def tile_multiheadselfattention_pa_kernel(tc, q_proj, k_proj, x, w_v, out):
                 ncol = P * blocks(ib, g)
                 nc.vector.tensor_reduce(out=m2[:, si:si + 1], in_=st[n]["sc"][si][:, 0:ncol], axis=AX.X, op=ALU.max)
             if ib >= 4:
-                nc.vector.tensor_scalar(
+                nc.gpsimd.tensor_scalar(
                     out=nm[:, 0:1], in0=m2[:, 0:1], scalar1=m2[:, 1:2], scalar2=-SCALE, op0=ALU.max, op1=ALU.mult,
                 )
             else:
-                nc.vector.tensor_scalar(out=nm[:], in0=m2[:], scalar1=-SCALE, scalar2=None, op0=ALU.mult)
+                nc.gpsimd.tensor_scalar(out=nm[:], in0=m2[:], scalar1=-SCALE, scalar2=0.0, op0=ALU.mult, op1=ALU.add)
             st[n]["nm"] = nm
 
         def exps(n):
@@ -258,31 +255,50 @@ def tile_multiheadselfattention_pa_kernel(tc, q_proj, k_proj, x, w_v, out):
                     nc.tensor.transpose(et[:, 4 * si + t, :], st[n]["e"][:, c0:c0 + P], ident_b[:])
             st[n]["et"] = et
 
-        def exits(n, vector_share):
+        def grouped(n):
             ib, slots = duos[n]
-            ge = ge_ring[("big" if ib >= 4 else "small", ib % 4)][n % N_GE]
+            ge = ge_ring[("big" if ib >= 4 else "small", ib % 4)][(n // 2) % N_GE]
             st[n]["ge"] = ge
-            ge4 = ge[:].rearrange("p (s i t) -> p s i t", s=2, t=4)
-            et = st[n]["et"]
-            if ib % 4 == 3 and not on_vector(ib, slots[1][0], slots[1][1]):
-                if not vector_share:
-                    nc.scalar.copy(out=ge4, in_=et[:].rearrange("p (s t) i -> p s i t", t=4))
-                return
+            return ge[:, 1024 * (n % 2):1024 * (n % 2) + 1024].rearrange("p (s i t) -> p s i t", s=2, t=4)
+
+        def full_slots(n):
+            ib, slots = duos[n]
+            return [si for si, (h, g) in enumerate(slots) if blocks(ib, g) == 4]
+
+        def exits_partial(n):
+            ib, slots = duos[n]
+            ge4 = grouped(n)
             for si, (h, g) in enumerate(slots):
-                if on_vector(ib, h, g) != vector_share:
-                    continue
                 nblk = blocks(ib, g)
-                src = et[:, 4 * si:4 * si + nblk, :].rearrange("p t i -> p i t")
-                dst = ge4[:, si, :, 0:nblk]
-                if vector_share:
-                    nc.vector.tensor_copy(out=dst, in_=src)
-                else:
-                    nc.scalar.copy(out=dst, in_=src)
+                if nblk < 4:
+                    nc.scalar.copy(
+                        out=ge4[:, si, :, 0:nblk],
+                        in_=st[n]["et"][:, 4 * si:4 * si + nblk, :].rearrange("p t i -> p i t"),
+                    )
+
+        def exits_full(n):
+            full = full_slots(n)
+            if not full:
+                return
+            ge4 = grouped(n)
+            width = 512 * len(full)
+            stg = work.tile([P, 1024], BF16, name="stg", tag="stg", bufs=3)
+            nc.vector.tensor_copy(
+                out=stg[:, 0:width], in_=st[n]["et"][:, 0:4 * len(full), :].rearrange("p a i -> p (a i)"),
+            )
+            nc.gpsimd.tensor_scalar(
+                out=ge4[:, 0:len(full), :, :],
+                in0=stg[:, 0:width].rearrange("p (s t i) -> p s i t", t=4, i=P),
+                scalar1=1.0, scalar2=0.0, op0=ALU.mult, op1=ALU.add,
+            )
 
         def quantise(n):
-            e_codes = work.tile([P, 256], U32, name="e_codes", tag="e_codes", align_bytes=64, bufs=8)
-            e_scales = work.tile([P, 256], U8, name="e_scales", tag="e_scales", align_bytes=64, bufs=8)
+            if n % 2 == 0:
+                return
+            e_codes = work.tile([P, 512], U32, name="e_codes", tag="e_codes", align_bytes=64, bufs=4)
+            e_scales = work.tile([P, 512], U8, name="e_scales", tag="e_scales", align_bytes=64, bufs=4)
             nc.vector.quantize_mx(out=e_codes[:].bitcast(FP8X4), scales=e_scales[:], in_=st[n]["ge"][:])
+            st[n - 1]["codes"] = (e_codes, e_scales)
             st[n]["codes"] = (e_codes, e_scales)
 
         def quad_end(n):
@@ -299,29 +315,42 @@ def tile_multiheadselfattention_pa_kernel(tc, q_proj, k_proj, x, w_v, out):
                 for si, (h, g) in enumerate(duos[n][1]):
                     nc.tensor.matmul_mx(
                         out=pv[:, h % 4, :],
-                        lhsT=e_codes[:, P * si:P * si + P].bitcast(FP8X4),
-                        lhsT_scale=e_scales[:, P * si:P * si + P],
+                        lhsT=e_codes[:, 256 * (n % 2) + P * si:256 * (n % 2) + P * si + P].bitcast(FP8X4),
+                        lhsT_scale=e_scales[:, 256 * (n % 2) + P * si:256 * (n % 2) + P * si + P],
                         rhs=v_codes[:, h, g, :].bitcast(FP8X4),
                         rhs_scale=v_scales[:, h, g, :],
                         start=(g == 0), stop=(g == ib // 4),
                     )
 
+        def row_sums(n):
+            ib, slots = duos[n]
+            if ib >= 4:
+                hq = slots[-1][0] // 4
+                rs_q = quad[(ib, hq, "rs")]
+                rsum = small.tile([P, 4], F32, name="rsum", tag="rsum")
+                nc.gpsimd.tensor_tensor(out=rsum[:], in0=rs_q[:, :, 0], in1=rs_q[:, :, 1], op=ALU.add)
+                quad[(ib, hq, "rsum")] = rsum
+
+        def reciprocals(n):
+            ib, slots = duos[n]
+            hq = slots[-1][0] // 4
+            rinv = small.tile([P, 4], F32, name="rinv", tag="rinv")
+            if ib >= 4:
+                nc.vector.reciprocal(out=rinv[:], in_=quad[(ib, hq, "rsum")][:])
+            else:
+                nc.vector.reciprocal(out=rinv[:], in_=quad[(ib, hq, "rs")][:, :, 0])
+            quad[(ib, hq, "rinv")] = rinv
+
         def finish(n):
             ib, slots = duos[n]
             hq = slots[-1][0] // 4
-            rs_q = quad[(ib, hq, "rs")]
-            rinv = small.tile([P, 4], F32, name="rinv", tag="rinv")
-            if ib >= 4:
-                rsum = small.tile([P, 4], F32, name="rsum", tag="rsum")
-                nc.vector.tensor_reduce(out=rsum[:], in_=rs_q[:], axis=AX.X, op=ALU.add)
-                nc.vector.reciprocal(out=rinv[:], in_=rsum[:])
-            else:
-                nc.vector.reciprocal(out=rinv[:], in_=rs_q[:, :, 0])
+            rinv = quad[(ib, hq, "rinv")]
             o_sb = work.tile([P, 512], F32, name="o_sb", tag="o_sb", bufs=3)
-            nc.vector.tensor_tensor(
-                out=o_sb[:].rearrange("p (h c) -> p h c", h=4), in0=quad[(ib, hq, "pv")][:],
-                in1=rinv[:].unsqueeze(2).to_broadcast([P, 4, P]), op=ALU.mult,
-            )
+            for a in range(4):
+                nc.scalar.activation(
+                    out=o_sb[:, P * a:P * a + P], in_=quad[(ib, hq, "pv")][:, a, :], func=ACT.Copy,
+                    scale=rinv[:, a:a + 1],
+                )
             nc.sync.dma_start(out=o2[P * ib:P * ib + P, 512 * hq:512 * hq + 512], in_=o_sb[:])
 
         def run(stage_fn, n, *more):
@@ -329,19 +358,23 @@ def tile_multiheadselfattention_pa_kernel(tc, q_proj, k_proj, x, w_v, out):
                 stage_fn(n, *more)
 
         with tc.manual_schedule():
-            for k in range(-2, n_duos + 4):
+            for k in range(-2, n_duos + 5):
                 run(exps, k)
-                run(exits, k - 2, True)
                 run(row_max, k + 1)
+                if quad_end(k - 1):
+                    row_sums(k - 1)
+                run(exits_full, k - 2)
                 run(qk, k + 2)
                 run(transposes, k)
-                run(exits, k - 1, False)
+                run(exits_partial, k - 1)
                 if 0 <= k < 4:
                     v_passes(4 + k)
-                run(quantise, k - 2)
+                run(quantise, k - 3)
                 if 1 <= k < 5:
                     v_quantise(3 + k)
                 if quad_end(k - 2):
-                    pv_passes(k - 2)
+                    reciprocals(k - 2)
                 if quad_end(k - 3):
-                    finish(k - 3)
+                    pv_passes(k - 3)
+                if quad_end(k - 4):
+                    finish(k - 4)

@@ -196,6 +196,9 @@ def tile_multiheadselfattention_pa_kernel(tc, q_proj, k_proj, x, w_v, out):
         def blocks(ib, g):
             return (ib % 4 + 1) if g == ib // 4 else 4
 
+        def on_vector(ib, h, g):
+            return g == ib // 4 and h % 2 == 1 and ib >= 1
+
         def qk(n):
             ib, slots = duos[n]
             st[n]["sc"] = []
@@ -255,42 +258,26 @@ def tile_multiheadselfattention_pa_kernel(tc, q_proj, k_proj, x, w_v, out):
                     nc.tensor.transpose(et[:, 4 * si + t, :], st[n]["e"][:, c0:c0 + P], ident_b[:])
             st[n]["et"] = et
 
-        def grouped(n):
+        def exits(n, vector_share):
             ib, slots = duos[n]
             ge = ge_ring[("big" if ib >= 4 else "small", ib % 4)][(n // 2) % N_GE]
             st[n]["ge"] = ge
-            return ge[:, 1024 * (n % 2):1024 * (n % 2) + 1024].rearrange("p (s i t) -> p s i t", s=2, t=4)
-
-        def full_slots(n):
-            ib, slots = duos[n]
-            return [si for si, (h, g) in enumerate(slots) if blocks(ib, g) == 4]
-
-        def exits_partial(n):
-            ib, slots = duos[n]
-            ge4 = grouped(n)
-            for si, (h, g) in enumerate(slots):
-                nblk = blocks(ib, g)
-                if nblk < 4:
-                    nc.scalar.copy(
-                        out=ge4[:, si, :, 0:nblk],
-                        in_=st[n]["et"][:, 4 * si:4 * si + nblk, :].rearrange("p t i -> p i t"),
-                    )
-
-        def exits_full(n):
-            full = full_slots(n)
-            if not full:
+            ge4 = ge[:, 1024 * (n % 2):1024 * (n % 2) + 1024].rearrange("p (s i t) -> p s i t", s=2, t=4)
+            et = st[n]["et"]
+            if ib % 4 == 3 and not on_vector(ib, slots[1][0], slots[1][1]):
+                if not vector_share:
+                    nc.scalar.copy(out=ge4, in_=et[:].rearrange("p (s t) i -> p s i t", t=4))
                 return
-            ge4 = grouped(n)
-            width = 512 * len(full)
-            stg = work.tile([P, 1024], BF16, name="stg", tag="stg", bufs=3)
-            nc.vector.tensor_copy(
-                out=stg[:, 0:width], in_=st[n]["et"][:, 0:4 * len(full), :].rearrange("p a i -> p (a i)"),
-            )
-            nc.gpsimd.tensor_scalar(
-                out=ge4[:, 0:len(full), :, :],
-                in0=stg[:, 0:width].rearrange("p (s t i) -> p s i t", t=4, i=P),
-                scalar1=1.0, scalar2=0.0, op0=ALU.mult, op1=ALU.add,
-            )
+            for si, (h, g) in enumerate(slots):
+                if on_vector(ib, h, g) != vector_share:
+                    continue
+                nblk = blocks(ib, g)
+                src = et[:, 4 * si:4 * si + nblk, :].rearrange("p t i -> p i t")
+                dst = ge4[:, si, :, 0:nblk]
+                if vector_share:
+                    nc.vector.tensor_copy(out=dst, in_=src)
+                else:
+                    nc.scalar.copy(out=dst, in_=src)
 
         def quantise(n):
             if n % 2 == 0:
@@ -322,35 +309,22 @@ def tile_multiheadselfattention_pa_kernel(tc, q_proj, k_proj, x, w_v, out):
                         start=(g == 0), stop=(g == ib // 4),
                     )
 
-        def row_sums(n):
-            ib, slots = duos[n]
-            if ib >= 4:
-                hq = slots[-1][0] // 4
-                rs_q = quad[(ib, hq, "rs")]
-                rsum = small.tile([P, 4], F32, name="rsum", tag="rsum")
-                nc.gpsimd.tensor_tensor(out=rsum[:], in0=rs_q[:, :, 0], in1=rs_q[:, :, 1], op=ALU.add)
-                quad[(ib, hq, "rsum")] = rsum
-
-        def reciprocals(n):
-            ib, slots = duos[n]
-            hq = slots[-1][0] // 4
-            rinv = small.tile([P, 4], F32, name="rinv", tag="rinv")
-            if ib >= 4:
-                nc.vector.reciprocal(out=rinv[:], in_=quad[(ib, hq, "rsum")][:])
-            else:
-                nc.vector.reciprocal(out=rinv[:], in_=quad[(ib, hq, "rs")][:, :, 0])
-            quad[(ib, hq, "rinv")] = rinv
-
         def finish(n):
             ib, slots = duos[n]
             hq = slots[-1][0] // 4
-            rinv = quad[(ib, hq, "rinv")]
+            rs_q = quad[(ib, hq, "rs")]
+            rinv = small.tile([P, 4], F32, name="rinv", tag="rinv")
+            if ib >= 4:
+                rsum = small.tile([P, 4], F32, name="rsum", tag="rsum")
+                nc.gpsimd.tensor_tensor(out=rsum[:], in0=rs_q[:, :, 0], in1=rs_q[:, :, 1], op=ALU.add)
+                nc.vector.reciprocal(out=rinv[:], in_=rsum[:])
+            else:
+                nc.vector.reciprocal(out=rinv[:], in_=rs_q[:, :, 0])
             o_sb = work.tile([P, 512], F32, name="o_sb", tag="o_sb", bufs=3)
-            for a in range(4):
-                nc.scalar.activation(
-                    out=o_sb[:, P * a:P * a + P], in_=quad[(ib, hq, "pv")][:, a, :], func=ACT.Copy,
-                    scale=rinv[:, a:a + 1],
-                )
+            nc.vector.tensor_tensor(
+                out=o_sb[:].rearrange("p (h c) -> p h c", h=4), in0=quad[(ib, hq, "pv")][:],
+                in1=rinv[:].unsqueeze(2).to_broadcast([P, 4, P]), op=ALU.mult,
+            )
             nc.sync.dma_start(out=o2[P * ib:P * ib + P, 512 * hq:512 * hq + 512], in_=o_sb[:])
 
         def run(stage_fn, n, *more):
@@ -358,23 +332,19 @@ def tile_multiheadselfattention_pa_kernel(tc, q_proj, k_proj, x, w_v, out):
                 stage_fn(n, *more)
 
         with tc.manual_schedule():
-            for k in range(-2, n_duos + 5):
+            for k in range(-2, n_duos + 4):
                 run(exps, k)
                 run(row_max, k + 1)
-                if quad_end(k - 1):
-                    row_sums(k - 1)
-                run(exits_full, k - 2)
+                run(exits, k - 2, True)
                 run(qk, k + 2)
                 run(transposes, k)
-                run(exits_partial, k - 1)
+                run(exits, k - 1, False)
                 if 0 <= k < 4:
                     v_passes(4 + k)
-                run(quantise, k - 3)
+                run(quantise, k - 2)
                 if 1 <= k < 5:
                     v_quantise(3 + k)
                 if quad_end(k - 2):
-                    reciprocals(k - 2)
+                    pv_passes(k - 2)
                 if quad_end(k - 3):
-                    pv_passes(k - 3)
-                if quad_end(k - 4):
-                    finish(k - 4)
+                    finish(k - 3)

@@ -37,9 +37,8 @@ def tile_multiheadselfattention_pa_kernel(tc, q_proj, k_proj, x, w_v, out):
         stage = ctx.enter_context(tc.tile_pool(name="stage", bufs=3))
         work = ctx.enter_context(tc.tile_pool(name="work", bufs=4))
         small = ctx.enter_context(tc.tile_pool(name="small", bufs=6))
-        ps_sc = ctx.enter_context(tc.psum_pool(name="ps_sc", bufs=4))
-        ps_et = ctx.enter_context(tc.psum_pool(name="ps_et", bufs=2))
-        ps_pv = ctx.enter_context(tc.psum_pool(name="ps_pv", bufs=2))
+        ps_sc = ctx.enter_context(tc.psum_pool(name="ps_sc", bufs=7))
+        ps_pv = ctx.enter_context(tc.psum_pool(name="ps_pv", bufs=1))
 
         x4 = []
         for j in range(4):
@@ -89,17 +88,14 @@ def tile_multiheadselfattention_pa_kernel(tc, q_proj, k_proj, x, w_v, out):
             for ibl in range(3):
                 ring = []
                 for r in range(N_GE):
-                    g_t = keep.tile([P, 2048], BF16, name="ge_%s%d_%d" % (kind, ibl, r), align_bytes=64)
-                    words = g_t[:].bitcast(I32).rearrange("p (d s w) -> p d s w", d=2, s=2)
-                    if kind == "big":
-                        nc.vector.memset(words[:, :, 1, :], 0)
-                    else:
-                        nc.vector.memset(g_t[:].bitcast(I32), 0)
+                    g_t = keep.tile([P, 1024], BF16, name="ge_%s%d_%d" % (kind, ibl, r), align_bytes=64)
+                    first = 512 if kind == "big" else 0
+                    nc.vector.memset(g_t[:, first:1024].bitcast(I32), 0)
                     ring.append(g_t)
                 ge_ring[(kind, ibl)] = ring
         ring = []
         for r in range(N_GE):
-            g_t = keep.tile([P, 2048], BF16, name="ge_full_%d" % r, align_bytes=64)
+            g_t = keep.tile([P, 1024], BF16, name="ge_full_%d" % r, align_bytes=64)
             ring.append(g_t)
         ge_ring[("big", 3)] = ring
         ge_ring[("small", 3)] = ring
@@ -125,7 +121,7 @@ def tile_multiheadselfattention_pa_kernel(tc, q_proj, k_proj, x, w_v, out):
         w_scales = keep.tile([P, 2, D], U8, name="w_scales", align_bytes=64)
         for half in range(2):
             for c in range(2):
-                gw = stage.tile([P, 2048], BF16, name="gw", tag="gw", align_bytes=64, bufs=2)
+                gw = stage.tile([P, 2048], BF16, name="gw", tag="gw", align_bytes=64, bufs=4)
                 n0 = 512 * half
                 dst = gw[:].rearrange("p (c i t) -> p c t i", i=4, t=4)
                 src = w_raw[:, 4 * c:4 * c + 4, n0:n0 + 512].rearrange("p t (c i) -> p c t i", i=4)
@@ -146,7 +142,7 @@ def tile_multiheadselfattention_pa_kernel(tc, q_proj, k_proj, x, w_v, out):
             gv = stage.tile([P, 1024], BF16, name="gv", tag="gv", align_bytes=64)
             gvs[h] = gv
             for g in range(2):
-                vp = ps_pv.tile([P, 4, P], F32, name="vp", tag="pv")
+                vp = ps_sc.tile([P, 4, P], F32, name="vp", tag="sc")
                 for t in range(4):
                     for c in range(2):
                         nc.tensor.matmul_mx(
@@ -174,11 +170,14 @@ def tile_multiheadselfattention_pa_kernel(tc, q_proj, k_proj, x, w_v, out):
 
         q_T = {}
         for ib in range(7, -1, -1):
-            qt = ps_et.tile([P, H, P], BF16, name="qt", tag="et")
+            qt = ps_sc.tile([P, H, P], BF16, name="qt", tag="sc")
             for h in range(H):
                 nc.tensor.transpose(qt[:, h, :], q_sb[ib][:, P * h:P * h + P], ident_b[:])
             q_Tt = keep.tile([P, D], BF16, name="q_T_%d" % ib)
-            nc.vector.tensor_copy(out=q_Tt[:], in_=qt[:].rearrange("p h i -> p (h i)"))
+            if ib % 2:
+                nc.scalar.copy(out=q_Tt[:], in_=qt[:].rearrange("p h i -> p (h i)"))
+            else:
+                nc.vector.tensor_copy(out=q_Tt[:], in_=qt[:].rearrange("p h i -> p (h i)"))
             q_T[ib] = q_Tt
 
         duos = []
@@ -197,7 +196,7 @@ def tile_multiheadselfattention_pa_kernel(tc, q_proj, k_proj, x, w_v, out):
             return (ib % 4 + 1) if g == ib // 4 else 4
 
         def on_vector(ib, h, g):
-            return g == ib // 4 and h % 2 == 1 and ib >= 1
+            return ib >= 4 and g == 1 and h % 2 == 1
 
         def qk(n):
             ib, slots = duos[n]
@@ -227,11 +226,11 @@ def tile_multiheadselfattention_pa_kernel(tc, q_proj, k_proj, x, w_v, out):
                 ncol = P * blocks(ib, g)
                 nc.vector.tensor_reduce(out=m2[:, si:si + 1], in_=st[n]["sc"][si][:, 0:ncol], axis=AX.X, op=ALU.max)
             if ib >= 4:
-                nc.gpsimd.tensor_scalar(
+                nc.vector.tensor_scalar(
                     out=nm[:, 0:1], in0=m2[:, 0:1], scalar1=m2[:, 1:2], scalar2=-SCALE, op0=ALU.max, op1=ALU.mult,
                 )
             else:
-                nc.gpsimd.tensor_scalar(out=nm[:], in0=m2[:], scalar1=-SCALE, scalar2=0.0, op0=ALU.mult, op1=ALU.add)
+                nc.vector.tensor_scalar(out=nm[:], in0=m2[:], scalar1=-SCALE, scalar2=None, op0=ALU.mult)
             st[n]["nm"] = nm
 
         def exps(n):
@@ -251,7 +250,7 @@ def tile_multiheadselfattention_pa_kernel(tc, q_proj, k_proj, x, w_v, out):
 
         def transposes(n):
             ib, slots = duos[n]
-            et = ps_et.tile([P, 8, P], BF16, name="et", tag="et")
+            et = ps_sc.tile([P, 8, P], BF16, name="et", tag="sc")
             for si, (h, g) in enumerate(slots):
                 for t in range(blocks(ib, g)):
                     c0 = 512 * si + P * t
@@ -260,9 +259,9 @@ def tile_multiheadselfattention_pa_kernel(tc, q_proj, k_proj, x, w_v, out):
 
         def exits(n, vector_share):
             ib, slots = duos[n]
-            ge = ge_ring[("big" if ib >= 4 else "small", ib % 4)][(n // 2) % N_GE]
+            ge = ge_ring[("big" if ib >= 4 else "small", ib % 4)][n % N_GE]
             st[n]["ge"] = ge
-            ge4 = ge[:, 1024 * (n % 2):1024 * (n % 2) + 1024].rearrange("p (s i t) -> p s i t", s=2, t=4)
+            ge4 = ge[:].rearrange("p (s i t) -> p s i t", s=2, t=4)
             et = st[n]["et"]
             if ib % 4 == 3 and not on_vector(ib, slots[1][0], slots[1][1]):
                 if not vector_share:
@@ -280,12 +279,9 @@ def tile_multiheadselfattention_pa_kernel(tc, q_proj, k_proj, x, w_v, out):
                     nc.scalar.copy(out=dst, in_=src)
 
         def quantise(n):
-            if n % 2 == 0:
-                return
-            e_codes = work.tile([P, 512], U32, name="e_codes", tag="e_codes", align_bytes=64, bufs=4)
-            e_scales = work.tile([P, 512], U8, name="e_scales", tag="e_scales", align_bytes=64, bufs=4)
+            e_codes = work.tile([P, 256], U32, name="e_codes", tag="e_codes", align_bytes=64, bufs=8)
+            e_scales = work.tile([P, 256], U8, name="e_scales", tag="e_scales", align_bytes=64, bufs=8)
             nc.vector.quantize_mx(out=e_codes[:].bitcast(FP8X4), scales=e_scales[:], in_=st[n]["ge"][:])
-            st[n - 1]["codes"] = (e_codes, e_scales)
             st[n]["codes"] = (e_codes, e_scales)
 
         def quad_end(n):
@@ -302,8 +298,8 @@ def tile_multiheadselfattention_pa_kernel(tc, q_proj, k_proj, x, w_v, out):
                 for si, (h, g) in enumerate(duos[n][1]):
                     nc.tensor.matmul_mx(
                         out=pv[:, h % 4, :],
-                        lhsT=e_codes[:, 256 * (n % 2) + P * si:256 * (n % 2) + P * si + P].bitcast(FP8X4),
-                        lhsT_scale=e_scales[:, 256 * (n % 2) + P * si:256 * (n % 2) + P * si + P],
+                        lhsT=e_codes[:, P * si:P * si + P].bitcast(FP8X4),
+                        lhsT_scale=e_scales[:, P * si:P * si + P],
                         rhs=v_codes[:, h, g, :].bitcast(FP8X4),
                         rhs_scale=v_scales[:, h, g, :],
                         start=(g == 0), stop=(g == ib // 4),
@@ -316,7 +312,7 @@ def tile_multiheadselfattention_pa_kernel(tc, q_proj, k_proj, x, w_v, out):
             rinv = small.tile([P, 4], F32, name="rinv", tag="rinv")
             if ib >= 4:
                 rsum = small.tile([P, 4], F32, name="rsum", tag="rsum")
-                nc.gpsimd.tensor_tensor(out=rsum[:], in0=rs_q[:, :, 0], in1=rs_q[:, :, 1], op=ALU.add)
+                nc.vector.tensor_reduce(out=rsum[:], in_=rs_q[:], axis=AX.X, op=ALU.add)
                 nc.vector.reciprocal(out=rinv[:], in_=rsum[:])
             else:
                 nc.vector.reciprocal(out=rinv[:], in_=rs_q[:, :, 0])
@@ -334,8 +330,8 @@ def tile_multiheadselfattention_pa_kernel(tc, q_proj, k_proj, x, w_v, out):
         with tc.manual_schedule():
             for k in range(-2, n_duos + 4):
                 run(exps, k)
-                run(row_max, k + 1)
                 run(exits, k - 2, True)
+                run(row_max, k + 1)
                 run(qk, k + 2)
                 run(transposes, k)
                 run(exits, k - 1, False)

@@ -88,14 +88,17 @@ def tile_multiheadselfattention_pa_kernel(tc, q_proj, k_proj, x, w_v, out):
             for ibl in range(3):
                 ring = []
                 for r in range(N_GE):
-                    g_t = keep.tile([P, 1024], BF16, name="ge_%s%d_%d" % (kind, ibl, r), align_bytes=64)
-                    first = 512 if kind == "big" else 0
-                    nc.vector.memset(g_t[:, first:1024].bitcast(I32), 0)
+                    g_t = keep.tile([P, 2048], BF16, name="ge_%s%d_%d" % (kind, ibl, r), align_bytes=64)
+                    words = g_t[:].bitcast(I32).rearrange("p (d s w) -> p d s w", d=2, s=2)
+                    if kind == "big":
+                        nc.vector.memset(words[:, :, 1, :], 0)
+                    else:
+                        nc.vector.memset(g_t[:].bitcast(I32), 0)
                     ring.append(g_t)
                 ge_ring[(kind, ibl)] = ring
         ring = []
         for r in range(N_GE):
-            g_t = keep.tile([P, 1024], BF16, name="ge_full_%d" % r, align_bytes=64)
+            g_t = keep.tile([P, 2048], BF16, name="ge_full_%d" % r, align_bytes=64)
             ring.append(g_t)
         ge_ring[("big", 3)] = ring
         ge_ring[("small", 3)] = ring
@@ -121,7 +124,7 @@ def tile_multiheadselfattention_pa_kernel(tc, q_proj, k_proj, x, w_v, out):
         w_scales = keep.tile([P, 2, D], U8, name="w_scales", align_bytes=64)
         for half in range(2):
             for c in range(2):
-                gw = stage.tile([P, 2048], BF16, name="gw", tag="gw", align_bytes=64, bufs=4)
+                gw = stage.tile([P, 2048], BF16, name="gw", tag="gw", align_bytes=64, bufs=2)
                 n0 = 512 * half
                 dst = gw[:].rearrange("p (c i t) -> p c t i", i=4, t=4)
                 src = w_raw[:, 4 * c:4 * c + 4, n0:n0 + 512].rearrange("p t (c i) -> p c t i", i=4)
@@ -174,20 +177,16 @@ def tile_multiheadselfattention_pa_kernel(tc, q_proj, k_proj, x, w_v, out):
             for h in range(H):
                 nc.tensor.transpose(qt[:, h, :], q_sb[ib][:, P * h:P * h + P], ident_b[:])
             q_Tt = keep.tile([P, D], BF16, name="q_T_%d" % ib)
-            if ib % 2:
-                nc.scalar.copy(out=q_Tt[:], in_=qt[:].rearrange("p h i -> p (h i)"))
-            else:
-                nc.vector.tensor_copy(out=q_Tt[:], in_=qt[:].rearrange("p h i -> p (h i)"))
+            nc.vector.tensor_copy(out=q_Tt[:], in_=qt[:].rearrange("p h i -> p (h i)"))
             q_T[ib] = q_Tt
 
         duos = []
-        for ib in range(7, -1, -1):
-            if ib >= 4:
-                for h in range(H):
+        for ib in range(7, 3, -1):
+            for hq in range(2):
+                for h in range(4 * hq, 4 * hq + 4):
                     duos.append((ib, [(h, 0), (h, 1)]))
-            else:
-                for d in range(4):
-                    duos.append((ib, [(2 * d, 0), (2 * d + 1, 0)]))
+                for h in range(4 * hq, 4 * hq + 4, 2):
+                    duos.append((ib - 4, [(h, 0), (h + 1, 0)]))
         n_duos = len(duos)
         st = [dict() for n in range(n_duos)]
         quad = {}
@@ -221,10 +220,15 @@ def tile_multiheadselfattention_pa_kernel(tc, q_proj, k_proj, x, w_v, out):
         def row_max(n):
             ib, slots = duos[n]
             m2 = small.tile([P, 2], F32, name="m2", tag="m2")
-            nm = small.tile([P, 2], F32, name="nm", tag="nm")
             for si, (h, g) in enumerate(slots):
                 ncol = P * blocks(ib, g)
                 nc.vector.tensor_reduce(out=m2[:, si:si + 1], in_=st[n]["sc"][si][:, 0:ncol], axis=AX.X, op=ALU.max)
+            st[n]["m2"] = m2
+
+        def biases(n):
+            ib, slots = duos[n]
+            m2 = st[n]["m2"]
+            nm = small.tile([P, 2], F32, name="nm", tag="nm")
             if ib >= 4:
                 nc.vector.tensor_scalar(
                     out=nm[:, 0:1], in0=m2[:, 0:1], scalar1=m2[:, 1:2], scalar2=-SCALE, op0=ALU.max, op1=ALU.mult,
@@ -259,9 +263,9 @@ def tile_multiheadselfattention_pa_kernel(tc, q_proj, k_proj, x, w_v, out):
 
         def exits(n, vector_share):
             ib, slots = duos[n]
-            ge = ge_ring[("big" if ib >= 4 else "small", ib % 4)][n % N_GE]
+            ge = ge_ring[("big" if ib >= 4 else "small", ib % 4)][(n // 2) % N_GE]
             st[n]["ge"] = ge
-            ge4 = ge[:].rearrange("p (s i t) -> p s i t", s=2, t=4)
+            ge4 = ge[:, 1024 * (n % 2):1024 * (n % 2) + 1024].rearrange("p (s i t) -> p s i t", s=2, t=4)
             et = st[n]["et"]
             if ib % 4 == 3 and not on_vector(ib, slots[1][0], slots[1][1]):
                 if not vector_share:
@@ -279,9 +283,12 @@ def tile_multiheadselfattention_pa_kernel(tc, q_proj, k_proj, x, w_v, out):
                     nc.scalar.copy(out=dst, in_=src)
 
         def quantise(n):
-            e_codes = work.tile([P, 256], U32, name="e_codes", tag="e_codes", align_bytes=64, bufs=8)
-            e_scales = work.tile([P, 256], U8, name="e_scales", tag="e_scales", align_bytes=64, bufs=8)
+            if n % 2 == 0:
+                return
+            e_codes = work.tile([P, 512], U32, name="e_codes", tag="e_codes", align_bytes=64, bufs=4)
+            e_scales = work.tile([P, 512], U8, name="e_scales", tag="e_scales", align_bytes=64, bufs=4)
             nc.vector.quantize_mx(out=e_codes[:].bitcast(FP8X4), scales=e_scales[:], in_=st[n]["ge"][:])
+            st[n - 1]["codes"] = (e_codes, e_scales)
             st[n]["codes"] = (e_codes, e_scales)
 
         def quad_end(n):
@@ -298,28 +305,38 @@ def tile_multiheadselfattention_pa_kernel(tc, q_proj, k_proj, x, w_v, out):
                 for si, (h, g) in enumerate(duos[n][1]):
                     nc.tensor.matmul_mx(
                         out=pv[:, h % 4, :],
-                        lhsT=e_codes[:, P * si:P * si + P].bitcast(FP8X4),
-                        lhsT_scale=e_scales[:, P * si:P * si + P],
+                        lhsT=e_codes[:, 256 * (n % 2) + P * si:256 * (n % 2) + P * si + P].bitcast(FP8X4),
+                        lhsT_scale=e_scales[:, 256 * (n % 2) + P * si:256 * (n % 2) + P * si + P],
                         rhs=v_codes[:, h, g, :].bitcast(FP8X4),
                         rhs_scale=v_scales[:, h, g, :],
                         start=(g == 0), stop=(g == ib // 4),
                     )
 
+        def row_sums(n):
+            ib, slots = duos[n]
+            hq = slots[-1][0] // 4
+            if ib >= 4:
+                rsum = small.tile([P, 4], F32, name="rsum", tag="rsum")
+                nc.vector.tensor_reduce(out=rsum[:], in_=quad[(ib, hq, "rs")][:], axis=AX.X, op=ALU.add)
+                quad[(ib, hq, "rsum")] = rsum
+
+        def reciprocals(n):
+            ib, slots = duos[n]
+            hq = slots[-1][0] // 4
+            rinv = small.tile([P, 4], F32, name="rinv", tag="rinv")
+            if ib >= 4:
+                nc.vector.reciprocal(out=rinv[:], in_=quad[(ib, hq, "rsum")][:])
+            else:
+                nc.vector.reciprocal(out=rinv[:], in_=quad[(ib, hq, "rs")][:, :, 0])
+            quad[(ib, hq, "rinv")] = rinv
+
         def finish(n):
             ib, slots = duos[n]
             hq = slots[-1][0] // 4
-            rs_q = quad[(ib, hq, "rs")]
-            rinv = small.tile([P, 4], F32, name="rinv", tag="rinv")
-            if ib >= 4:
-                rsum = small.tile([P, 4], F32, name="rsum", tag="rsum")
-                nc.vector.tensor_reduce(out=rsum[:], in_=rs_q[:], axis=AX.X, op=ALU.add)
-                nc.vector.reciprocal(out=rinv[:], in_=rsum[:])
-            else:
-                nc.vector.reciprocal(out=rinv[:], in_=rs_q[:, :, 0])
             o_sb = work.tile([P, 512], F32, name="o_sb", tag="o_sb", bufs=3)
             nc.vector.tensor_tensor(
                 out=o_sb[:].rearrange("p (h c) -> p h c", h=4), in0=quad[(ib, hq, "pv")][:],
-                in1=rinv[:].unsqueeze(2).to_broadcast([P, 4, P]), op=ALU.mult,
+                in1=quad[(ib, hq, "rinv")][:].unsqueeze(2).to_broadcast([P, 4, P]), op=ALU.mult,
             )
             nc.sync.dma_start(out=o2[P * ib:P * ib + P, 512 * hq:512 * hq + 512], in_=o_sb[:])
 
@@ -328,19 +345,24 @@ def tile_multiheadselfattention_pa_kernel(tc, q_proj, k_proj, x, w_v, out):
                 stage_fn(n, *more)
 
         with tc.manual_schedule():
-            for k in range(-2, n_duos + 4):
+            for k in range(-2, n_duos + 5):
+                run(biases, k)
+                run(exits, k - 2, False)
                 run(exps, k)
-                run(exits, k - 2, True)
                 run(row_max, k + 1)
+                run(exits, k - 2, True)
                 run(qk, k + 2)
                 run(transposes, k)
-                run(exits, k - 1, False)
                 if 0 <= k < 4:
                     v_passes(4 + k)
-                run(quantise, k - 2)
+                run(quantise, k - 3)
                 if 1 <= k < 5:
                     v_quantise(3 + k)
+                if quad_end(k - 1):
+                    row_sums(k - 1)
                 if quad_end(k - 2):
-                    pv_passes(k - 2)
+                    reciprocals(k - 2)
                 if quad_end(k - 3):
-                    finish(k - 3)
+                    pv_passes(k - 3)
+                if quad_end(k - 4):
+                    finish(k - 4)

@@ -195,7 +195,7 @@ def tile_multiheadselfattention_pa_kernel(tc, q_proj, k_proj, x, w_v, out):
             return (ib % 4 + 1) if g == ib // 4 else 4
 
         def on_vector(ib, h, g):
-            return ib >= 4 and g == 1 and h % 2 == 1
+            return 4 <= ib < 7 and g == 1 and h % 2 == 1
 
         def qk(n):
             ib, slots = duos[n]

@@ -167,7 +167,7 @@ def tile_multiheadselfattention_pa_kernel(tc, q_proj, k_proj, x, w_v, out):
                 scales=v_scales[:, h, :, :].rearrange("p g c -> p (g c)"), in_=gvs[h][:],
             )
 
-        for h in range(4):
+        for h in range(H):
             v_passes(h)
             v_quantise(h)
 
@@ -195,7 +195,7 @@ def tile_multiheadselfattention_pa_kernel(tc, q_proj, k_proj, x, w_v, out):
             return (ib % 4 + 1) if g == ib // 4 else 4
 
         def on_vector(ib, h, g):
-            return 4 <= ib < 7 and g == 1 and h % 2 == 1
+            return ib >= 4 and g == 1 and h % 2 == 1
 
         def qk(n):
             ib, slots = duos[n]
@@ -353,11 +353,7 @@ def tile_multiheadselfattention_pa_kernel(tc, q_proj, k_proj, x, w_v, out):
                 run(exits, k - 2, True)
                 run(qk, k + 2)
                 run(transposes, k)
-                if 0 <= k < 4:
-                    v_passes(4 + k)
                 run(quantise, k - 3)
-                if 1 <= k < 5:
-                    v_quantise(3 + k)
                 if quad_end(k - 1):
                     row_sums(k - 1)
                 if quad_end(k - 2):

@@ -21,7 +21,7 @@ SCALE = 128.0 ** -0.5
 NEG = -(2.0 ** 40)
 FLOPS = 2 * S * D * D + 2 * (2 * H * (512 * 512 + 512 * 1024) * 128)
 
-N_GE = 2
+N_E = 3
 
 
 def tile_multiheadselfattention_pa_kernel(tc, q_proj, k_proj, x, w_v, out):
@@ -77,47 +77,59 @@ def tile_multiheadselfattention_pa_kernel(tc, q_proj, k_proj, x, w_v, out):
             base=0, pattern=[[-1, P]], channel_multiplier=1,
         )
         mask_b = const.tile([P, P], BF16, name="mask_b")
-        nc.vector.tensor_copy(out=mask_b[:], in_=mask_f[:])
+        nc.vector.tensor_copy(
+            out=mask_b[:].rearrange("p (dh m dl) -> p dh m dl", m=8, dl=2),
+            in_=mask_f[:].rearrange("p (dh dl m) -> p dh m dl", m=8, dl=2),
+        )
+        perm_f = const.tile([P, P], F32, name="perm_f")
+        nc.vector.tensor_copy(
+            out=perm_f[:].rearrange("p (dl dh m) -> p dl dh m", dl=2, m=8),
+            in_=ident_f[:].rearrange("p (dh dl m) -> p dl dh m", dl=2, m=8),
+        )
         warm = const.tile([P, 2], F32, name="warm")
         nc.vector.memset(warm[:], 0.0)
         warm2 = const.tile([P, 2], F32, name="warm2")
         nc.scalar.activation(out=warm2[:], in_=warm[:], func=ACT.Exp)
 
-        ge_ring = {}
+        e_ring = {}
         for kind in ("big", "small"):
             for ibl in range(3):
                 ring = []
-                for r in range(N_GE):
-                    g_t = keep.tile([P, 2048], BF16, name="ge_%s%d_%d" % (kind, ibl, r), align_bytes=64)
-                    words = g_t[:].bitcast(I32).rearrange("p (d s w) -> p d s w", d=2, s=2)
+                for r in range(N_E):
+                    e_t = keep.tile([P, 1024], BF16, name="e_%s%d_%d" % (kind, ibl, r), align_bytes=64)
+                    words = e_t[:].bitcast(I32).rearrange("p (s w) -> p s w", s=2)
+                    w0 = 64 * (ibl + 1)
                     if kind == "big":
-                        nc.vector.memset(words[:, :, 1, :], 0)
+                        nc.vector.memset(words[:, 1, w0:256], 0)
                     else:
-                        nc.vector.memset(g_t[:].bitcast(I32), 0)
-                    ring.append(g_t)
-                ge_ring[(kind, ibl)] = ring
+                        nc.vector.memset(words[:, :, w0:256], 0)
+                    ring.append(e_t)
+                e_ring[(kind, ibl)] = ring
         ring = []
-        for r in range(N_GE):
-            g_t = keep.tile([P, 2048], BF16, name="ge_full_%d" % r, align_bytes=64)
-            ring.append(g_t)
-        ge_ring[("big", 3)] = ring
-        ge_ring[("small", 3)] = ring
+        for r in range(N_E):
+            e_t = keep.tile([P, 1024], BF16, name="e_full_%d" % r, align_bytes=64)
+            ring.append(e_t)
+        e_ring[("big", 3)] = ring
+        e_ring[("small", 3)] = ring
 
-        x_codes = keep.tile([P, 8, 256], U32, name="x_codes", align_bytes=64)
-        x_scales = keep.tile([P, 8, 256], U8, name="x_scales", align_bytes=64)
-        for sb in range(8):
-            xw = x4[sb // 2][:].bitcast(F32)
-            xt = ps_sc.tile([P, 4, P], F32, name="xt", tag="sc")
-            for kw in range(4):
-                c0 = 512 * (sb % 2) + P * kw
-                nc.tensor.transpose(xt[:, kw, :], xw[:, c0:c0 + P], ident_f[:])
-            gx = stage.tile([P, 1024], BF16, name="gx", tag="gx", align_bytes=64)
-            nc.scalar.copy(
-                out=gx[:].bitcast(F32).rearrange("p (c s u) -> p c s u", c=2, u=2),
-                in_=xt[:].rearrange("p (c u) s -> p c s u", u=2),
-            )
+        x_codes = keep.tile([P, 4, 512], U32, name="x_codes", align_bytes=64)
+        x_scales = keep.tile([P, 4, 512], U8, name="x_scales", align_bytes=64)
+        for gu in range(4):
+            gx = stage.tile([P, 2048], BF16, name="gx", tag="gx", align_bytes=64)
+            gxw = gx[:].bitcast(F32).rearrange("p (ce a s u) -> p ce a s u", ce=4, a=2, u=2)
+            for a in range(2):
+                xw = x4[gu][:].bitcast(F32)
+                xt = ps_sc.tile([P, 4, P], F32, name="xt", tag="sc")
+                for c in range(2):
+                    for u in range(2):
+                        c0 = 512 * a + 256 * c + P * u
+                        nc.tensor.transpose(xt[:, 2 * u + c, :], xw[:, c0:c0 + P], perm_f[:])
+                nc.scalar.copy(
+                    out=gxw[:, :, a, :, :],
+                    in_=xt[:].rearrange("p (u c) (e s) -> p (c e) s u", u=2, e=2),
+                )
             nc.vector.quantize_mx(
-                out=x_codes[:, sb, :].bitcast(FP8X4), scales=x_scales[:, sb, :], in_=gx[:],
+                out=x_codes[:, gu, :].bitcast(FP8X4), scales=x_scales[:, gu, :], in_=gx[:],
             )
 
         w_codes = keep.tile([P, 2, D], U32, name="w_codes", align_bytes=64)
@@ -150,8 +162,8 @@ def tile_multiheadselfattention_pa_kernel(tc, q_proj, k_proj, x, w_v, out):
                     for c in range(2):
                         nc.tensor.matmul_mx(
                             out=vp[:, t, :],
-                            lhsT=x_codes[:, 4 * g + t, P * c:P * c + P].bitcast(FP8X4),
-                            lhsT_scale=x_scales[:, 4 * g + t, P * c:P * c + P],
+                            lhsT=x_codes[:, 2 * g + t // 2, 256 * c + P * (t % 2):256 * c + P * (t % 2) + P].bitcast(FP8X4),
+                            lhsT_scale=x_scales[:, 2 * g + t // 2, 256 * c + P * (t % 2):256 * c + P * (t % 2) + P],
                             rhs=w_codes[:, c, P * h:P * h + P].bitcast(FP8X4),
                             rhs_scale=w_scales[:, c, P * h:P * h + P],
                             start=(c == 0), stop=(c == 1),
@@ -194,9 +206,6 @@ def tile_multiheadselfattention_pa_kernel(tc, q_proj, k_proj, x, w_v, out):
         def blocks(ib, g):
             return (ib % 4 + 1) if g == ib // 4 else 4
 
-        def on_vector(ib, h, g):
-            return ib >= 4 and g == 1 and h % 2 == 1
-
         def qk(n):
             ib, slots = duos[n]
             st[n]["sc"] = []
@@ -205,9 +214,9 @@ def tile_multiheadselfattention_pa_kernel(tc, q_proj, k_proj, x, w_v, out):
                 ncol = P * blocks(ib, g)
                 sc = ps_sc.tile([P, 512], F32, name="sc", tag="sc")
                 nc.tensor.matmul(
-                    out=sc[:, 0:ncol].rearrange("p (d m) -> p m d", m=8),
+                    out=sc[:, 0:ncol].rearrange("p (dh m dl) -> p m dh dl", m=8, dl=2),
                     lhsT=q_T[ib][:, P * h:P * h + P],
-                    rhs=k_sb[:, :, P * h + 64 * g:P * h + 64 * g + ncol // 8],
+                    rhs=k_sb[:, :, P * h + 64 * g:P * h + 64 * g + ncol // 8].rearrange("p m (dh dl) -> p m dh dl", dl=2),
                     start=True, stop=(not diag),
                 )
                 if diag:
@@ -241,7 +250,7 @@ def tile_multiheadselfattention_pa_kernel(tc, q_proj, k_proj, x, w_v, out):
             ib, slots = duos[n]
             if slots[0][0] % 4 == 0:
                 quad[(ib, slots[0][0] // 4, "rs")] = small.tile([P, 4, 2], F32, name="rs_q", tag="rs_q")
-            e_t = work.tile([P, 1024], BF16, name="e_t", tag="e_t")
+            e_t = e_ring[("big" if ib >= 4 else "small", ib % 4)][n % N_E]
             for si, (h, g) in enumerate(slots):
                 ncol = P * blocks(ib, g)
                 col = 0 if ib >= 4 else si
@@ -253,34 +262,23 @@ def tile_multiheadselfattention_pa_kernel(tc, q_proj, k_proj, x, w_v, out):
             st[n]["e"] = e_t
 
         def transposes(n):
-            ib, slots = duos[n]
-            et = ps_sc.tile([P, 8, P], BF16, name="et", tag="sc")
-            for si, (h, g) in enumerate(slots):
-                for t in range(blocks(ib, g)):
-                    c0 = 512 * si + P * t
-                    nc.tensor.transpose(et[:, 4 * si + t, :], st[n]["e"][:, c0:c0 + P], ident_b[:])
+            et = ps_sc.tile([P, 4, P], F32, name="et", tag="sc")
+            ew = st[n]["e"][:].bitcast(F32)
+            for su in range(4):
+                nc.tensor.transpose(et[:, su, :], ew[:, P * su:P * su + P], ident_f[:])
             st[n]["et"] = et
 
-        def exits(n, vector_share):
-            ib, slots = duos[n]
-            ge = ge_ring[("big" if ib >= 4 else "small", ib % 4)][(n // 2) % N_GE]
-            st[n]["ge"] = ge
-            ge4 = ge[:, 1024 * (n % 2):1024 * (n % 2) + 1024].rearrange("p (s i t) -> p s i t", s=2, t=4)
-            et = st[n]["et"]
-            if ib % 4 == 3 and not on_vector(ib, slots[1][0], slots[1][1]):
-                if not vector_share:
-                    nc.scalar.copy(out=ge4, in_=et[:].rearrange("p (s t) i -> p s i t", t=4))
-                return
-            for si, (h, g) in enumerate(slots):
-                if on_vector(ib, h, g) != vector_share:
-                    continue
-                nblk = blocks(ib, g)
-                src = et[:, 4 * si:4 * si + nblk, :].rearrange("p t i -> p i t")
-                dst = ge4[:, si, :, 0:nblk]
-                if vector_share:
-                    nc.vector.tensor_copy(out=dst, in_=src)
-                else:
-                    nc.scalar.copy(out=dst, in_=src)
+        def exits(n):
+            if n % 2 == 0:
+                st[n]["ge"] = work.tile([P, 2048], BF16, name="ge", tag="ge", align_bytes=64, bufs=3)
+            else:
+                st[n]["ge"] = st[n - 1]["ge"]
+            gew = st[n]["ge"][:].bitcast(F32)
+            w0 = 512 * (n % 2)
+            nc.scalar.copy(
+                out=gew[:, w0:w0 + 512].rearrange("p (s i u) -> p s i u", s=2, u=2),
+                in_=st[n]["et"][:].rearrange("p (s u) i -> p s i u", u=2),
+            )
 
         def quantise(n):
             if n % 2 == 0:
@@ -340,17 +338,16 @@ def tile_multiheadselfattention_pa_kernel(tc, q_proj, k_proj, x, w_v, out):
             )
             nc.sync.dma_start(out=o2[P * ib:P * ib + P, 512 * hq:512 * hq + 512], in_=o_sb[:])
 
-        def run(stage_fn, n, *more):
+        def run(stage_fn, n):
             if 0 <= n < n_duos:
-                stage_fn(n, *more)
+                stage_fn(n)
 
         with tc.manual_schedule():
             for k in range(-2, n_duos + 5):
                 run(biases, k)
-                run(exits, k - 2, False)
+                run(exits, k - 2)
                 run(exps, k)
                 run(row_max, k + 1)
-                run(exits, k - 2, True)
                 run(qk, k + 2)
                 run(transposes, k)
                 run(quantise, k - 3)

@@ -21,7 +21,8 @@ SCALE = 128.0 ** -0.5
 NEG = -(2.0 ** 40)
 FLOPS = 2 * S * D * D + 2 * (2 * H * (512 * 512 + 512 * 1024) * 128)
 
-N_E = 3
+N_E = 2
+N_PAIRS = 17
 
 
 def tile_multiheadselfattention_pa_kernel(tc, q_proj, k_proj, x, w_v, out):
@@ -34,13 +35,35 @@ def tile_multiheadselfattention_pa_kernel(tc, q_proj, k_proj, x, w_v, out):
     with ExitStack() as ctx:
         const = ctx.enter_context(tc.tile_pool(name="const", bufs=1))
         keep = ctx.enter_context(tc.tile_pool(name="keep", bufs=1))
-        stage = ctx.enter_context(tc.tile_pool(name="stage", bufs=3))
+        stage = ctx.enter_context(tc.tile_pool(name="stage", bufs=2))
         work = ctx.enter_context(tc.tile_pool(name="work", bufs=4))
         small = ctx.enter_context(tc.tile_pool(name="small", bufs=6))
-        ps_sc = ctx.enter_context(tc.psum_pool(name="ps_sc", bufs=7))
-        ps_pv = ctx.enter_context(tc.psum_pool(name="ps_pv", bufs=1))
+        ps_sc = ctx.enter_context(tc.psum_pool(name="ps_sc", bufs=4))
+        ps_et = ctx.enter_context(tc.psum_pool(name="ps_et", bufs=2))
+        ps_aux = ctx.enter_context(tc.psum_pool(name="ps_aux", bufs=2))
 
+        k_sb = keep.tile([P, 8, D], BF16, name="k_sb")
+        q_sb = {}
         x4 = []
+        w_raw = keep.tile([P, 8, D], BF16, name="w_raw")
+
+        def load_k(hq):
+            for j in range(2):
+                nc.sync.dma_start(
+                    out=k_sb[:, 4 * j:4 * j + 4, 512 * hq:512 * hq + 512],
+                    in_=k2[512 * j:512 * j + 512, 512 * hq:512 * hq + 512].rearrange("(m p) d -> p m d", p=P),
+                )
+
+        for ib in range(8):
+            q_sb[ib] = keep.tile([P, D], BF16, name="q_sb_%d" % ib)
+
+        def load_q(ib, c0, c1):
+            nc.sync.dma_start(out=q_sb[ib][:, c0:c1], in_=q2[P * ib:P * ib + P, c0:c1])
+
+        load_q(7, 0, 512)
+        load_k(0)
+        load_q(3, 0, D)
+        load_q(7, 512, D)
         for j in range(4):
             xt_sb = keep.tile([P, 2048], BF16, name="x4_%d" % j)
             nc.sync.dma_start(
@@ -48,23 +71,14 @@ def tile_multiheadselfattention_pa_kernel(tc, q_proj, k_proj, x, w_v, out):
                 in_=x2[256 * j:256 * j + 256, :].rearrange("(b p) k -> p b k", p=P),
             )
             x4.append(xt_sb)
-        w_raw = keep.tile([P, 8, D], BF16, name="w_raw")
+        load_k(1)
         for cu in range(4):
             nc.sync.dma_start(
                 out=w_raw[:, 2 * cu:2 * cu + 2, :],
                 in_=w_v[256 * cu:256 * cu + 256, :].rearrange("(p e) n -> p e n", e=2),
             )
-        q_sb = {}
-        for ib in range(7, -1, -1):
-            q_t = keep.tile([P, D], BF16, name="q_sb_%d" % ib)
-            nc.sync.dma_start(out=q_t[:], in_=q2[P * ib:P * ib + P, :])
-            q_sb[ib] = q_t
-        k_sb = keep.tile([P, 8, D], BF16, name="k_sb")
-        for j in range(4):
-            nc.sync.dma_start(
-                out=k_sb[:, 2 * j:2 * j + 2, :],
-                in_=k2[256 * j:256 * j + 256, :].rearrange("(m p) d -> p m d", p=P),
-            )
+        for ib in (6, 2, 5, 1, 4, 0):
+            load_q(ib, 0, D)
 
         ident_f = const.tile([P, P], F32, name="ident_f")
         make_identity(nc, ident_f[:])
@@ -114,83 +128,119 @@ def tile_multiheadselfattention_pa_kernel(tc, q_proj, k_proj, x, w_v, out):
 
         x_codes = keep.tile([P, 4, 512], U32, name="x_codes", align_bytes=64)
         x_scales = keep.tile([P, 4, 512], U8, name="x_scales", align_bytes=64)
-        for gu in range(4):
-            gx = stage.tile([P, 2048], BF16, name="gx", tag="gx", align_bytes=64)
-            gxw = gx[:].bitcast(F32).rearrange("p (ce a s u) -> p ce a s u", ce=4, a=2, u=2)
-            for a in range(2):
-                xw = x4[gu][:].bitcast(F32)
-                xt = ps_sc.tile([P, 4, P], F32, name="xt", tag="sc")
-                for c in range(2):
-                    for u in range(2):
-                        c0 = 512 * a + 256 * c + P * u
-                        nc.tensor.transpose(xt[:, 2 * u + c, :], xw[:, c0:c0 + P], perm_f[:])
-                nc.scalar.copy(
-                    out=gxw[:, :, a, :, :],
-                    in_=xt[:].rearrange("p (u c) (e s) -> p (c e) s u", u=2, e=2),
-                )
-            nc.vector.quantize_mx(
-                out=x_codes[:, gu, :].bitcast(FP8X4), scales=x_scales[:, gu, :], in_=gx[:],
-            )
-
         w_codes = keep.tile([P, 2, D], U32, name="w_codes", align_bytes=64)
         w_scales = keep.tile([P, 2, D], U8, name="w_scales", align_bytes=64)
-        for half in range(2):
-            for c in range(2):
-                gw = stage.tile([P, 2048], BF16, name="gw", tag="gw", align_bytes=64, bufs=2)
-                n0 = 512 * half
-                dst = gw[:].rearrange("p (c i t) -> p c t i", i=4, t=4)
-                src = w_raw[:, 4 * c:4 * c + 4, n0:n0 + 512].rearrange("p t (c i) -> p c t i", i=4)
-                if c == 0:
-                    nc.vector.tensor_copy(out=dst, in_=src)
-                else:
-                    nc.scalar.copy(out=dst, in_=src)
-                nc.vector.quantize_mx(
-                    out=w_codes[:, c, n0:n0 + 512].bitcast(FP8X4),
-                    scales=w_scales[:, c, n0:n0 + 512], in_=gw[:],
-                )
-
         v_codes = keep.tile([P, H, 2, P], U32, name="v_codes", align_bytes=64)
         v_scales = keep.tile([P, H, 2, P], U8, name="v_scales", align_bytes=64)
-        gvs = {}
+        q_T = {}
+        held = {}
 
-        def v_passes(h):
-            gv = stage.tile([P, 1024], BF16, name="gv", tag="gv", align_bytes=64)
-            gvs[h] = gv
-            for g in range(2):
-                vp = ps_sc.tile([P, 4, P], F32, name="vp", tag="sc")
-                for t in range(4):
-                    for c in range(2):
-                        nc.tensor.matmul_mx(
-                            out=vp[:, t, :],
-                            lhsT=x_codes[:, 2 * g + t // 2, 256 * c + P * (t % 2):256 * c + P * (t % 2) + P].bitcast(FP8X4),
-                            lhsT_scale=x_scales[:, 2 * g + t // 2, 256 * c + P * (t % 2):256 * c + P * (t % 2) + P],
-                            rhs=w_codes[:, c, P * h:P * h + P].bitcast(FP8X4),
-                            rhs_scale=w_scales[:, c, P * h:P * h + P],
-                            start=(c == 0), stop=(c == 1),
-                        )
-                nc.scalar.copy(
-                    out=gv[:, 512 * g:512 * g + 512].rearrange("p (c t) -> p c t", t=4),
-                    in_=vp[:].rearrange("p t c -> p c t"),
-                )
+        def x_tensor(gu, a):
+            xw = x4[gu][:].bitcast(F32)
+            xt = ps_aux.tile([P, 4, P], F32, name="xt", tag="aux")
+            for c in range(2):
+                for u in range(2):
+                    c0 = 512 * a + 256 * c + P * u
+                    nc.tensor.transpose(xt[:, 2 * u + c, :], xw[:, c0:c0 + P], perm_f[:])
+            held[("xt", gu, a)] = xt
 
-        def v_quantise(h):
-            nc.vector.quantize_mx(
-                out=v_codes[:, h, :, :].rearrange("p g c -> p (g c)").bitcast(FP8X4),
-                scales=v_scales[:, h, :, :].rearrange("p g c -> p (g c)"), in_=gvs[h][:],
+        def x_exit(gu, a):
+            if a == 0:
+                held[("gx", gu)] = stage.tile([P, 2048], BF16, name="gx", tag="gx", align_bytes=64)
+            gxw = held[("gx", gu)][:].bitcast(F32).rearrange("p (ce a s u) -> p ce a s u", ce=4, a=2, u=2)
+            nc.scalar.copy(
+                out=gxw[:, :, a, :, :],
+                in_=held[("xt", gu, a)][:].rearrange("p (u c) (e s) -> p (c e) s u", u=2, e=2),
             )
 
-        for h in range(H):
-            v_passes(h)
-            v_quantise(h)
+        def x_quantise(gu, a):
+            if a == 1:
+                nc.vector.quantize_mx(
+                    out=x_codes[:, gu, :].bitcast(FP8X4), scales=x_scales[:, gu, :], in_=held[("gx", gu)][:],
+                )
 
-        q_T = {}
-        for ib in range(7, -1, -1):
-            qt = ps_sc.tile([P, H, P], BF16, name="qt", tag="sc")
-            for h in range(H):
+        def w_regroup(c, n0):
+            gw = stage.tile([P, 1024], BF16, name="gw", tag="gw", align_bytes=64)
+            held[("gw", c, n0)] = gw
+            nc.vector.tensor_copy(
+                out=gw[:].rearrange("p (c i t) -> p c t i", i=4, t=4),
+                in_=w_raw[:, 4 * c:4 * c + 4, n0:n0 + 256].rearrange("p t (c i) -> p c t i", i=4),
+            )
+
+        def w_quantise(c, n0):
+            nc.vector.quantize_mx(
+                out=w_codes[:, c, n0:n0 + 256].bitcast(FP8X4),
+                scales=w_scales[:, c, n0:n0 + 256], in_=held[("gw", c, n0)][:],
+            )
+
+        def v_tensor(h, g):
+            vp = ps_aux.tile([P, 4, P], F32, name="vp", tag="aux")
+            for t in range(4):
+                for c in range(2):
+                    x0 = 256 * c + P * (t % 2)
+                    nc.tensor.matmul_mx(
+                        out=vp[:, t, :],
+                        lhsT=x_codes[:, 2 * g + t // 2, x0:x0 + P].bitcast(FP8X4),
+                        lhsT_scale=x_scales[:, 2 * g + t // 2, x0:x0 + P],
+                        rhs=w_codes[:, c, P * h:P * h + P].bitcast(FP8X4),
+                        rhs_scale=w_scales[:, c, P * h:P * h + P],
+                        start=(c == 0), stop=(c == 1),
+                    )
+            held[("vp", h, g)] = vp
+
+        def v_exit(h, g):
+            if g == 0:
+                held[("gv", h)] = stage.tile([P, 1024], BF16, name="gv", tag="gv", align_bytes=64)
+            nc.scalar.copy(
+                out=held[("gv", h)][:, 512 * g:512 * g + 512].rearrange("p (c t) -> p c t", t=4),
+                in_=held[("vp", h, g)][:].rearrange("p t c -> p c t"),
+            )
+
+        def v_quantise(h, g):
+            if g == 1:
+                nc.vector.quantize_mx(
+                    out=v_codes[:, h, :, :].rearrange("p g c -> p (g c)").bitcast(FP8X4),
+                    scales=v_scales[:, h, :, :].rearrange("p g c -> p (g c)"), in_=held[("gv", h)][:],
+                )
+
+        for ib in range(8):
+            q_T[ib] = keep.tile([P, D], BF16, name="q_T_%d" % ib)
+
+        def q_tensor(ib, h0, h1):
+            qt = ps_aux.tile([P, H, P], BF16, name="qt", tag="aux")
+            for h in range(h0, h1):
                 nc.tensor.transpose(qt[:, h, :], q_sb[ib][:, P * h:P * h + P], ident_b[:])
-            q_Tt = keep.tile([P, D], BF16, name="q_T_%d" % ib)
-            nc.vector.tensor_copy(out=q_Tt[:], in_=qt[:].rearrange("p h i -> p (h i)"))
-            q_T[ib] = q_Tt
+            held[("qt", ib, h0)] = qt
+
+        def q_exit(ib, h0, h1):
+            nc.vector.tensor_copy(
+                out=q_T[ib][:, P * h0:P * h1], in_=held[("qt", ib, h0)][:, h0:h1, :].rearrange("p h i -> p (h i)"),
+            )
+
+        side = [(q_tensor, q_exit, None, (3, 0, H)), (q_tensor, q_exit, None, (7, 4, H))]
+        for gu in range(4):
+            for a in range(2):
+                side.append((x_tensor, x_exit, x_quantise, (gu, a)))
+            if gu >= 2:
+                side.append((q_tensor, q_exit, None, ((6, 2)[gu - 2], 0, H)))
+        for h in range(H):
+            for g in range(2):
+                side.append((v_tensor, v_exit, v_quantise, (h, g)))
+            if h == 3:
+                V_LOW = len(side) + 2
+            if h in (3, 4, 5, 6):
+                side.append((q_tensor, q_exit, None, ((5, 1, 4, 0)[h - 3], 0, H)))
+        V_ALL = len(side) + 2
+        w_parts = [(c, 256 * j) for j in range(4) for c in range(2)]
+        W_STEP = 5
+
+        def side_part(k, part):
+            if 0 <= k - part < len(side) and side[k - part][part] is not None:
+                side[k - part][part](*side[k - part][3])
+
+        def w_part(k, part):
+            if 0 <= k - W_STEP - part < len(w_parts):
+                (w_regroup if part == 0 else w_quantise)(*w_parts[k - W_STEP - part])
 
         duos = []
         for ib in range(7, 3, -1):
@@ -206,10 +256,10 @@ def tile_multiheadselfattention_pa_kernel(tc, q_proj, k_proj, x, w_v, out):
         def blocks(ib, g):
             return (ib % 4 + 1) if g == ib // 4 else 4
 
-        def qk(n):
+        def qk(n, si):
             ib, slots = duos[n]
-            st[n]["sc"] = []
-            for h, g in slots:
+            st[n].setdefault("sc", [])
+            for h, g in slots[si:si + 1]:
                 diag = (g == ib // 4)
                 ncol = P * blocks(ib, g)
                 sc = ps_sc.tile([P, 512], F32, name="sc", tag="sc")
@@ -226,13 +276,13 @@ def tile_multiheadselfattention_pa_kernel(tc, q_proj, k_proj, x, w_v, out):
                     )
                 st[n]["sc"].append(sc)
 
-        def row_max(n):
+        def row_max(n, si):
             ib, slots = duos[n]
-            m2 = small.tile([P, 2], F32, name="m2", tag="m2")
-            for si, (h, g) in enumerate(slots):
-                ncol = P * blocks(ib, g)
-                nc.vector.tensor_reduce(out=m2[:, si:si + 1], in_=st[n]["sc"][si][:, 0:ncol], axis=AX.X, op=ALU.max)
-            st[n]["m2"] = m2
+            if si == 0:
+                st[n]["m2"] = small.tile([P, 2], F32, name="m2", tag="m2")
+            h, g = slots[si]
+            ncol = P * blocks(ib, g)
+            nc.vector.tensor_reduce(out=st[n]["m2"][:, si:si + 1], in_=st[n]["sc"][si][:, 0:ncol], axis=AX.X, op=ALU.max)
 
         def biases(n):
             ib, slots = duos[n]
@@ -246,31 +296,31 @@ def tile_multiheadselfattention_pa_kernel(tc, q_proj, k_proj, x, w_v, out):
                 nc.vector.tensor_scalar(out=nm[:], in0=m2[:], scalar1=-SCALE, scalar2=None, op0=ALU.mult)
             st[n]["nm"] = nm
 
-        def exps(n):
+        def exps(n, si):
             ib, slots = duos[n]
-            if slots[0][0] % 4 == 0:
-                quad[(ib, slots[0][0] // 4, "rs")] = small.tile([P, 4, 2], F32, name="rs_q", tag="rs_q")
-            e_t = e_ring[("big" if ib >= 4 else "small", ib % 4)][n % N_E]
-            for si, (h, g) in enumerate(slots):
-                ncol = P * blocks(ib, g)
-                col = 0 if ib >= 4 else si
-                nc.scalar.activation(
-                    out=e_t[:, 512 * si:512 * si + ncol], in_=st[n]["sc"][si][:, 0:ncol], func=ACT.Exp,
-                    bias=st[n]["nm"][:, col:col + 1], scale=SCALE,
-                    accum_out=quad[(ib, h // 4, "rs")][:, h % 4, g:g + 1],
-                )
-            st[n]["e"] = e_t
+            if si == 0:
+                if slots[0][0] % 4 == 0:
+                    quad[(ib, slots[0][0] // 4, "rs")] = small.tile([P, 4, 2], F32, name="rs_q", tag="rs_q", bufs=4)
+                st[n]["e"] = e_ring[("big" if ib >= 4 else "small", ib % 4)][n % N_E]
+            h, g = slots[si]
+            ncol = P * blocks(ib, g)
+            col = 0 if ib >= 4 else si
+            nc.scalar.activation(
+                out=st[n]["e"][:, 512 * si:512 * si + ncol], in_=st[n]["sc"][si][:, 0:ncol], func=ACT.Exp,
+                bias=st[n]["nm"][:, col:col + 1], scale=SCALE,
+                accum_out=quad[(ib, h // 4, "rs")][:, h % 4, g:g + 1],
+            )
 
-        def transposes(n):
-            et = ps_sc.tile([P, 4, P], F32, name="et", tag="sc")
+        def transposes(n, si):
+            if si == 0:
+                st[n]["et"] = ps_et.tile([P, 4, P], F32, name="et", tag="et")
             ew = st[n]["e"][:].bitcast(F32)
-            for su in range(4):
-                nc.tensor.transpose(et[:, su, :], ew[:, P * su:P * su + P], ident_f[:])
-            st[n]["et"] = et
+            for su in (2 * si, 2 * si + 1):
+                nc.tensor.transpose(st[n]["et"][:, su, :], ew[:, P * su:P * su + P], ident_f[:])
 
         def exits(n):
             if n % 2 == 0:
-                st[n]["ge"] = work.tile([P, 2048], BF16, name="ge", tag="ge", align_bytes=64, bufs=3)
+                st[n]["ge"] = work.tile([P, 2048], BF16, name="ge", tag="ge", align_bytes=64, bufs=2)
             else:
                 st[n]["ge"] = st[n - 1]["ge"]
             gew = st[n]["ge"][:].bitcast(F32)
@@ -283,8 +333,8 @@ def tile_multiheadselfattention_pa_kernel(tc, q_proj, k_proj, x, w_v, out):
         def quantise(n):
             if n % 2 == 0:
                 return
-            e_codes = work.tile([P, 512], U32, name="e_codes", tag="e_codes", align_bytes=64, bufs=4)
-            e_scales = work.tile([P, 512], U8, name="e_scales", tag="e_scales", align_bytes=64, bufs=4)
+            e_codes = work.tile([P, 512], U32, name="e_codes", tag="e_codes", align_bytes=64, bufs=N_PAIRS)
+            e_scales = work.tile([P, 512], U8, name="e_scales", tag="e_scales", align_bytes=64, bufs=N_PAIRS)
             nc.vector.quantize_mx(out=e_codes[:].bitcast(FP8X4), scales=e_scales[:], in_=st[n]["ge"][:])
             st[n - 1]["codes"] = (e_codes, e_scales)
             st[n]["codes"] = (e_codes, e_scales)
@@ -292,10 +342,19 @@ def tile_multiheadselfattention_pa_kernel(tc, q_proj, k_proj, x, w_v, out):
         def quad_end(n):
             return 0 <= n < n_duos and duos[n][1][-1][0] % 4 == 3
 
+        ends = [n for n in range(n_duos) if quad_end(n)]
+        pv_at = {}
+        waiting = list(ends)
+        for k in range(n_duos + 5):
+            ready = [n for n in waiting if k >= n + 4 and k >= (V_LOW if duos[n][1][-1][0] < 4 else V_ALL)]
+            if ready:
+                pv_at[k] = ready[0]
+                waiting.remove(ready[0])
+
         def pv_passes(n_last):
             ib, slots = duos[n_last]
             hq = slots[-1][0] // 4
-            pv = ps_pv.tile([P, 4, P], F32, name="pv", tag="pv")
+            pv = ps_aux.tile([P, 4, P], F32, name="pv", tag="aux")
             quad[(ib, hq, "pv")] = pv
             n_first = n_last - (3 if ib >= 4 else 1)
             for n in range(n_first, n_last + 1):
@@ -321,7 +380,7 @@ def tile_multiheadselfattention_pa_kernel(tc, q_proj, k_proj, x, w_v, out):
         def reciprocals(n):
             ib, slots = duos[n]
             hq = slots[-1][0] // 4
-            rinv = small.tile([P, 4], F32, name="rinv", tag="rinv")
+            rinv = small.tile([P, 4], F32, name="rinv", tag="rinv", bufs=16)
             if ib >= 4:
                 nc.vector.reciprocal(out=rinv[:], in_=quad[(ib, hq, "rsum")][:])
             else:
@@ -338,24 +397,35 @@ def tile_multiheadselfattention_pa_kernel(tc, q_proj, k_proj, x, w_v, out):
             )
             nc.sync.dma_start(out=o2[P * ib:P * ib + P, 512 * hq:512 * hq + 512], in_=o_sb[:])
 
-        def run(stage_fn, n):
+        def run(stage_fn, n, *more):
             if 0 <= n < n_duos:
-                stage_fn(n)
+                stage_fn(n, *more)
 
         with tc.manual_schedule():
-            for k in range(-2, n_duos + 5):
-                run(biases, k)
-                run(exits, k - 2)
-                run(exps, k)
-                run(row_max, k + 1)
-                run(qk, k + 2)
-                run(transposes, k)
-                run(quantise, k - 3)
+            q_tensor(7, 0, 4)
+            q_exit(7, 0, 4)
+            for k in range(-2, n_duos + 6):
+                run(exps, k, 0)
+                run(exps, k, 1)
+                run(exits, k - 1)
+                run(row_max, k + 1, 0)
+                run(row_max, k + 1, 1)
+                run(quantise, k - 2)
+                run(biases, k + 1)
+                side_part(k, 1)
+                if k - 1 in pv_at:
+                    finish(pv_at[k - 1])
+                side_part(k, 2)
+                w_part(k, 1)
+                w_part(k, 0)
                 if quad_end(k - 1):
                     row_sums(k - 1)
                 if quad_end(k - 2):
                     reciprocals(k - 2)
-                if quad_end(k - 3):
-                    pv_passes(k - 3)
-                if quad_end(k - 4):
-                    finish(k - 4)
+                run(qk, k + 2, 0)
+                run(transposes, k, 0)
+                run(qk, k + 2, 1)
+                run(transposes, k, 1)
+                side_part(k, 0)
+                if k in pv_at:
+                    pv_passes(pv_at[k])

@@ -22,7 +22,7 @@ NEG = -(2.0 ** 40)
 FLOPS = 2 * S * D * D + 2 * (2 * H * (512 * 512 + 512 * 1024) * 128)
 
 N_E = 2
-N_PAIRS = 17
+N_CODES = 34
 
 
 def tile_multiheadselfattention_pa_kernel(tc, q_proj, k_proj, x, w_v, out):
@@ -60,17 +60,21 @@ def tile_multiheadselfattention_pa_kernel(tc, q_proj, k_proj, x, w_v, out):
         def load_q(ib, c0, c1):
             nc.sync.dma_start(out=q_sb[ib][:, c0:c1], in_=q2[P * ib:P * ib + P, c0:c1])
 
-        load_q(7, 0, 512)
-        load_k(0)
-        load_q(3, 0, D)
-        load_q(7, 512, D)
-        for j in range(4):
-            xt_sb = keep.tile([P, 2048], BF16, name="x4_%d" % j)
+        def load_x(gu):
+            xt_sb = keep.tile([P, 2048], BF16, name="x4_%d" % gu)
             nc.sync.dma_start(
                 out=xt_sb[:].rearrange("p (b k) -> p b k", b=2),
-                in_=x2[256 * j:256 * j + 256, :].rearrange("(b p) k -> p b k", p=P),
+                in_=x2[256 * gu:256 * gu + 256, :].rearrange("(b p) k -> p b k", p=P),
             )
             x4.append(xt_sb)
+
+        load_q(7, 0, 512)
+        load_k(0)
+        load_x(0)
+        load_q(3, 0, D)
+        load_q(7, 512, D)
+        for gu in range(1, 4):
+            load_x(gu)
         load_k(1)
         for cu in range(4):
             nc.sync.dma_start(
@@ -191,7 +195,7 @@ def tile_multiheadselfattention_pa_kernel(tc, q_proj, k_proj, x, w_v, out):
         def v_exit(h, g):
             if g == 0:
                 held[("gv", h)] = stage.tile([P, 1024], BF16, name="gv", tag="gv", align_bytes=64)
-            nc.scalar.copy(
+            (nc.vector.tensor_copy if (2 * h + g) % 3 == 2 else nc.scalar.copy)(
                 out=held[("gv", h)][:, 512 * g:512 * g + 512].rearrange("p (c t) -> p c t", t=4),
                 in_=held[("vp", h, g)][:].rearrange("p t c -> p c t"),
             )
@@ -217,26 +221,35 @@ def tile_multiheadselfattention_pa_kernel(tc, q_proj, k_proj, x, w_v, out):
                 out=q_T[ib][:, P * h0:P * h1], in_=held[("qt", ib, h0)][:, h0:h1, :].rearrange("p h i -> p (h i)"),
             )
 
-        side = [(q_tensor, q_exit, None, (3, 0, H)), (q_tensor, q_exit, None, (7, 4, H))]
+        def q_side(ib, h0, h1):
+            side.append((q_tensor, q_exit, None, (ib, h0, h1)))
+
+        SIDE_STEP = -2
+        side = []
         for gu in range(4):
             for a in range(2):
                 side.append((x_tensor, x_exit, x_quantise, (gu, a)))
-            if gu >= 2:
-                side.append((q_tensor, q_exit, None, ((6, 2)[gu - 2], 0, H)))
+            if gu == 0:
+                q_side(3, 0, H)
+                q_side(7, 4, H)
+        q_side(6, 0, H)
         for h in range(H):
             for g in range(2):
                 side.append((v_tensor, v_exit, v_quantise, (h, g)))
             if h == 3:
-                V_LOW = len(side) + 2
-            if h in (3, 4, 5, 6):
-                side.append((q_tensor, q_exit, None, ((5, 1, 4, 0)[h - 3], 0, H)))
-        V_ALL = len(side) + 2
+                V_LOW = SIDE_STEP + len(side) + 2
+            if h in (1, 3, 5):
+                q_side((2, 5, 1)[h // 2], 0, H)
+        V_ALL = SIDE_STEP + len(side) + 2
+        q_side(4, 0, H)
+        q_side(0, 0, H)
         w_parts = [(c, 256 * j) for j in range(4) for c in range(2)]
         W_STEP = 5
 
         def side_part(k, part):
-            if 0 <= k - part < len(side) and side[k - part][part] is not None:
-                side[k - part][part](*side[k - part][3])
+            i = k - part - SIDE_STEP
+            if 0 <= i < len(side) and side[i][part] is not None:
+                side[i][part](*side[i][3])
 
         def w_part(k, part):
             if 0 <= k - W_STEP - part < len(w_parts):
@@ -319,24 +332,17 @@ def tile_multiheadselfattention_pa_kernel(tc, q_proj, k_proj, x, w_v, out):
                 nc.tensor.transpose(st[n]["et"][:, su, :], ew[:, P * su:P * su + P], ident_f[:])
 
         def exits(n):
-            if n % 2 == 0:
-                st[n]["ge"] = work.tile([P, 2048], BF16, name="ge", tag="ge", align_bytes=64, bufs=2)
-            else:
-                st[n]["ge"] = st[n - 1]["ge"]
-            gew = st[n]["ge"][:].bitcast(F32)
-            w0 = 512 * (n % 2)
+            ge = work.tile([P, 1024], BF16, name="ge", tag="ge", align_bytes=64, bufs=3)
             nc.scalar.copy(
-                out=gew[:, w0:w0 + 512].rearrange("p (s i u) -> p s i u", s=2, u=2),
+                out=ge[:].bitcast(F32).rearrange("p (s i u) -> p s i u", s=2, u=2),
                 in_=st[n]["et"][:].rearrange("p (s u) i -> p s i u", u=2),
             )
+            st[n]["ge"] = ge
 
         def quantise(n):
-            if n % 2 == 0:
-                return
-            e_codes = work.tile([P, 512], U32, name="e_codes", tag="e_codes", align_bytes=64, bufs=N_PAIRS)
-            e_scales = work.tile([P, 512], U8, name="e_scales", tag="e_scales", align_bytes=64, bufs=N_PAIRS)
+            e_codes = work.tile([P, 2 * P], U32, name="e_codes", tag="e_codes", align_bytes=64, bufs=N_CODES)
+            e_scales = work.tile([P, 2 * P], U8, name="e_scales", tag="e_scales", align_bytes=64, bufs=N_CODES)
             nc.vector.quantize_mx(out=e_codes[:].bitcast(FP8X4), scales=e_scales[:], in_=st[n]["ge"][:])
-            st[n - 1]["codes"] = (e_codes, e_scales)
             st[n]["codes"] = (e_codes, e_scales)
 
         def quad_end(n):
@@ -362,8 +368,8 @@ def tile_multiheadselfattention_pa_kernel(tc, q_proj, k_proj, x, w_v, out):
                 for si, (h, g) in enumerate(duos[n][1]):
                     nc.tensor.matmul_mx(
                         out=pv[:, h % 4, :],
-                        lhsT=e_codes[:, 256 * (n % 2) + P * si:256 * (n % 2) + P * si + P].bitcast(FP8X4),
-                        lhsT_scale=e_scales[:, 256 * (n % 2) + P * si:256 * (n % 2) + P * si + P],
+                        lhsT=e_codes[:, P * si:P * si + P].bitcast(FP8X4),
+                        lhsT_scale=e_scales[:, P * si:P * si + P],
                         rhs=v_codes[:, h, g, :].bitcast(FP8X4),
                         rhs_scale=v_scales[:, h, g, :],
                         start=(g == 0), stop=(g == ib // 4),

@@ -1,4 +1,5 @@
 from contextlib import ExitStack
+from functools import partial
 
 import concourse.mybir as mybir
 from concourse.masks import make_identity
@@ -21,8 +22,9 @@ SCALE = 128.0 ** -0.5
 NEG = -(2.0 ** 40)
 FLOPS = 2 * S * D * D + 2 * (2 * H * (512 * 512 + 512 * 1024) * 128)
 
-N_E = 2
 N_CODES = 34
+SIDE_STEP = -2
+W_STEP = 5
 
 
 def tile_multiheadselfattention_pa_kernel(tc, q_proj, k_proj, x, w_v, out):
@@ -38,44 +40,44 @@ def tile_multiheadselfattention_pa_kernel(tc, q_proj, k_proj, x, w_v, out):
         stage = ctx.enter_context(tc.tile_pool(name="stage", bufs=2))
         work = ctx.enter_context(tc.tile_pool(name="work", bufs=4))
         small = ctx.enter_context(tc.tile_pool(name="small", bufs=6))
-        ps_sc = ctx.enter_context(tc.psum_pool(name="ps_sc", bufs=4))
-        ps_et = ctx.enter_context(tc.psum_pool(name="ps_et", bufs=2))
-        ps_aux = ctx.enter_context(tc.psum_pool(name="ps_aux", bufs=2))
+        ps_sc = ctx.enter_context(tc.psum_pool(name="ps_sc", bufs=5))
+        ps_aux = ctx.enter_context(tc.psum_pool(name="ps_aux", bufs=3))
 
         k_sb = keep.tile([P, 8, D], BF16, name="k_sb")
-        q_sb = {}
-        x4 = []
         w_raw = keep.tile([P, 8, D], BF16, name="w_raw")
-
-        def load_k(hq):
-            for j in range(2):
-                nc.sync.dma_start(
-                    out=k_sb[:, 4 * j:4 * j + 4, 512 * hq:512 * hq + 512],
-                    in_=k2[512 * j:512 * j + 512, 512 * hq:512 * hq + 512].rearrange("(m p) d -> p m d", p=P),
-                )
-
+        q_sb = {}
+        q_T = {}
+        x4 = {}
         for ib in range(8):
             q_sb[ib] = keep.tile([P, D], BF16, name="q_sb_%d" % ib)
+            q_T[ib] = keep.tile([P, D], BF16, name="q_T_%d" % ib)
+
+        def load_k(c0, c1):
+            for j in range(2):
+                nc.sync.dma_start(
+                    out=k_sb[:, 4 * j:4 * j + 4, c0:c1],
+                    in_=k2[512 * j:512 * j + 512, c0:c1].rearrange("(m p) d -> p m d", p=P),
+                )
 
         def load_q(ib, c0, c1):
             nc.sync.dma_start(out=q_sb[ib][:, c0:c1], in_=q2[P * ib:P * ib + P, c0:c1])
 
         def load_x(gu):
-            xt_sb = keep.tile([P, 2048], BF16, name="x4_%d" % gu)
+            x4[gu] = keep.tile([P, 2048], BF16, name="x4_%d" % gu)
             nc.sync.dma_start(
-                out=xt_sb[:].rearrange("p (b k) -> p b k", b=2),
+                out=x4[gu][:].rearrange("p (b k) -> p b k", b=2),
                 in_=x2[256 * gu:256 * gu + 256, :].rearrange("(b p) k -> p b k", p=P),
             )
-            x4.append(xt_sb)
 
-        load_q(7, 0, 512)
-        load_k(0)
+        load_q(7, 0, 256)
+        load_k(0, 256)
+        load_k(256, 512)
+        load_q(7, 256, D)
         load_x(0)
         load_q(3, 0, D)
-        load_q(7, 512, D)
         for gu in range(1, 4):
             load_x(gu)
-        load_k(1)
+        load_k(512, D)
         for cu in range(4):
             nc.sync.dma_start(
                 out=w_raw[:, 2 * cu:2 * cu + 2, :],
@@ -94,74 +96,69 @@ def tile_multiheadselfattention_pa_kernel(tc, q_proj, k_proj, x, w_v, out):
             out=mask_f[:], in_=mask_f[:], compare_op=ALU.is_ge, fill=NEG,
             base=0, pattern=[[-1, P]], channel_multiplier=1,
         )
-        mask_b = const.tile([P, P], BF16, name="mask_b")
-        nc.vector.tensor_copy(
-            out=mask_b[:].rearrange("p (dh m dl) -> p dh m dl", m=8, dl=2),
-            in_=mask_f[:].rearrange("p (dh dl m) -> p dh m dl", m=8, dl=2),
-        )
-        perm_f = const.tile([P, P], F32, name="perm_f")
-        nc.vector.tensor_copy(
-            out=perm_f[:].rearrange("p (dl dh m) -> p dl dh m", dl=2, m=8),
-            in_=ident_f[:].rearrange("p (dh dl m) -> p dl dh m", dl=2, m=8),
-        )
         warm = const.tile([P, 2], F32, name="warm")
         nc.vector.memset(warm[:], 0.0)
         warm2 = const.tile([P, 2], F32, name="warm2")
         nc.scalar.activation(out=warm2[:], in_=warm[:], func=ACT.Exp)
+        mask_b = const.tile([P, P], BF16, name="mask_b")
+        perm_f = const.tile([P, P], F32, name="perm_f")
+        for a in range(2):
+            nc.vector.tensor_copy(
+                out=mask_b[:].rearrange("p (a r m e) -> p a r m e", a=2, m=4, e=2)[:, a],
+                in_=mask_f[:].rearrange("p (r e a m) -> p a r m e", e=2, a=2, m=4)[:, a],
+            )
+            nc.vector.tensor_copy(
+                out=perm_f[:].rearrange("p (a e r m) -> p a e r m", a=2, e=2, m=4)[:, a],
+                in_=ident_f[:].rearrange("p (r e a m) -> p a e r m", e=2, a=2, m=4)[:, a],
+            )
 
         e_ring = {}
-        for kind in ("big", "small"):
-            for ibl in range(3):
-                ring = []
-                for r in range(N_E):
-                    e_t = keep.tile([P, 1024], BF16, name="e_%s%d_%d" % (kind, ibl, r), align_bytes=64)
-                    words = e_t[:].bitcast(I32).rearrange("p (s w) -> p s w", s=2)
-                    w0 = 64 * (ibl + 1)
-                    if kind == "big":
-                        nc.vector.memset(words[:, 1, w0:256], 0)
-                    else:
-                        nc.vector.memset(words[:, :, w0:256], 0)
-                    ring.append(e_t)
-                e_ring[(kind, ibl)] = ring
-        ring = []
-        for r in range(N_E):
-            e_t = keep.tile([P, 1024], BF16, name="e_full_%d" % r, align_bytes=64)
-            ring.append(e_t)
-        e_ring[("big", 3)] = ring
-        e_ring[("small", 3)] = ring
+        for kind, count in (("whole4", 4), ("whole3", 4), ("half", 2), ("quarter", 2)):
+            for r in range(count):
+                e_t = keep.tile([P, 512], BF16, name="e_%s_%d" % (kind, r), align_bytes=64)
+                words = e_t[:].bitcast(I32)
+                if kind == "whole3":
+                    nc.vector.memset(words.rearrange("p (a w) -> p a w", a=2)[:, :, 96:128], 0)
+                e_ring.setdefault(kind, []).append(e_t)
 
-        x_codes = keep.tile([P, 4, 512], U32, name="x_codes", align_bytes=64)
-        x_scales = keep.tile([P, 4, 512], U8, name="x_scales", align_bytes=64)
+        x_codes = keep.tile([P, 2, 2, 512], U32, name="x_codes", align_bytes=64)
+        x_scales = keep.tile([P, 2, 2, 512], U8, name="x_scales", align_bytes=64)
         w_codes = keep.tile([P, 2, D], U32, name="w_codes", align_bytes=64)
         w_scales = keep.tile([P, 2, D], U8, name="w_scales", align_bytes=64)
         v_codes = keep.tile([P, H, 2, P], U32, name="v_codes", align_bytes=64)
         v_scales = keep.tile([P, H, 2, P], U8, name="v_scales", align_bytes=64)
-        q_T = {}
+        v_part = {1: (v_codes, v_scales)}
+        for share in (2, 4):
+            part_codes = keep.tile([P, H, 2, P], U32, name="v_codes_%d" % share, align_bytes=64)
+            part_scales = keep.tile([P, H, 2, P], U8, name="v_scales_%d" % share, align_bytes=64)
+            nc.gpsimd.memset(part_codes[:], 0)
+            nc.gpsimd.memset(part_scales[:].bitcast(U32), 0)
+            v_part[share] = (part_codes, part_scales)
         held = {}
 
-        def x_tensor(gu, a):
-            xw = x4[gu][:].bitcast(F32)
+        def x_tensor(g, b):
+            xw = x4[2 * g + b // 2][:].bitcast(F32)
             xt = ps_aux.tile([P, 4, P], F32, name="xt", tag="aux")
             for c in range(2):
                 for u in range(2):
-                    c0 = 512 * a + 256 * c + P * u
+                    c0 = 512 * (b % 2) + 256 * c + P * u
                     nc.tensor.transpose(xt[:, 2 * u + c, :], xw[:, c0:c0 + P], perm_f[:])
-            held[("xt", gu, a)] = xt
+            held[("xt", g, b)] = xt
 
-        def x_exit(gu, a):
-            if a == 0:
-                held[("gx", gu)] = stage.tile([P, 2048], BF16, name="gx", tag="gx", align_bytes=64)
-            gxw = held[("gx", gu)][:].bitcast(F32).rearrange("p (ce a s u) -> p ce a s u", ce=4, a=2, u=2)
+        def x_exit(g, b):
+            if b == 0:
+                held[("gx", g)] = stage.tile([P, 4096], BF16, name="gx", tag="gx", align_bytes=64)
+            gxw = held[("gx", g)][:].bitcast(F32).rearrange("p (ct b s u) -> p ct b s u", ct=8, b=4, u=2)
             nc.scalar.copy(
-                out=gxw[:, :, a, :, :],
-                in_=held[("xt", gu, a)][:].rearrange("p (u c) (e s) -> p (c e) s u", u=2, e=2),
+                out=gxw[:, :, b, :, :],
+                in_=held[("xt", g, b)][:].rearrange("p (u c) (t s) -> p (c t) s u", u=2, t=4),
             )
 
-        def x_quantise(gu, a):
-            if a == 1:
-                nc.vector.quantize_mx(
-                    out=x_codes[:, gu, :].bitcast(FP8X4), scales=x_scales[:, gu, :], in_=held[("gx", gu)][:],
-                )
+        def x_quantise(g, c):
+            nc.vector.quantize_mx(
+                out=x_codes[:, g, c, :].bitcast(FP8X4), scales=x_scales[:, g, c, :],
+                in_=held[("gx", g)][:, 2048 * c:2048 * c + 2048],
+            )
 
         def w_regroup(c, n0):
             gw = stage.tile([P, 1024], BF16, name="gw", tag="gw", align_bytes=64)
@@ -181,11 +178,10 @@ def tile_multiheadselfattention_pa_kernel(tc, q_proj, k_proj, x, w_v, out):
             vp = ps_aux.tile([P, 4, P], F32, name="vp", tag="aux")
             for t in range(4):
                 for c in range(2):
-                    x0 = 256 * c + P * (t % 2)
                     nc.tensor.matmul_mx(
                         out=vp[:, t, :],
-                        lhsT=x_codes[:, 2 * g + t // 2, x0:x0 + P].bitcast(FP8X4),
-                        lhsT_scale=x_scales[:, 2 * g + t // 2, x0:x0 + P],
+                        lhsT=x_codes[:, g, c, P * t:P * t + P].bitcast(FP8X4),
+                        lhsT_scale=x_scales[:, g, c, P * t:P * t + P],
                         rhs=w_codes[:, c, P * h:P * h + P].bitcast(FP8X4),
                         rhs_scale=w_scales[:, c, P * h:P * h + P],
                         start=(c == 0), stop=(c == 1),
@@ -195,20 +191,31 @@ def tile_multiheadselfattention_pa_kernel(tc, q_proj, k_proj, x, w_v, out):
         def v_exit(h, g):
             if g == 0:
                 held[("gv", h)] = stage.tile([P, 1024], BF16, name="gv", tag="gv", align_bytes=64)
-            (nc.vector.tensor_copy if (2 * h + g) % 3 == 2 else nc.scalar.copy)(
+            (nc.vector.tensor_copy if g == 1 else nc.scalar.copy)(
                 out=held[("gv", h)][:, 512 * g:512 * g + 512].rearrange("p (c t) -> p c t", t=4),
                 in_=held[("vp", h, g)][:].rearrange("p t c -> p c t"),
             )
 
-        def v_quantise(h, g):
-            if g == 1:
-                nc.vector.quantize_mx(
-                    out=v_codes[:, h, :, :].rearrange("p g c -> p (g c)").bitcast(FP8X4),
-                    scales=v_scales[:, h, :, :].rearrange("p g c -> p (g c)"), in_=held[("gv", h)][:],
-                )
+        def v_quantise(h):
+            nc.vector.quantize_mx(
+                out=v_codes[:, h, :, :].rearrange("p g c -> p (g c)").bitcast(FP8X4),
+                scales=v_scales[:, h, :, :].rearrange("p g c -> p (g c)"), in_=held[("gv", h)][:],
+            )
+            if h % 4 == 3:
+                v_parts(h // 4)
 
-        for ib in range(8):
-            q_T[ib] = keep.tile([P, D], BF16, name="q_T_%d" % ib)
+        def v_parts(hq):
+            for share in (2, 4):
+                live = P // share
+                for i in range(share):
+                    for whole, part, rows in (
+                        (v_codes, v_part[share][0], [(0, live)]),
+                        (v_scales, v_part[share][1], [(r, r + 4) for r in range(0, live, 32)]),
+                    ):
+                        for r0, r1 in rows:
+                            src = whole[r0:r1, 4 * hq + i:4 * hq + 4:share, :, :].rearrange("p j g c -> p j (g c)")
+                            dst = part[live * i + r0:live * i + r1, 4 * hq + i:4 * hq + 4:share, :, :].rearrange("p j g c -> p j (g c)")
+                            nc.sync.dma_start(out=dst.bitcast(I32), in_=src.bitcast(I32))
 
         def q_tensor(ib, h0, h1):
             qt = ps_aux.tile([P, H, P], BF16, name="qt", tag="aux")
@@ -217,39 +224,45 @@ def tile_multiheadselfattention_pa_kernel(tc, q_proj, k_proj, x, w_v, out):
             held[("qt", ib, h0)] = qt
 
         def q_exit(ib, h0, h1):
-            nc.vector.tensor_copy(
+            (nc.scalar.copy if ib in (6, 2) else nc.vector.tensor_copy)(
                 out=q_T[ib][:, P * h0:P * h1], in_=held[("qt", ib, h0)][:, h0:h1, :].rearrange("p h i -> p (h i)"),
             )
 
-        def q_side(ib, h0, h1):
-            side.append((q_tensor, q_exit, None, (ib, h0, h1)))
-
-        SIDE_STEP = -2
         side = []
-        for gu in range(4):
-            for a in range(2):
-                side.append((x_tensor, x_exit, x_quantise, (gu, a)))
-            if gu == 0:
-                q_side(3, 0, H)
-                q_side(7, 4, H)
-        q_side(6, 0, H)
+
+        def q_side(ib, h0, h1, quantising=None):
+            side.append((partial(q_tensor, ib, h0, h1), partial(q_exit, ib, h0, h1), quantising))
+
+        def x_side(g, b, quantising=None):
+            side.append((partial(x_tensor, g, b), partial(x_exit, g, b), quantising))
+
+        q_side(7, 2, H)
+        x_side(0, 0)
+        x_side(0, 1)
+        q_side(3, 0, H)
+        x_side(0, 2)
+        x_side(0, 3, partial(x_quantise, 0, 0))
+        x_side(1, 0, partial(x_quantise, 0, 1))
+        x_side(1, 1)
+        x_side(1, 2)
+        x_side(1, 3, partial(x_quantise, 1, 0))
+        q_side(6, 0, H, partial(x_quantise, 1, 1))
         for h in range(H):
             for g in range(2):
-                side.append((v_tensor, v_exit, v_quantise, (h, g)))
+                side.append((partial(v_tensor, h, g), partial(v_exit, h, g), partial(v_quantise, h) if g == 1 else None))
             if h == 3:
                 V_LOW = SIDE_STEP + len(side) + 2
-            if h in (1, 3, 5):
+            if h in (0, 2, 4):
                 q_side((2, 5, 1)[h // 2], 0, H)
         V_ALL = SIDE_STEP + len(side) + 2
         q_side(4, 0, H)
         q_side(0, 0, H)
         w_parts = [(c, 256 * j) for j in range(4) for c in range(2)]
-        W_STEP = 5
 
         def side_part(k, part):
             i = k - part - SIDE_STEP
             if 0 <= i < len(side) and side[i][part] is not None:
-                side[i][part](*side[i][3])
+                side[i][part]()
 
         def w_part(k, part):
             if 0 <= k - W_STEP - part < len(w_parts):
@@ -263,39 +276,51 @@ def tile_multiheadselfattention_pa_kernel(tc, q_proj, k_proj, x, w_v, out):
                 for h in range(4 * hq, 4 * hq + 4, 2):
                     duos.append((ib - 4, [(h, 0), (h + 1, 0)]))
         n_duos = len(duos)
-        st = [dict() for n in range(n_duos)]
+        st = [{"parts": [], "sc": []} for n in range(n_duos)]
         quad = {}
+        used = {}
+        e_tiles = {}
+        codes = {}
 
         def blocks(ib, g):
             return (ib % 4 + 1) if g == ib // 4 else 4
 
+        def sharing(ib, g):
+            return {1: 4, 2: 2, 3: 1, 4: 1}[blocks(ib, g)]
+
+        def e_key(ib, h, g):
+            return (ib, h - h % sharing(ib, g), g)
+
         def qk(n, si):
             ib, slots = duos[n]
-            st[n].setdefault("sc", [])
-            for h, g in slots[si:si + 1]:
-                diag = (g == ib // 4)
-                ncol = P * blocks(ib, g)
-                sc = ps_sc.tile([P, 512], F32, name="sc", tag="sc")
+            h, g = slots[si]
+            diag = (g == ib // 4)
+            ncol = 64 * blocks(ib, g)
+            sc = ps_sc.tile([P, 2, 256], F32, name="sc", tag="sc")
+            for a in range(2):
+                d0 = P * h + 64 * g
                 nc.tensor.matmul(
-                    out=sc[:, 0:ncol].rearrange("p (dh m dl) -> p m dh dl", m=8, dl=2),
+                    out=sc[:, a, 0:ncol].rearrange("p (r m e) -> p m r e", m=4, e=2),
                     lhsT=q_T[ib][:, P * h:P * h + P],
-                    rhs=k_sb[:, :, P * h + 64 * g:P * h + 64 * g + ncol // 8].rearrange("p m (dh dl) -> p m dh dl", dl=2),
+                    rhs=k_sb[:, 4 * a:4 * a + 4, d0:d0 + ncol // 4].rearrange("p m (r e) -> p m r e", e=2),
                     start=True, stop=(not diag),
                 )
                 if diag:
-                    c0 = P * (ib % 4)
                     nc.tensor.matmul(
-                        out=sc[:, c0:c0 + P], lhsT=ident_b[:], rhs=mask_b[:], start=False, stop=True,
+                        out=sc[:, a, ncol - 64:ncol], lhsT=ident_b[:], rhs=mask_b[:, 64 * a:64 * a + 64],
+                        start=False, stop=True,
                     )
-                st[n]["sc"].append(sc)
+            st[n]["sc"].append(sc)
 
         def row_max(n, si):
             ib, slots = duos[n]
             if si == 0:
                 st[n]["m2"] = small.tile([P, 2], F32, name="m2", tag="m2")
             h, g = slots[si]
-            ncol = P * blocks(ib, g)
-            nc.vector.tensor_reduce(out=st[n]["m2"][:, si:si + 1], in_=st[n]["sc"][si][:, 0:ncol], axis=AX.X, op=ALU.max)
+            ncol = 64 * blocks(ib, g)
+            nc.vector.tensor_reduce(
+                out=st[n]["m2"][:, si:si + 1], in_=st[n]["sc"][si][:, :, 0:ncol], axis=AX.XY, op=ALU.max,
+            )
 
         def biases(n):
             ib, slots = duos[n]
@@ -311,46 +336,64 @@ def tile_multiheadselfattention_pa_kernel(tc, q_proj, k_proj, x, w_v, out):
 
         def exps(n, si):
             ib, slots = duos[n]
-            if si == 0:
-                if slots[0][0] % 4 == 0:
-                    quad[(ib, slots[0][0] // 4, "rs")] = small.tile([P, 4, 2], F32, name="rs_q", tag="rs_q", bufs=4)
-                st[n]["e"] = e_ring[("big" if ib >= 4 else "small", ib % 4)][n % N_E]
+            if si == 0 and slots[0][0] % 4 == 0:
+                quad[(ib, slots[0][0] // 4, "rs")] = small.tile([P, 4, 2], F32, name="rs_q", tag="rs_q", bufs=4)
             h, g = slots[si]
-            ncol = P * blocks(ib, g)
+            nblk = blocks(ib, g)
+            share = sharing(ib, g)
+            key = e_key(ib, h, g)
+            if key not in e_tiles:
+                kind = ("quarter", "half", "whole3", "whole4")[nblk - 1]
+                i = used.get(kind, 0)
+                used[kind] = i + 1
+                e_tiles[key] = e_ring[kind][i % len(e_ring[kind])]
+            e_out = e_tiles[key][:].rearrange("p (a s w) -> p a s w", a=2, s=share)[:, :, h % share, 0:64 * nblk]
             col = 0 if ib >= 4 else si
             nc.scalar.activation(
-                out=st[n]["e"][:, 512 * si:512 * si + ncol], in_=st[n]["sc"][si][:, 0:ncol], func=ACT.Exp,
+                out=e_out, in_=st[n]["sc"][si][:, :, 0:64 * nblk], func=ACT.Exp,
                 bias=st[n]["nm"][:, col:col + 1], scale=SCALE,
                 accum_out=quad[(ib, h // 4, "rs")][:, h % 4, g:g + 1],
             )
+            if h % share == share - 1:
+                st[n]["parts"].append((si, key))
 
         def transposes(n, si):
-            if si == 0:
-                st[n]["et"] = ps_et.tile([P, 4, P], F32, name="et", tag="et")
-            ew = st[n]["e"][:].bitcast(F32)
-            for su in (2 * si, 2 * si + 1):
-                nc.tensor.transpose(st[n]["et"][:, su, :], ew[:, P * su:P * su + P], ident_f[:])
+            for j, (sj, key) in enumerate(st[n]["parts"]):
+                if sj == si:
+                    if j == 0:
+                        st[n]["et"] = ps_aux.tile([P, 4, P], F32, name="et", tag="aux")
+                    ew = e_tiles[key][:].bitcast(F32)
+                    for a in range(2):
+                        nc.tensor.transpose(st[n]["et"][:, 2 * j + a, :], ew[:, P * a:P * a + P], ident_f[:])
 
         def exits(n):
+            count = len(st[n]["parts"])
+            if count == 0:
+                return
             ge = work.tile([P, 1024], BF16, name="ge", tag="ge", align_bytes=64, bufs=3)
             nc.scalar.copy(
-                out=ge[:].bitcast(F32).rearrange("p (s i u) -> p s i u", s=2, u=2),
-                in_=st[n]["et"][:].rearrange("p (s u) i -> p s i u", u=2),
+                out=ge[:].bitcast(F32)[:, 0:256 * count].rearrange("p (s i a) -> p s i a", s=count, a=2),
+                in_=st[n]["et"][:, 0:2 * count, :].rearrange("p (s a) i -> p s i a", a=2),
             )
             st[n]["ge"] = ge
 
         def quantise(n):
+            count = len(st[n]["parts"])
+            if count == 0:
+                return
             e_codes = work.tile([P, 2 * P], U32, name="e_codes", tag="e_codes", align_bytes=64, bufs=N_CODES)
             e_scales = work.tile([P, 2 * P], U8, name="e_scales", tag="e_scales", align_bytes=64, bufs=N_CODES)
-            nc.vector.quantize_mx(out=e_codes[:].bitcast(FP8X4), scales=e_scales[:], in_=st[n]["ge"][:])
-            st[n]["codes"] = (e_codes, e_scales)
+            nc.vector.quantize_mx(
+                out=e_codes[:, 0:P * count].bitcast(FP8X4), scales=e_scales[:, 0:P * count], in_=st[n]["ge"][:, 0:512 * count],
+            )
+            for j, (sj, key) in enumerate(st[n]["parts"]):
+                codes[key] = (e_codes[:, P * j:P * j + P], e_scales[:, P * j:P * j + P])
 
         def quad_end(n):
             return 0 <= n < n_duos and duos[n][1][-1][0] % 4 == 3
 
-        ends = [n for n in range(n_duos) if quad_end(n)]
         pv_at = {}
-        waiting = list(ends)
+        waiting = [n for n in range(n_duos) if quad_end(n)]
         for k in range(n_duos + 5):
             ready = [n for n in waiting if k >= n + 4 and k >= (V_LOW if duos[n][1][-1][0] < 4 else V_ALL)]
             if ready:
@@ -362,16 +405,16 @@ def tile_multiheadselfattention_pa_kernel(tc, q_proj, k_proj, x, w_v, out):
             hq = slots[-1][0] // 4
             pv = ps_aux.tile([P, 4, P], F32, name="pv", tag="aux")
             quad[(ib, hq, "pv")] = pv
-            n_first = n_last - (3 if ib >= 4 else 1)
-            for n in range(n_first, n_last + 1):
-                e_codes, e_scales = st[n]["codes"]
-                for si, (h, g) in enumerate(duos[n][1]):
+            for h in range(4 * hq, 4 * hq + 4):
+                for g in range(ib // 4 + 1):
+                    e_codes, e_scales = codes[e_key(ib, h, g)]
+                    part_codes, part_scales = v_part[sharing(ib, g)]
                     nc.tensor.matmul_mx(
                         out=pv[:, h % 4, :],
-                        lhsT=e_codes[:, P * si:P * si + P].bitcast(FP8X4),
-                        lhsT_scale=e_scales[:, P * si:P * si + P],
-                        rhs=v_codes[:, h, g, :].bitcast(FP8X4),
-                        rhs_scale=v_scales[:, h, g, :],
+                        lhsT=e_codes.bitcast(FP8X4),
+                        lhsT_scale=e_scales,
+                        rhs=part_codes[:, h, g, :].bitcast(FP8X4),
+                        rhs_scale=part_scales[:, h, g, :],
                         start=(g == 0), stop=(g == ib // 4),
                     )
 
@@ -397,10 +440,15 @@ def tile_multiheadselfattention_pa_kernel(tc, q_proj, k_proj, x, w_v, out):
             ib, slots = duos[n]
             hq = slots[-1][0] // 4
             o_sb = work.tile([P, 512], F32, name="o_sb", tag="o_sb", bufs=3)
-            nc.vector.tensor_tensor(
-                out=o_sb[:].rearrange("p (h c) -> p h c", h=4), in0=quad[(ib, hq, "pv")][:],
-                in1=quad[(ib, hq, "rinv")][:].unsqueeze(2).to_broadcast([P, 4, P]), op=ALU.mult,
-            )
+            pv, rinv = quad[(ib, hq, "pv")], quad[(ib, hq, "rinv")]
+            if False:
+                for j in range(4):
+                    nc.scalar.activation(out=o_sb[:, P * j:P * j + P], in_=pv[:, j, :], func=ACT.Copy, scale=rinv[:, j:j + 1])
+            else:
+                nc.vector.tensor_tensor(
+                    out=o_sb[:].rearrange("p (h c) -> p h c", h=4), in0=pv[:],
+                    in1=rinv[:].unsqueeze(2).to_broadcast([P, 4, P]), op=ALU.mult,
+                )
             nc.sync.dma_start(out=o2[P * ib:P * ib + P, 512 * hq:512 * hq + 512], in_=o_sb[:])
 
         def run(stage_fn, n, *more):
@@ -408,8 +456,8 @@ def tile_multiheadselfattention_pa_kernel(tc, q_proj, k_proj, x, w_v, out):
                 stage_fn(n, *more)
 
         with tc.manual_schedule():
-            q_tensor(7, 0, 4)
-            q_exit(7, 0, 4)
+            q_tensor(7, 0, 2)
+            q_exit(7, 0, 2)
             for k in range(-2, n_duos + 6):
                 run(exps, k, 0)
                 run(exps, k, 1)

@@ -24,7 +24,6 @@ FLOPS = 2 * S * D * D + 2 * (2 * H * (512 * 512 + 512 * 1024) * 128)
 
 N_CODES = 34
 SIDE_STEP = -2
-W_STEP = 5
 
 
 def tile_multiheadselfattention_pa_kernel(tc, q_proj, k_proj, x, w_v, out):
@@ -45,12 +44,8 @@ def tile_multiheadselfattention_pa_kernel(tc, q_proj, k_proj, x, w_v, out):
 
         k_sb = keep.tile([P, 8, D], BF16, name="k_sb")
         w_raw = keep.tile([P, 8, D], BF16, name="w_raw")
-        q_sb = {}
-        q_T = {}
+        q_sb = keep.tile([P, 8, D], BF16, name="q_sb")
         x4 = {}
-        for ib in range(8):
-            q_sb[ib] = keep.tile([P, D], BF16, name="q_sb_%d" % ib)
-            q_T[ib] = keep.tile([P, D], BF16, name="q_T_%d" % ib)
 
         def load_k(c0, c1):
             for j in range(2):
@@ -59,8 +54,15 @@ def tile_multiheadselfattention_pa_kernel(tc, q_proj, k_proj, x, w_v, out):
                     in_=k2[512 * j:512 * j + 512, c0:c1].rearrange("(m p) d -> p m d", p=P),
                 )
 
-        def load_q(ib, c0, c1):
-            nc.sync.dma_start(out=q_sb[ib][:, c0:c1], in_=q2[P * ib:P * ib + P, c0:c1])
+        def load_q(ibs, c0, c1):
+            nc.sync.dma_start(out=q_sb[:, ibs, c0:c1], in_=q2[:, c0:c1].rearrange("(i p) c -> p i c", p=P)[:, ibs, :])
+
+        def load_w(c0, c1):
+            for cu in range(4):
+                nc.sync.dma_start(
+                    out=w_raw[:, 2 * cu:2 * cu + 2, c0:c1],
+                    in_=w_v[256 * cu:256 * cu + 256, c0:c1].rearrange("(p e) n -> p e n", e=2),
+                )
 
         def load_x(gu):
             x4[gu] = keep.tile([P, 2048], BF16, name="x4_%d" % gu)
@@ -69,22 +71,21 @@ def tile_multiheadselfattention_pa_kernel(tc, q_proj, k_proj, x, w_v, out):
                 in_=x2[256 * gu:256 * gu + 256, :].rearrange("(b p) k -> p b k", p=P),
             )
 
-        load_q(7, 0, 256)
+        load_q(slice(7, 8), 0, 256)
         load_k(0, 256)
+        load_q(slice(7, 8), 256, 512)
         load_k(256, 512)
-        load_q(7, 256, D)
         load_x(0)
-        load_q(3, 0, D)
+        load_q(slice(3, 7, 3), 0, 512)
         for gu in range(1, 4):
             load_x(gu)
+        load_w(0, 512)
+        load_q(slice(0, 3), 0, 512)
+        load_q(slice(4, 6), 0, 512)
         load_k(512, D)
-        for cu in range(4):
-            nc.sync.dma_start(
-                out=w_raw[:, 2 * cu:2 * cu + 2, :],
-                in_=w_v[256 * cu:256 * cu + 256, :].rearrange("(p e) n -> p e n", e=2),
-            )
-        for ib in (6, 2, 5, 1, 4, 0):
-            load_q(ib, 0, D)
+        load_w(512, D)
+        load_q(slice(0, 4), 512, D)
+        load_q(slice(4, 8), 512, D)
 
         ident_f = const.tile([P, P], F32, name="ident_f")
         make_identity(nc, ident_f[:])
@@ -121,6 +122,15 @@ def tile_multiheadselfattention_pa_kernel(tc, q_proj, k_proj, x, w_v, out):
                     nc.vector.memset(words.rearrange("p (a w) -> p a w", a=2)[:, :, 96:128], 0)
                 e_ring.setdefault(kind, []).append(e_t)
 
+        rs_ring = []
+        for r in range(4):
+            rs_t = keep.tile([P, 8, 2], F32, name="rs_%d" % r)
+            nc.vector.memset(rs_t[:], 0.0)
+            rs_ring.append(rs_t)
+
+        def sums_of(ib, hq):
+            return rs_ring[(4 * hq + 3 - ib % 4) % 4]
+
         x_codes = keep.tile([P, 2, 2, 512], U32, name="x_codes", align_bytes=64)
         x_scales = keep.tile([P, 2, 2, 512], U8, name="x_scales", align_bytes=64)
         w_codes = keep.tile([P, 2, D], U32, name="w_codes", align_bytes=64)
@@ -154,24 +164,25 @@ def tile_multiheadselfattention_pa_kernel(tc, q_proj, k_proj, x, w_v, out):
                 in_=held[("xt", g, b)][:].rearrange("p (u c) (t s) -> p (c t) s u", u=2, t=4),
             )
 
-        def x_quantise(g, c):
-            nc.vector.quantize_mx(
-                out=x_codes[:, g, c, :].bitcast(FP8X4), scales=x_scales[:, g, c, :],
-                in_=held[("gx", g)][:, 2048 * c:2048 * c + 2048],
-            )
+        def x_quantise(g):
+            for c in range(2):
+                nc.vector.quantize_mx(
+                    out=x_codes[:, g, c, :].bitcast(FP8X4), scales=x_scales[:, g, c, :],
+                    in_=held[("gx", g)][:, 2048 * c:2048 * c + 2048],
+                )
 
         def w_regroup(c, n0):
-            gw = stage.tile([P, 1024], BF16, name="gw", tag="gw", align_bytes=64)
+            gw = stage.tile([P, 2048], BF16, name="gw", tag="gw", align_bytes=64)
             held[("gw", c, n0)] = gw
             nc.vector.tensor_copy(
                 out=gw[:].rearrange("p (c i t) -> p c t i", i=4, t=4),
-                in_=w_raw[:, 4 * c:4 * c + 4, n0:n0 + 256].rearrange("p t (c i) -> p c t i", i=4),
+                in_=w_raw[:, 4 * c:4 * c + 4, n0:n0 + 512].rearrange("p t (c i) -> p c t i", i=4),
             )
 
         def w_quantise(c, n0):
             nc.vector.quantize_mx(
-                out=w_codes[:, c, n0:n0 + 256].bitcast(FP8X4),
-                scales=w_scales[:, c, n0:n0 + 256], in_=held[("gw", c, n0)][:],
+                out=w_codes[:, c, n0:n0 + 512].bitcast(FP8X4),
+                scales=w_scales[:, c, n0:n0 + 512], in_=held[("gw", c, n0)][:],
             )
 
         def v_tensor(h, g):
@@ -191,7 +202,7 @@ def tile_multiheadselfattention_pa_kernel(tc, q_proj, k_proj, x, w_v, out):
         def v_exit(h, g):
             if g == 0:
                 held[("gv", h)] = stage.tile([P, 1024], BF16, name="gv", tag="gv", align_bytes=64)
-            (nc.vector.tensor_copy if g == 1 else nc.scalar.copy)(
+            (nc.vector.tensor_copy if False else nc.scalar.copy)(
                 out=held[("gv", h)][:, 512 * g:512 * g + 512].rearrange("p (c t) -> p c t", t=4),
                 in_=held[("vp", h, g)][:].rearrange("p t c -> p c t"),
             )
@@ -217,47 +228,72 @@ def tile_multiheadselfattention_pa_kernel(tc, q_proj, k_proj, x, w_v, out):
                             dst = part[live * i + r0:live * i + r1, 4 * hq + i:4 * hq + 4:share, :, :].rearrange("p j g c -> p j (g c)")
                             nc.sync.dma_start(out=dst.bitcast(I32), in_=src.bitcast(I32))
 
-        def q_tensor(ib, h0, h1):
-            qt = ps_aux.tile([P, H, P], BF16, name="qt", tag="aux")
-            for h in range(h0, h1):
-                nc.tensor.transpose(qt[:, h, :], q_sb[ib][:, P * h:P * h + P], ident_b[:])
-            held[("qt", ib, h0)] = qt
+        order = [(ib - d, hq) for hq in range(2) for ib in range(7, 3, -1) for d in (0, 4)]
+        q_T = keep.tile([P, 16, 512], BF16, name="q_T")
 
-        def q_exit(ib, h0, h1):
-            (nc.scalar.copy if ib in (6, 2) else nc.vector.tensor_copy)(
-                out=q_T[ib][:, P * h0:P * h1], in_=held[("qt", ib, h0)][:, h0:h1, :].rearrange("p h i -> p (h i)"),
+        def q_tensor(i0, i1, h0, h1):
+            qt = ps_aux.tile([P, 2, 4, P], BF16, name="qt", tag="aux")
+            for i in range(i0, i1):
+                ib, hq = order[i]
+                for h in range(h0, h1):
+                    c0 = 512 * hq + P * h
+                    nc.tensor.transpose(qt[:, i - i0, h, :], q_sb[:, ib, c0:c0 + P], ident_b[:])
+            held[("qt", i0, h0)] = qt
+
+        def q_exit(i0, i1, h0, h1):
+            n = (i1 - i0) * (h1 - h0) * P
+            (nc.scalar.copy if False else nc.vector.tensor_copy)(
+                out=q_T[:, i0:i1, :].rearrange("p i c -> p (i c)")[:, P * h0:P * h0 + n],
+                in_=held[("qt", i0, h0)][:].rearrange("p i h c -> p (i h c)")[:, P * h0:P * h0 + n],
             )
 
         side = []
+        PAUSE = (None, None, None)
 
-        def q_side(ib, h0, h1, quantising=None):
-            side.append((partial(q_tensor, ib, h0, h1), partial(q_exit, ib, h0, h1), quantising))
+        def q_side(i0, i1, h0=0, h1=4):
+            side.append((partial(q_tensor, i0, i1, h0, h1), partial(q_exit, i0, i1, h0, h1), None))
 
-        def x_side(g, b, quantising=None):
-            side.append((partial(x_tensor, g, b), partial(x_exit, g, b), quantising))
+        def x_side(g, b):
+            side.append((partial(x_tensor, g, b), partial(x_exit, g, b), partial(x_quantise, g) if b == 3 else None))
 
-        q_side(7, 2, H)
+        def v_side(h, g):
+            side.append((partial(v_tensor, h, g), partial(v_exit, h, g), partial(v_quantise, h) if g == 1 else None))
+
+        q_side(0, 1, 2, 4)
         x_side(0, 0)
         x_side(0, 1)
-        q_side(3, 0, H)
+        q_side(1, 3)
         x_side(0, 2)
-        x_side(0, 3, partial(x_quantise, 0, 0))
-        x_side(1, 0, partial(x_quantise, 0, 1))
-        x_side(1, 1)
-        x_side(1, 2)
-        x_side(1, 3, partial(x_quantise, 1, 0))
-        q_side(6, 0, H, partial(x_quantise, 1, 1))
-        for h in range(H):
+        x_side(0, 3)
+        x_side(1, 0)
+        q_side(3, 5)
+        for b in range(1, 4):
+            x_side(1, b)
+        for h in range(2):
             for g in range(2):
-                side.append((partial(v_tensor, h, g), partial(v_exit, h, g), partial(v_quantise, h) if g == 1 else None))
-            if h == 3:
-                V_LOW = SIDE_STEP + len(side) + 2
-            if h in (0, 2, 4):
-                q_side((2, 5, 1)[h // 2], 0, H)
-        V_ALL = SIDE_STEP + len(side) + 2
-        q_side(4, 0, H)
-        q_side(0, 0, H)
-        w_parts = [(c, 256 * j) for j in range(4) for c in range(2)]
+                v_side(h, g)
+        q_side(5, 7)
+        for h in range(2, 4):
+            for g in range(2):
+                v_side(h, g)
+        V_LOW = SIDE_STEP + len(side) + 1
+        q_side(7, 9)
+        for h in range(4, 8):
+            for g in range(2):
+                if h >= 7:
+                    side.append(PAUSE)
+                v_side(h, g)
+            if h == 5:
+                q_side(9, 11)
+            if h == 6:
+                q_side(11, 13)
+        V_ALL = SIDE_STEP + len(side) + 1
+        side.extend([PAUSE] * 3)
+        q_side(13, 15)
+        side.extend([PAUSE] * 5)
+        q_side(15, 16)
+
+        w_parts = {4: (0, 0), 6: (1, 0), 14: (0, 512), 16: (1, 512)}
 
         def side_part(k, part):
             i = k - part - SIDE_STEP
@@ -265,12 +301,12 @@ def tile_multiheadselfattention_pa_kernel(tc, q_proj, k_proj, x, w_v, out):
                 side[i][part]()
 
         def w_part(k, part):
-            if 0 <= k - W_STEP - part < len(w_parts):
-                (w_regroup if part == 0 else w_quantise)(*w_parts[k - W_STEP - part])
+            if k - part in w_parts:
+                (w_regroup if part == 0 else w_quantise)(*w_parts[k - part])
 
         duos = []
-        for ib in range(7, 3, -1):
-            for hq in range(2):
+        for hq in range(2):
+            for ib in range(7, 3, -1):
                 for h in range(4 * hq, 4 * hq + 4):
                     duos.append((ib, [(h, 0), (h, 1)]))
                 for h in range(4 * hq, 4 * hq + 4, 2):
@@ -297,19 +333,19 @@ def tile_multiheadselfattention_pa_kernel(tc, q_proj, k_proj, x, w_v, out):
             diag = (g == ib // 4)
             ncol = 64 * blocks(ib, g)
             sc = ps_sc.tile([P, 2, 256], F32, name="sc", tag="sc")
+            d0 = P * h + 64 * g
             for a in range(2):
-                d0 = P * h + 64 * g
                 nc.tensor.matmul(
                     out=sc[:, a, 0:ncol].rearrange("p (r m e) -> p m r e", m=4, e=2),
-                    lhsT=q_T[ib][:, P * h:P * h + P],
+                    lhsT=q_T[:, order.index((ib, h // 4)), P * (h % 4):P * (h % 4) + P],
                     rhs=k_sb[:, 4 * a:4 * a + 4, d0:d0 + ncol // 4].rearrange("p m (r e) -> p m r e", e=2),
-                    start=True, stop=(not diag),
+                    start=(a == 0), stop=(a == 1 and not diag),
                 )
-                if diag:
-                    nc.tensor.matmul(
-                        out=sc[:, a, ncol - 64:ncol], lhsT=ident_b[:], rhs=mask_b[:, 64 * a:64 * a + 64],
-                        start=False, stop=True,
-                    )
+            if diag:
+                nc.tensor.matmul(
+                    out=sc[:, :, ncol - 64:ncol], lhsT=ident_b[:], rhs=mask_b[:].rearrange("p (a w) -> p a w", a=2),
+                    start=False, stop=True,
+                )
             st[n]["sc"].append(sc)
 
         def row_max(n, si):
@@ -336,8 +372,6 @@ def tile_multiheadselfattention_pa_kernel(tc, q_proj, k_proj, x, w_v, out):
 
         def exps(n, si):
             ib, slots = duos[n]
-            if si == 0 and slots[0][0] % 4 == 0:
-                quad[(ib, slots[0][0] // 4, "rs")] = small.tile([P, 4, 2], F32, name="rs_q", tag="rs_q", bufs=4)
             h, g = slots[si]
             nblk = blocks(ib, g)
             share = sharing(ib, g)
@@ -352,7 +386,7 @@ def tile_multiheadselfattention_pa_kernel(tc, q_proj, k_proj, x, w_v, out):
             nc.scalar.activation(
                 out=e_out, in_=st[n]["sc"][si][:, :, 0:64 * nblk], func=ACT.Exp,
                 bias=st[n]["nm"][:, col:col + 1], scale=SCALE,
-                accum_out=quad[(ib, h // 4, "rs")][:, h % 4, g:g + 1],
+                accum_out=sums_of(ib, h // 4)[:, 4 * (ib < 4) + h % 4, g:g + 1],
             )
             if h % share == share - 1:
                 st[n]["parts"].append((si, key))
@@ -396,7 +430,7 @@ def tile_multiheadselfattention_pa_kernel(tc, q_proj, k_proj, x, w_v, out):
         waiting = [n for n in range(n_duos) if quad_end(n)]
         for k in range(n_duos + 5):
             ready = [n for n in waiting if k >= n + 4 and k >= (V_LOW if duos[n][1][-1][0] < 4 else V_ALL)]
-            if ready:
+            if ready and (k - SIDE_STEP >= len(side) or side[k - SIDE_STEP] == PAUSE):
                 pv_at[k] = ready[0]
                 waiting.remove(ready[0])
 
@@ -421,20 +455,20 @@ def tile_multiheadselfattention_pa_kernel(tc, q_proj, k_proj, x, w_v, out):
         def row_sums(n):
             ib, slots = duos[n]
             hq = slots[-1][0] // 4
-            if ib >= 4:
-                rsum = small.tile([P, 4], F32, name="rsum", tag="rsum")
-                nc.vector.tensor_reduce(out=rsum[:], in_=quad[(ib, hq, "rs")][:], axis=AX.X, op=ALU.add)
+            if ib < 4:
+                rs = sums_of(ib, hq)
+                rsum = small.tile([P, 8], F32, name="rsum", tag="rsum")
+                nc.gpsimd.tensor_tensor(out=rsum[:], in0=rs[:, :, 0], in1=rs[:, :, 1], op=ALU.add)
                 quad[(ib, hq, "rsum")] = rsum
 
         def reciprocals(n):
             ib, slots = duos[n]
             hq = slots[-1][0] // 4
-            rinv = small.tile([P, 4], F32, name="rinv", tag="rinv", bufs=16)
-            if ib >= 4:
+            if ib < 4:
+                rinv = small.tile([P, 8], F32, name="rinv", tag="rinv", bufs=8)
                 nc.vector.reciprocal(out=rinv[:], in_=quad[(ib, hq, "rsum")][:])
-            else:
-                nc.vector.reciprocal(out=rinv[:], in_=quad[(ib, hq, "rs")][:, :, 0])
-            quad[(ib, hq, "rinv")] = rinv
+                quad[(ib + 4, hq, "rinv")] = rinv[:, 0:4]
+                quad[(ib, hq, "rinv")] = rinv[:, 4:8]
 
         def finish(n):
             ib, slots = duos[n]
@@ -447,7 +481,7 @@ def tile_multiheadselfattention_pa_kernel(tc, q_proj, k_proj, x, w_v, out):
             else:
                 nc.vector.tensor_tensor(
                     out=o_sb[:].rearrange("p (h c) -> p h c", h=4), in0=pv[:],
-                    in1=rinv[:].unsqueeze(2).to_broadcast([P, 4, P]), op=ALU.mult,
+                    in1=rinv.unsqueeze(2).to_broadcast([P, 4, P]), op=ALU.mult,
                 )
             nc.sync.dma_start(out=o2[P * ib:P * ib + P, 512 * hq:512 * hq + 512], in_=o_sb[:])
 
@@ -456,8 +490,8 @@ def tile_multiheadselfattention_pa_kernel(tc, q_proj, k_proj, x, w_v, out):
                 stage_fn(n, *more)
 
         with tc.manual_schedule():
-            q_tensor(7, 0, 2)
-            q_exit(7, 0, 2)
+            q_tensor(0, 1, 0, 2)
+            q_exit(0, 1, 0, 2)
             for k in range(-2, n_duos + 6):
                 run(exps, k, 0)
                 run(exps, k, 1)

@@ -75,17 +75,16 @@ def tile_multiheadselfattention_pa_kernel(tc, q_proj, k_proj, x, w_v, out):
         load_k(0, 256)
         load_q(slice(7, 8), 256, 512)
         load_k(256, 512)
-        load_x(0)
         load_q(slice(3, 7, 3), 0, 512)
-        for gu in range(1, 4):
+        for gu in range(4):
             load_x(gu)
-        load_w(0, 512)
-        load_q(slice(0, 3), 0, 512)
-        load_q(slice(4, 6), 0, 512)
+        load_w(0, D)
+        load_q(slice(2, 6, 3), 0, D)
+        load_q(slice(1, 5, 3), 0, D)
+        load_q(slice(0, 1), 0, D)
         load_k(512, D)
-        load_w(512, D)
-        load_q(slice(0, 4), 512, D)
-        load_q(slice(4, 8), 512, D)
+        load_q(slice(7, 8), 512, D)
+        load_q(slice(3, 7, 3), 512, D)
 
         ident_f = const.tile([P, P], F32, name="ident_f")
         make_identity(nc, ident_f[:])
@@ -141,8 +140,9 @@ def tile_multiheadselfattention_pa_kernel(tc, q_proj, k_proj, x, w_v, out):
         for share in (2, 4):
             part_codes = keep.tile([P, H, 2, P], U32, name="v_codes_%d" % share, align_bytes=64)
             part_scales = keep.tile([P, H, 2, P], U8, name="v_scales_%d" % share, align_bytes=64)
-            nc.gpsimd.memset(part_codes[:], 0)
-            nc.gpsimd.memset(part_scales[:].bitcast(U32), 0)
+            for h in range(H):
+                nc.gpsimd.memset(part_codes[:, h, :, :], 0)
+                nc.gpsimd.memset(part_scales[:, h, :, :].bitcast(U32), 0)
             v_part[share] = (part_codes, part_scales)
         held = {}
 
@@ -229,7 +229,11 @@ def tile_multiheadselfattention_pa_kernel(tc, q_proj, k_proj, x, w_v, out):
                             nc.sync.dma_start(out=dst.bitcast(I32), in_=src.bitcast(I32))
 
         order = [(ib - d, hq) for hq in range(2) for ib in range(7, 3, -1) for d in (0, 4)]
-        q_T = keep.tile([P, 16, 512], BF16, name="q_T")
+        q_T = {}
+        for i0, i1 in [(0, 1)] + [(i, i + 2) for i in range(1, 15, 2)] + [(15, 16)]:
+            q_t = keep.tile([P, i1 - i0, 512], BF16, name="q_T_%d" % i0)
+            for i in range(i0, i1):
+                q_T[i] = (q_t, i - i0)
 
         def q_tensor(i0, i1, h0, h1):
             qt = ps_aux.tile([P, 2, 4, P], BF16, name="qt", tag="aux")
@@ -243,7 +247,7 @@ def tile_multiheadselfattention_pa_kernel(tc, q_proj, k_proj, x, w_v, out):
         def q_exit(i0, i1, h0, h1):
             n = (i1 - i0) * (h1 - h0) * P
             (nc.scalar.copy if False else nc.vector.tensor_copy)(
-                out=q_T[:, i0:i1, :].rearrange("p i c -> p (i c)")[:, P * h0:P * h0 + n],
+                out=q_T[i0][0][:].rearrange("p i c -> p (i c)")[:, P * h0:P * h0 + n],
                 in_=held[("qt", i0, h0)][:].rearrange("p i h c -> p (i h c)")[:, P * h0:P * h0 + n],
             )
 
@@ -260,9 +264,9 @@ def tile_multiheadselfattention_pa_kernel(tc, q_proj, k_proj, x, w_v, out):
             side.append((partial(v_tensor, h, g), partial(v_exit, h, g), partial(v_quantise, h) if g == 1 else None))
 
         q_side(0, 1, 2, 4)
+        q_side(1, 3)
         x_side(0, 0)
         x_side(0, 1)
-        q_side(1, 3)
         x_side(0, 2)
         x_side(0, 3)
         x_side(1, 0)
@@ -293,7 +297,7 @@ def tile_multiheadselfattention_pa_kernel(tc, q_proj, k_proj, x, w_v, out):
         side.extend([PAUSE] * 5)
         q_side(15, 16)
 
-        w_parts = {4: (0, 0), 6: (1, 0), 14: (0, 512), 16: (1, 512)}
+        w_parts = {6: (0, 0), 8: (1, 0), 14: (0, 512), 16: (1, 512)}
 
         def side_part(k, part):
             i = k - part - SIDE_STEP
@@ -330,6 +334,7 @@ def tile_multiheadselfattention_pa_kernel(tc, q_proj, k_proj, x, w_v, out):
         def qk(n, si):
             ib, slots = duos[n]
             h, g = slots[si]
+            q_t, i = q_T[order.index((ib, h // 4))]
             diag = (g == ib // 4)
             ncol = 64 * blocks(ib, g)
             sc = ps_sc.tile([P, 2, 256], F32, name="sc", tag="sc")
@@ -337,7 +342,7 @@ def tile_multiheadselfattention_pa_kernel(tc, q_proj, k_proj, x, w_v, out):
             for a in range(2):
                 nc.tensor.matmul(
                     out=sc[:, a, 0:ncol].rearrange("p (r m e) -> p m r e", m=4, e=2),
-                    lhsT=q_T[:, order.index((ib, h // 4)), P * (h % 4):P * (h % 4) + P],
+                    lhsT=q_t[:, i, P * (h % 4):P * (h % 4) + P],
                     rhs=k_sb[:, 4 * a:4 * a + 4, d0:d0 + ncol // 4].rearrange("p m (r e) -> p m r e", e=2),
                     start=(a == 0), stop=(a == 1 and not diag),
                 )
@@ -458,7 +463,7 @@ def tile_multiheadselfattention_pa_kernel(tc, q_proj, k_proj, x, w_v, out):
             if ib < 4:
                 rs = sums_of(ib, hq)
                 rsum = small.tile([P, 8], F32, name="rsum", tag="rsum")
-                nc.gpsimd.tensor_tensor(out=rsum[:], in0=rs[:, :, 0], in1=rs[:, :, 1], op=ALU.add)
+                nc.vector.tensor_tensor(out=rsum[:], in0=rs[:, :, 0], in1=rs[:, :, 1], op=ALU.add)
                 quad[(ib, hq, "rsum")] = rsum
 
         def reciprocals(n):
@@ -499,6 +504,10 @@ def tile_multiheadselfattention_pa_kernel(tc, q_proj, k_proj, x, w_v, out):
                 run(row_max, k + 1, 0)
                 run(row_max, k + 1, 1)
                 run(quantise, k - 2)
+                if quad_end(k - 1):
+                    row_sums(k - 1)
+                if quad_end(k - 2):
+                    reciprocals(k - 2)
                 run(biases, k + 1)
                 side_part(k, 1)
                 if k - 1 in pv_at:
@@ -506,10 +515,6 @@ def tile_multiheadselfattention_pa_kernel(tc, q_proj, k_proj, x, w_v, out):
                 side_part(k, 2)
                 w_part(k, 1)
                 w_part(k, 0)
-                if quad_end(k - 1):
-                    row_sums(k - 1)
-                if quad_end(k - 2):
-                    reciprocals(k - 2)
                 run(qk, k + 2, 0)
                 run(transposes, k, 0)
                 run(qk, k + 2, 1)

@@ -101,15 +101,15 @@ def tile_multiheadselfattention_pa_kernel(tc, q_proj, k_proj, x, w_v, out):
         warm2 = const.tile([P, 2], F32, name="warm2")
         nc.scalar.activation(out=warm2[:], in_=warm[:], func=ACT.Exp)
         mask_b = const.tile([P, P], BF16, name="mask_b")
+        nc.vector.tensor_copy(
+            out=mask_b[:].rearrange("p (r ma e) -> p r ma e", ma=8, e=2),
+            in_=mask_f[:].rearrange("p (r e ma) -> p r ma e", ma=8, e=2),
+        )
         perm_f = const.tile([P, P], F32, name="perm_f")
         for a in range(2):
             nc.vector.tensor_copy(
-                out=mask_b[:].rearrange("p (a r m e) -> p a r m e", a=2, m=4, e=2)[:, a],
-                in_=mask_f[:].rearrange("p (r e a m) -> p a r m e", e=2, a=2, m=4)[:, a],
-            )
-            nc.vector.tensor_copy(
                 out=perm_f[:].rearrange("p (a e r m) -> p a e r m", a=2, e=2, m=4)[:, a],
-                in_=ident_f[:].rearrange("p (r e a m) -> p a e r m", e=2, a=2, m=4)[:, a],
+                in_=ident_f[:].rearrange("p (r e m a) -> p a e r m", e=2, a=2, m=4)[:, a],
             )
 
         e_ring = {}
@@ -118,7 +118,7 @@ def tile_multiheadselfattention_pa_kernel(tc, q_proj, k_proj, x, w_v, out):
                 e_t = keep.tile([P, 512], BF16, name="e_%s_%d" % (kind, r), align_bytes=64)
                 words = e_t[:].bitcast(I32)
                 if kind == "whole3":
-                    nc.vector.memset(words.rearrange("p (a w) -> p a w", a=2)[:, :, 96:128], 0)
+                    nc.vector.memset(words[:, 192:256], 0)
                 e_ring.setdefault(kind, []).append(e_t)
 
         rs_ring = []
@@ -336,21 +336,17 @@ def tile_multiheadselfattention_pa_kernel(tc, q_proj, k_proj, x, w_v, out):
             h, g = slots[si]
             q_t, i = q_T[order.index((ib, h // 4))]
             diag = (g == ib // 4)
-            ncol = 64 * blocks(ib, g)
-            sc = ps_sc.tile([P, 2, 256], F32, name="sc", tag="sc")
+            ncol = P * blocks(ib, g)
+            sc = ps_sc.tile([P, 512], F32, name="sc", tag="sc")
             d0 = P * h + 64 * g
-            for a in range(2):
-                nc.tensor.matmul(
-                    out=sc[:, a, 0:ncol].rearrange("p (r m e) -> p m r e", m=4, e=2),
-                    lhsT=q_t[:, i, P * (h % 4):P * (h % 4) + P],
-                    rhs=k_sb[:, 4 * a:4 * a + 4, d0:d0 + ncol // 4].rearrange("p m (r e) -> p m r e", e=2),
-                    start=(a == 0), stop=(a == 1 and not diag),
-                )
+            nc.tensor.matmul(
+                out=sc[:, 0:ncol].rearrange("p (r m e) -> p m r e", m=8, e=2),
+                lhsT=q_t[:, i, P * (h % 4):P * (h % 4) + P],
+                rhs=k_sb[:, :, d0:d0 + ncol // 8].rearrange("p m (r e) -> p m r e", e=2),
+                start=True, stop=(not diag),
+            )
             if diag:
-                nc.tensor.matmul(
-                    out=sc[:, :, ncol - 64:ncol], lhsT=ident_b[:], rhs=mask_b[:].rearrange("p (a w) -> p a w", a=2),
-                    start=False, stop=True,
-                )
+                nc.tensor.matmul(out=sc[:, ncol - P:ncol], lhsT=ident_b[:], rhs=mask_b[:], start=False, stop=True)
             st[n]["sc"].append(sc)
 
         def row_max(n, si):
@@ -358,9 +354,9 @@ def tile_multiheadselfattention_pa_kernel(tc, q_proj, k_proj, x, w_v, out):
             if si == 0:
                 st[n]["m2"] = small.tile([P, 2], F32, name="m2", tag="m2")
             h, g = slots[si]
-            ncol = 64 * blocks(ib, g)
+            ncol = P * blocks(ib, g)
             nc.vector.tensor_reduce(
-                out=st[n]["m2"][:, si:si + 1], in_=st[n]["sc"][si][:, :, 0:ncol], axis=AX.XY, op=ALU.max,
+                out=st[n]["m2"][:, si:si + 1], in_=st[n]["sc"][si][:, 0:ncol], axis=AX.X, op=ALU.max,
             )
 
         def biases(n):
@@ -386,10 +382,10 @@ def tile_multiheadselfattention_pa_kernel(tc, q_proj, k_proj, x, w_v, out):
                 i = used.get(kind, 0)
                 used[kind] = i + 1
                 e_tiles[key] = e_ring[kind][i % len(e_ring[kind])]
-            e_out = e_tiles[key][:].rearrange("p (a s w) -> p a s w", a=2, s=share)[:, :, h % share, 0:64 * nblk]
+            c0 = 512 // share * (h % share)
             col = 0 if ib >= 4 else si
             nc.scalar.activation(
-                out=e_out, in_=st[n]["sc"][si][:, :, 0:64 * nblk], func=ACT.Exp,
+                out=e_tiles[key][:, c0:c0 + P * nblk], in_=st[n]["sc"][si][:, 0:P * nblk], func=ACT.Exp,
                 bias=st[n]["nm"][:, col:col + 1], scale=SCALE,
                 accum_out=sums_of(ib, h // 4)[:, 4 * (ib < 4) + h % 4, g:g + 1],
             )
@@ -403,7 +399,7 @@ def tile_multiheadselfattention_pa_kernel(tc, q_proj, k_proj, x, w_v, out):
                         st[n]["et"] = ps_aux.tile([P, 4, P], F32, name="et", tag="aux")
                     ew = e_tiles[key][:].bitcast(F32)
                     for a in range(2):
-                        nc.tensor.transpose(st[n]["et"][:, 2 * j + a, :], ew[:, P * a:P * a + P], ident_f[:])
+                        nc.tensor.transpose(st[n]["et"][:, 2 * j + a, :], ew[:, a:2 * P:2], ident_f[:])
 
         def exits(n):
             count = len(st[n]["parts"])
@@ -480,7 +476,7 @@ def tile_multiheadselfattention_pa_kernel(tc, q_proj, k_proj, x, w_v, out):
             hq = slots[-1][0] // 4
             o_sb = work.tile([P, 512], F32, name="o_sb", tag="o_sb", bufs=3)
             pv, rinv = quad[(ib, hq, "pv")], quad[(ib, hq, "rinv")]
-            if False:
+            if hq == 1 and ib in (7, 6):
                 for j in range(4):
                     nc.scalar.activation(out=o_sb[:, P * j:P * j + P], in_=pv[:, j, :], func=ACT.Copy, scale=rinv[:, j:j + 1])
             else:

@@ -140,11 +140,14 @@ def tile_multiheadselfattention_pa_kernel(tc, q_proj, k_proj, x, w_v, out):
         for share in (2, 4):
             part_codes = keep.tile([P, H, 2, P], U32, name="v_codes_%d" % share, align_bytes=64)
             part_scales = keep.tile([P, H, 2, P], U8, name="v_scales_%d" % share, align_bytes=64)
-            for h in range(H):
-                nc.gpsimd.memset(part_codes[:, h, :, :], 0)
-                nc.gpsimd.memset(part_scales[:, h, :, :].bitcast(U32), 0)
             v_part[share] = (part_codes, part_scales)
         held = {}
+
+        def zero_parts(share):
+            nc.vector.memset(v_part[share][0][:], 0)
+            nc.vector.memset(v_part[share][1][:].bitcast(U32), 0)
+
+        zero_parts(2)
 
         def x_tensor(g, b):
             xw = x4[2 * g + b // 2][:].bitcast(F32)
@@ -202,7 +205,7 @@ def tile_multiheadselfattention_pa_kernel(tc, q_proj, k_proj, x, w_v, out):
         def v_exit(h, g):
             if g == 0:
                 held[("gv", h)] = stage.tile([P, 1024], BF16, name="gv", tag="gv", align_bytes=64)
-            (nc.vector.tensor_copy if False else nc.scalar.copy)(
+            (nc.vector.tensor_copy if g == 1 and h < 2 else nc.scalar.copy)(
                 out=held[("gv", h)][:, 512 * g:512 * g + 512].rearrange("p (c t) -> p c t", t=4),
                 in_=held[("vp", h, g)][:].rearrange("p t c -> p c t"),
             )
@@ -476,7 +479,7 @@ def tile_multiheadselfattention_pa_kernel(tc, q_proj, k_proj, x, w_v, out):
             hq = slots[-1][0] // 4
             o_sb = work.tile([P, 512], F32, name="o_sb", tag="o_sb", bufs=3)
             pv, rinv = quad[(ib, hq, "pv")], quad[(ib, hq, "rinv")]
-            if hq == 1 and ib in (7, 6):
+            if False:
                 for j in range(4):
                     nc.scalar.activation(out=o_sb[:, P * j:P * j + P], in_=pv[:, j, :], func=ACT.Copy, scale=rinv[:, j:j + 1])
             else:
@@ -493,6 +496,7 @@ def tile_multiheadselfattention_pa_kernel(tc, q_proj, k_proj, x, w_v, out):
         with tc.manual_schedule():
             q_tensor(0, 1, 0, 2)
             q_exit(0, 1, 0, 2)
+            zero_parts(4)
             for k in range(-2, n_duos + 6):
                 run(exps, k, 0)
                 run(exps, k, 1)

@@ -100,6 +100,20 @@ def tile_multiheadselfattention_pa_kernel(tc, q_proj, k_proj, x, w_v, out):
         nc.vector.memset(warm[:], 0.0)
         warm2 = const.tile([P, 2], F32, name="warm2")
         nc.scalar.activation(out=warm2[:], in_=warm[:], func=ACT.Exp)
+        v_codes = keep.tile([P, H, 2, P], U32, name="v_codes", align_bytes=64)
+        v_scales = keep.tile([P, H, 2, P], U8, name="v_scales", align_bytes=64)
+        v_part = {1: (v_codes, v_scales)}
+        for share in (2, 4):
+            part_codes = keep.tile([P, H, 2, P], U32, name="v_codes_%d" % share, align_bytes=64)
+            part_scales = keep.tile([P, H, 2, P], U8, name="v_scales_%d" % share, align_bytes=64)
+            v_part[share] = (part_codes, part_scales)
+
+        def zero_part(share, h0, h1):
+            nc.vector.memset(v_part[share][0][:, h0:h1, :, :].bitcast(I32), 0)
+            nc.vector.memset(v_part[share][1][:, h0:h1, :, :].bitcast(I32), 0)
+
+        zero_part(2, 0, H)
+
         mask_b = const.tile([P, P], BF16, name="mask_b")
         nc.vector.tensor_copy(
             out=mask_b[:].rearrange("p (r ma e) -> p r ma e", ma=8, e=2),
@@ -118,7 +132,7 @@ def tile_multiheadselfattention_pa_kernel(tc, q_proj, k_proj, x, w_v, out):
                 e_t = keep.tile([P, 512], BF16, name="e_%s_%d" % (kind, r), align_bytes=64)
                 words = e_t[:].bitcast(I32)
                 if kind == "whole3":
-                    nc.vector.memset(words[:, 192:256], 0)
+                    nc.vector.memset(words.rearrange("p (a w) -> p a w", a=2)[:, :, 96:128], 0)
                 e_ring.setdefault(kind, []).append(e_t)
 
         rs_ring = []
@@ -134,20 +148,7 @@ def tile_multiheadselfattention_pa_kernel(tc, q_proj, k_proj, x, w_v, out):
         x_scales = keep.tile([P, 2, 2, 512], U8, name="x_scales", align_bytes=64)
         w_codes = keep.tile([P, 2, D], U32, name="w_codes", align_bytes=64)
         w_scales = keep.tile([P, 2, D], U8, name="w_scales", align_bytes=64)
-        v_codes = keep.tile([P, H, 2, P], U32, name="v_codes", align_bytes=64)
-        v_scales = keep.tile([P, H, 2, P], U8, name="v_scales", align_bytes=64)
-        v_part = {1: (v_codes, v_scales)}
-        for share in (2, 4):
-            part_codes = keep.tile([P, H, 2, P], U32, name="v_codes_%d" % share, align_bytes=64)
-            part_scales = keep.tile([P, H, 2, P], U8, name="v_scales_%d" % share, align_bytes=64)
-            v_part[share] = (part_codes, part_scales)
         held = {}
-
-        def zero_parts(share):
-            nc.vector.memset(v_part[share][0][:], 0)
-            nc.vector.memset(v_part[share][1][:].bitcast(U32), 0)
-
-        zero_parts(2)
 
         def x_tensor(g, b):
             xw = x4[2 * g + b // 2][:].bitcast(F32)
@@ -162,7 +163,7 @@ def tile_multiheadselfattention_pa_kernel(tc, q_proj, k_proj, x, w_v, out):
             if b == 0:
                 held[("gx", g)] = stage.tile([P, 4096], BF16, name="gx", tag="gx", align_bytes=64)
             gxw = held[("gx", g)][:].bitcast(F32).rearrange("p (ct b s u) -> p ct b s u", ct=8, b=4, u=2)
-            nc.scalar.copy(
+            (nc.vector.tensor_copy if g == 0 and b % 2 == 1 else nc.scalar.copy)(
                 out=gxw[:, :, b, :, :],
                 in_=held[("xt", g, b)][:].rearrange("p (u c) (t s) -> p (c t) s u", u=2, t=4),
             )
@@ -205,7 +206,7 @@ def tile_multiheadselfattention_pa_kernel(tc, q_proj, k_proj, x, w_v, out):
         def v_exit(h, g):
             if g == 0:
                 held[("gv", h)] = stage.tile([P, 1024], BF16, name="gv", tag="gv", align_bytes=64)
-            (nc.vector.tensor_copy if g == 1 and h < 2 else nc.scalar.copy)(
+            (nc.vector.tensor_copy if g == 1 and h % 2 == 0 else nc.scalar.copy)(
                 out=held[("gv", h)][:, 512 * g:512 * g + 512].rearrange("p (c t) -> p c t", t=4),
                 in_=held[("vp", h, g)][:].rearrange("p t c -> p c t"),
             )
@@ -385,10 +386,10 @@ def tile_multiheadselfattention_pa_kernel(tc, q_proj, k_proj, x, w_v, out):
                 i = used.get(kind, 0)
                 used[kind] = i + 1
                 e_tiles[key] = e_ring[kind][i % len(e_ring[kind])]
-            c0 = 512 // share * (h % share)
+            e_out = e_tiles[key][:].rearrange("p (a s x e) -> p a s x e", a=2, s=share, e=2)[:, :, h % share, 0:32 * nblk, :]
             col = 0 if ib >= 4 else si
             nc.scalar.activation(
-                out=e_tiles[key][:, c0:c0 + P * nblk], in_=st[n]["sc"][si][:, 0:P * nblk], func=ACT.Exp,
+                out=e_out, in_=st[n]["sc"][si][:, 0:P * nblk].rearrange("p (x a e) -> p a x e", a=2, e=2), func=ACT.Exp,
                 bias=st[n]["nm"][:, col:col + 1], scale=SCALE,
                 accum_out=sums_of(ib, h // 4)[:, 4 * (ib < 4) + h % 4, g:g + 1],
             )
@@ -402,7 +403,7 @@ def tile_multiheadselfattention_pa_kernel(tc, q_proj, k_proj, x, w_v, out):
                         st[n]["et"] = ps_aux.tile([P, 4, P], F32, name="et", tag="aux")
                     ew = e_tiles[key][:].bitcast(F32)
                     for a in range(2):
-                        nc.tensor.transpose(st[n]["et"][:, 2 * j + a, :], ew[:, a:2 * P:2], ident_f[:])
+                        nc.tensor.transpose(st[n]["et"][:, 2 * j + a, :], ew[:, P * a:P * a + P], ident_f[:])
 
         def exits(n):
             count = len(st[n]["parts"])
@@ -479,15 +480,14 @@ def tile_multiheadselfattention_pa_kernel(tc, q_proj, k_proj, x, w_v, out):
             hq = slots[-1][0] // 4
             o_sb = work.tile([P, 512], F32, name="o_sb", tag="o_sb", bufs=3)
             pv, rinv = quad[(ib, hq, "pv")], quad[(ib, hq, "rinv")]
-            if False:
-                for j in range(4):
-                    nc.scalar.activation(out=o_sb[:, P * j:P * j + P], in_=pv[:, j, :], func=ACT.Copy, scale=rinv[:, j:j + 1])
-            else:
+            step = 2 if n == n_duos - 1 else 4
+            for j in range(0, 4, step):
                 nc.vector.tensor_tensor(
-                    out=o_sb[:].rearrange("p (h c) -> p h c", h=4), in0=pv[:],
-                    in1=rinv.unsqueeze(2).to_broadcast([P, 4, P]), op=ALU.mult,
+                    out=o_sb[:, P * j:P * (j + step)].rearrange("p (h c) -> p h c", h=step), in0=pv[:, j:j + step, :],
+                    in1=rinv[:, j:j + step].unsqueeze(2).to_broadcast([P, step, P]), op=ALU.mult,
                 )
-            nc.sync.dma_start(out=o2[P * ib:P * ib + P, 512 * hq:512 * hq + 512], in_=o_sb[:])
+                c0 = 512 * hq + P * j
+                nc.sync.dma_start(out=o2[P * ib:P * ib + P, c0:c0 + P * step], in_=o_sb[:, P * j:P * (j + step)])
 
         def run(stage_fn, n, *more):
             if 0 <= n < n_duos:
@@ -496,7 +496,6 @@ def tile_multiheadselfattention_pa_kernel(tc, q_proj, k_proj, x, w_v, out):
         with tc.manual_schedule():
             q_tensor(0, 1, 0, 2)
             q_exit(0, 1, 0, 2)
-            zero_parts(4)
             for k in range(-2, n_duos + 6):
                 run(exps, k, 0)
                 run(exps, k, 1)
@@ -513,6 +512,8 @@ def tile_multiheadselfattention_pa_kernel(tc, q_proj, k_proj, x, w_v, out):
                 if k - 1 in pv_at:
                     finish(pv_at[k - 1])
                 side_part(k, 2)
+                if 1 <= k < 5:
+                    zero_part(4, 2 * (k - 1), 2 * (k - 1 + 1))
                 w_part(k, 1)
                 w_part(k, 0)
                 run(qk, k + 2, 0)

from contextlib import ExitStack
from functools import partial

import concourse.mybir as mybir
from concourse.masks import make_identity

F32 = mybir.dt.float32
BF16 = mybir.dt.bfloat16
U32 = mybir.dt.uint32
U8 = mybir.dt.uint8
I32 = mybir.dt.int32
FP8X4 = mybir.dt.float8_e4m3fn_x4
ALU = mybir.AluOpType
ACT = mybir.ActivationFunctionType
AX = mybir.AxisListType

P = 128
S = 1024
D = 1024
H = 8
SCALE = 128.0 ** -0.5
NEG = -(2.0 ** 40)
FLOPS = 2 * S * D * D + 2 * (2 * H * (512 * 512 + 512 * 1024) * 128)

N_CODES = 34
SIDE_STEP = -2


def tile_multiheadselfattention_pa_kernel(tc, q_proj, k_proj, x, w_v, out):
    nc = tc.nc
    q2 = q_proj.rearrange("b s d -> (b s) d")
    k2 = k_proj.rearrange("b s d -> (b s) d")
    x2 = x.rearrange("b s d -> (b s) d")
    o2 = out.rearrange("b s d -> (b s) d")

    with ExitStack() as ctx:
        const = ctx.enter_context(tc.tile_pool(name="const", bufs=1))
        keep = ctx.enter_context(tc.tile_pool(name="keep", bufs=1))
        stage = ctx.enter_context(tc.tile_pool(name="stage", bufs=2))
        work = ctx.enter_context(tc.tile_pool(name="work", bufs=4))
        small = ctx.enter_context(tc.tile_pool(name="small", bufs=6))
        ps_sc = ctx.enter_context(tc.psum_pool(name="ps_sc", bufs=5))
        ps_aux = ctx.enter_context(tc.psum_pool(name="ps_aux", bufs=3))

        k_sb = keep.tile([P, 8, D], BF16, name="k_sb")
        w_raw = keep.tile([P, 8, D], BF16, name="w_raw")
        q_sb = keep.tile([P, 8, D], BF16, name="q_sb")
        x4 = {}

        def load_k(c0, c1):
            for j in range(2):
                nc.sync.dma_start(
                    out=k_sb[:, 4 * j:4 * j + 4, c0:c1],
                    in_=k2[512 * j:512 * j + 512, c0:c1].rearrange("(m p) d -> p m d", p=P),
                )

        def load_q(ibs, c0, c1):
            nc.sync.dma_start(out=q_sb[:, ibs, c0:c1], in_=q2[:, c0:c1].rearrange("(i p) c -> p i c", p=P)[:, ibs, :])

        def load_w(c0, c1):
            for cu in range(4):
                nc.sync.dma_start(
                    out=w_raw[:, 2 * cu:2 * cu + 2, c0:c1],
                    in_=w_v[256 * cu:256 * cu + 256, c0:c1].rearrange("(p e) n -> p e n", e=2),
                )

        def load_x(gu):
            x4[gu] = keep.tile([P, 2048], BF16, name="x4_%d" % gu)
            nc.sync.dma_start(
                out=x4[gu][:].rearrange("p (b k) -> p b k", b=2),
                in_=x2[256 * gu:256 * gu + 256, :].rearrange("(b p) k -> p b k", p=P),
            )

        load_q(slice(7, 8), 0, 256)
        load_k(0, 256)
        load_q(slice(7, 8), 256, 512)
        load_k(256, 512)
        load_q(slice(3, 7, 3), 0, 512)
        for gu in range(4):
            load_x(gu)
        load_w(0, D)
        load_q(slice(2, 6, 3), 0, D)
        load_q(slice(1, 5, 3), 0, D)
        load_q(slice(0, 1), 0, D)
        load_k(512, D)
        load_q(slice(7, 8), 512, D)
        load_q(slice(3, 7, 3), 512, D)

        ident_f = const.tile([P, P], F32, name="ident_f")
        make_identity(nc, ident_f[:])
        ident_b = const.tile([P, P], BF16, name="ident_b")
        make_identity(nc, ident_b[:])
        mask_f = const.tile([P, P], F32, name="mask_f")
        nc.gpsimd.memset(mask_f[:], 0.0)
        nc.gpsimd.affine_select(
            out=mask_f[:], in_=mask_f[:], compare_op=ALU.is_ge, fill=NEG,
            base=0, pattern=[[-1, P]], channel_multiplier=1,
        )
        warm = const.tile([P, 2], F32, name="warm")
        nc.vector.memset(warm[:], 0.0)
        warm2 = const.tile([P, 2], F32, name="warm2")
        nc.scalar.activation(out=warm2[:], in_=warm[:], func=ACT.Exp)
        v_codes = keep.tile([P, H, 2, P], U32, name="v_codes", align_bytes=64)
        v_scales = keep.tile([P, H, 2, P], U8, name="v_scales", align_bytes=64)
        v_part = {1: (v_codes, v_scales)}
        for share in (2, 4):
            part_codes = keep.tile([P, H, 2, P], U32, name="v_codes_%d" % share, align_bytes=64)
            part_scales = keep.tile([P, H, 2, P], U8, name="v_scales_%d" % share, align_bytes=64)
            v_part[share] = (part_codes, part_scales)

        def zero_part(share, h0, h1):
            nc.vector.memset(v_part[share][0][:, h0:h1, :, :].bitcast(I32), 0)
            nc.vector.memset(v_part[share][1][:, h0:h1, :, :].bitcast(I32), 0)

        zero_part(2, 0, H)

        mask_b = const.tile([P, P], BF16, name="mask_b")
        nc.vector.tensor_copy(
            out=mask_b[:].rearrange("p (r ma e) -> p r ma e", ma=8, e=2),
            in_=mask_f[:].rearrange("p (r e ma) -> p r ma e", ma=8, e=2),
        )
        perm_f = const.tile([P, P], F32, name="perm_f")
        for a in range(2):
            nc.vector.tensor_copy(
                out=perm_f[:].rearrange("p (a e r m) -> p a e r m", a=2, e=2, m=4)[:, a],
                in_=ident_f[:].rearrange("p (r e m a) -> p a e r m", e=2, a=2, m=4)[:, a],
            )

        e_ring = {}
        for kind, count in (("whole4", 4), ("whole3", 4), ("half", 2), ("quarter", 2)):
            for r in range(count):
                e_t = keep.tile([P, 512], BF16, name="e_%s_%d" % (kind, r), align_bytes=64)
                words = e_t[:].bitcast(I32)
                if kind == "whole3":
                    nc.vector.memset(words.rearrange("p (a w) -> p a w", a=2)[:, :, 96:128], 0)
                e_ring.setdefault(kind, []).append(e_t)

        rs_ring = []
        for r in range(4):
            rs_t = keep.tile([P, 8, 2], F32, name="rs_%d" % r)
            nc.vector.memset(rs_t[:], 0.0)
            rs_ring.append(rs_t)

        def sums_of(ib, hq):
            return rs_ring[(4 * hq + 3 - ib % 4) % 4]

        x_codes = keep.tile([P, 2, 2, 512], U32, name="x_codes", align_bytes=64)
        x_scales = keep.tile([P, 2, 2, 512], U8, name="x_scales", align_bytes=64)
        w_codes = keep.tile([P, 2, D], U32, name="w_codes", align_bytes=64)
        w_scales = keep.tile([P, 2, D], U8, name="w_scales", align_bytes=64)
        held = {}

        def x_tensor(g, b):
            xw = x4[2 * g + b // 2][:].bitcast(F32)
            xt = ps_aux.tile([P, 4, P], F32, name="xt", tag="aux")
            for c in range(2):
                for u in range(2):
                    c0 = 512 * (b % 2) + 256 * c + P * u
                    nc.tensor.transpose(xt[:, 2 * u + c, :], xw[:, c0:c0 + P], perm_f[:])
            held[("xt", g, b)] = xt

        def x_exit(g, b):
            if b == 0:
                held[("gx", g)] = stage.tile([P, 4096], BF16, name="gx", tag="gx", align_bytes=64)
            gxw = held[("gx", g)][:].bitcast(F32).rearrange("p (ct b s u) -> p ct b s u", ct=8, b=4, u=2)
            (nc.vector.tensor_copy if g == 0 and b % 2 == 1 else nc.scalar.copy)(
                out=gxw[:, :, b, :, :],
                in_=held[("xt", g, b)][:].rearrange("p (u c) (t s) -> p (c t) s u", u=2, t=4),
            )

        def x_quantise(g):
            for c in range(2):
                nc.vector.quantize_mx(
                    out=x_codes[:, g, c, :].bitcast(FP8X4), scales=x_scales[:, g, c, :],
                    in_=held[("gx", g)][:, 2048 * c:2048 * c + 2048],
                )

        def w_regroup(c, n0):
            gw = stage.tile([P, 2048], BF16, name="gw", tag="gw", align_bytes=64)
            held[("gw", c, n0)] = gw
            nc.vector.tensor_copy(
                out=gw[:].rearrange("p (c i t) -> p c t i", i=4, t=4),
                in_=w_raw[:, 4 * c:4 * c + 4, n0:n0 + 512].rearrange("p t (c i) -> p c t i", i=4),
            )

        def w_quantise(c, n0):
            nc.vector.quantize_mx(
                out=w_codes[:, c, n0:n0 + 512].bitcast(FP8X4),
                scales=w_scales[:, c, n0:n0 + 512], in_=held[("gw", c, n0)][:],
            )

        def v_tensor(h, g):
            vp = ps_aux.tile([P, 4, P], F32, name="vp", tag="aux")
            for t in range(4):
                for c in range(2):
                    nc.tensor.matmul_mx(
                        out=vp[:, t, :],
                        lhsT=x_codes[:, g, c, P * t:P * t + P].bitcast(FP8X4),
                        lhsT_scale=x_scales[:, g, c, P * t:P * t + P],
                        rhs=w_codes[:, c, P * h:P * h + P].bitcast(FP8X4),
                        rhs_scale=w_scales[:, c, P * h:P * h + P],
                        start=(c == 0), stop=(c == 1),
                    )
            held[("vp", h, g)] = vp

        def v_exit(h, g):
            if g == 0:
                held[("gv", h)] = stage.tile([P, 1024], BF16, name="gv", tag="gv", align_bytes=64)
            (nc.vector.tensor_copy if g == 1 and h % 2 == 0 else nc.scalar.copy)(
                out=held[("gv", h)][:, 512 * g:512 * g + 512].rearrange("p (c t) -> p c t", t=4),
                in_=held[("vp", h, g)][:].rearrange("p t c -> p c t"),
            )

        def v_quantise(h):
            nc.vector.quantize_mx(
                out=v_codes[:, h, :, :].rearrange("p g c -> p (g c)").bitcast(FP8X4),
                scales=v_scales[:, h, :, :].rearrange("p g c -> p (g c)"), in_=held[("gv", h)][:],
            )
            if h % 4 == 3:
                v_parts(h // 4)

        def v_parts(hq):
            for share in (2, 4):
                live = P // share
                for i in range(share):
                    for whole, part, rows in (
                        (v_codes, v_part[share][0], [(0, live)]),
                        (v_scales, v_part[share][1], [(r, r + 4) for r in range(0, live, 32)]),
                    ):
                        for r0, r1 in rows:
                            src = whole[r0:r1, 4 * hq + i:4 * hq + 4:share, :, :].rearrange("p j g c -> p j (g c)")
                            dst = part[live * i + r0:live * i + r1, 4 * hq + i:4 * hq + 4:share, :, :].rearrange("p j g c -> p j (g c)")
                            nc.sync.dma_start(out=dst.bitcast(I32), in_=src.bitcast(I32))

        order = [(ib - d, hq) for hq in range(2) for ib in range(7, 3, -1) for d in (0, 4)]
        q_T = {}
        for i0, i1 in [(0, 1)] + [(i, i + 2) for i in range(1, 15, 2)] + [(15, 16)]:
            q_t = keep.tile([P, i1 - i0, 512], BF16, name="q_T_%d" % i0)
            for i in range(i0, i1):
                q_T[i] = (q_t, i - i0)

        def q_tensor(i0, i1, h0, h1):
            qt = ps_aux.tile([P, 2, 4, P], BF16, name="qt", tag="aux")
            for i in range(i0, i1):
                ib, hq = order[i]
                for h in range(h0, h1):
                    c0 = 512 * hq + P * h
                    nc.tensor.transpose(qt[:, i - i0, h, :], q_sb[:, ib, c0:c0 + P], ident_b[:])
            held[("qt", i0, h0)] = qt

        def q_exit(i0, i1, h0, h1):
            n = (i1 - i0) * (h1 - h0) * P
            (nc.scalar.copy if False else nc.vector.tensor_copy)(
                out=q_T[i0][0][:].rearrange("p i c -> p (i c)")[:, P * h0:P * h0 + n],
                in_=held[("qt", i0, h0)][:].rearrange("p i h c -> p (i h c)")[:, P * h0:P * h0 + n],
            )

        side = []
        PAUSE = (None, None, None)

        def q_side(i0, i1, h0=0, h1=4):
            side.append((partial(q_tensor, i0, i1, h0, h1), partial(q_exit, i0, i1, h0, h1), None))

        def x_side(g, b):
            side.append((partial(x_tensor, g, b), partial(x_exit, g, b), partial(x_quantise, g) if b == 3 else None))

        def v_side(h, g):
            side.append((partial(v_tensor, h, g), partial(v_exit, h, g), partial(v_quantise, h) if g == 1 else None))

        q_side(0, 1, 2, 4)
        q_side(1, 3)
        x_side(0, 0)
        x_side(0, 1)
        x_side(0, 2)
        x_side(0, 3)
        x_side(1, 0)
        q_side(3, 5)
        for b in range(1, 4):
            x_side(1, b)
        for h in range(2):
            for g in range(2):
                v_side(h, g)
        q_side(5, 7)
        for h in range(2, 4):
            for g in range(2):
                v_side(h, g)
        V_LOW = SIDE_STEP + len(side) + 1
        q_side(7, 9)
        for h in range(4, 8):
            for g in range(2):
                if h >= 7:
                    side.append(PAUSE)
                v_side(h, g)
            if h == 5:
                q_side(9, 11)
            if h == 6:
                q_side(11, 13)
        V_ALL = SIDE_STEP + len(side) + 1
        side.extend([PAUSE] * 3)
        q_side(13, 15)
        side.extend([PAUSE] * 5)
        q_side(15, 16)

        w_parts = {6: (0, 0), 8: (1, 0), 14: (0, 512), 16: (1, 512)}

        def side_part(k, part):
            i = k - part - SIDE_STEP
            if 0 <= i < len(side) and side[i][part] is not None:
                side[i][part]()

        def w_part(k, part):
            if k - part in w_parts:
                (w_regroup if part == 0 else w_quantise)(*w_parts[k - part])

        duos = []
        for hq in range(2):
            for ib in range(7, 3, -1):
                for h in range(4 * hq, 4 * hq + 4):
                    duos.append((ib, [(h, 0), (h, 1)]))
                for h in range(4 * hq, 4 * hq + 4, 2):
                    duos.append((ib - 4, [(h, 0), (h + 1, 0)]))
        n_duos = len(duos)
        st = [{"parts": [], "sc": []} for n in range(n_duos)]
        quad = {}
        used = {}
        e_tiles = {}
        codes = {}

        def blocks(ib, g):
            return (ib % 4 + 1) if g == ib // 4 else 4

        def sharing(ib, g):
            return {1: 4, 2: 2, 3: 1, 4: 1}[blocks(ib, g)]

        def e_key(ib, h, g):
            return (ib, h - h % sharing(ib, g), g)

        def qk(n, si):
            ib, slots = duos[n]
            h, g = slots[si]
            q_t, i = q_T[order.index((ib, h // 4))]
            diag = (g == ib // 4)
            ncol = P * blocks(ib, g)
            sc = ps_sc.tile([P, 512], F32, name="sc", tag="sc")
            d0 = P * h + 64 * g
            nc.tensor.matmul(
                out=sc[:, 0:ncol].rearrange("p (r m e) -> p m r e", m=8, e=2),
                lhsT=q_t[:, i, P * (h % 4):P * (h % 4) + P],
                rhs=k_sb[:, :, d0:d0 + ncol // 8].rearrange("p m (r e) -> p m r e", e=2),
                start=True, stop=(not diag),
            )
            if diag:
                nc.tensor.matmul(out=sc[:, ncol - P:ncol], lhsT=ident_b[:], rhs=mask_b[:], start=False, stop=True)
            st[n]["sc"].append(sc)

        def row_max(n, si):
            ib, slots = duos[n]
            if si == 0:
                st[n]["m2"] = small.tile([P, 2], F32, name="m2", tag="m2")
            h, g = slots[si]
            ncol = P * blocks(ib, g)
            nc.vector.tensor_reduce(
                out=st[n]["m2"][:, si:si + 1], in_=st[n]["sc"][si][:, 0:ncol], axis=AX.X, op=ALU.max,
            )

        def biases(n):
            ib, slots = duos[n]
            m2 = st[n]["m2"]
            nm = small.tile([P, 2], F32, name="nm", tag="nm")
            if ib >= 4:
                nc.vector.tensor_scalar(
                    out=nm[:, 0:1], in0=m2[:, 0:1], scalar1=m2[:, 1:2], scalar2=-SCALE, op0=ALU.max, op1=ALU.mult,
                )
            else:
                nc.vector.tensor_scalar(out=nm[:], in0=m2[:], scalar1=-SCALE, scalar2=None, op0=ALU.mult)
            st[n]["nm"] = nm

        def exps(n, si):
            ib, slots = duos[n]
            h, g = slots[si]
            nblk = blocks(ib, g)
            share = sharing(ib, g)
            key = e_key(ib, h, g)
            if key not in e_tiles:
                kind = ("quarter", "half", "whole3", "whole4")[nblk - 1]
                i = used.get(kind, 0)
                used[kind] = i + 1
                e_tiles[key] = e_ring[kind][i % len(e_ring[kind])]
            e_out = e_tiles[key][:].rearrange("p (a s x e) -> p a s x e", a=2, s=share, e=2)[:, :, h % share, 0:32 * nblk, :]
            col = 0 if ib >= 4 else si
            nc.scalar.activation(
                out=e_out, in_=st[n]["sc"][si][:, 0:P * nblk].rearrange("p (x a e) -> p a x e", a=2, e=2), func=ACT.Exp,
                bias=st[n]["nm"][:, col:col + 1], scale=SCALE,
                accum_out=sums_of(ib, h // 4)[:, 4 * (ib < 4) + h % 4, g:g + 1],
            )
            if h % share == share - 1:
                st[n]["parts"].append((si, key))

        def transposes(n, si):
            for j, (sj, key) in enumerate(st[n]["parts"]):
                if sj == si:
                    if j == 0:
                        st[n]["et"] = ps_aux.tile([P, 4, P], F32, name="et", tag="aux")
                    ew = e_tiles[key][:].bitcast(F32)
                    for a in range(2):
                        nc.tensor.transpose(st[n]["et"][:, 2 * j + a, :], ew[:, P * a:P * a + P], ident_f[:])

        def exits(n):
            count = len(st[n]["parts"])
            if count == 0:
                return
            ge = work.tile([P, 1024], BF16, name="ge", tag="ge", align_bytes=64, bufs=3)
            nc.scalar.copy(
                out=ge[:].bitcast(F32)[:, 0:256 * count].rearrange("p (s i a) -> p s i a", s=count, a=2),
                in_=st[n]["et"][:, 0:2 * count, :].rearrange("p (s a) i -> p s i a", a=2),
            )
            st[n]["ge"] = ge

        def quantise(n):
            count = len(st[n]["parts"])
            if count == 0:
                return
            e_codes = work.tile([P, 2 * P], U32, name="e_codes", tag="e_codes", align_bytes=64, bufs=N_CODES)
            e_scales = work.tile([P, 2 * P], U8, name="e_scales", tag="e_scales", align_bytes=64, bufs=N_CODES)
            nc.vector.quantize_mx(
                out=e_codes[:, 0:P * count].bitcast(FP8X4), scales=e_scales[:, 0:P * count], in_=st[n]["ge"][:, 0:512 * count],
            )
            for j, (sj, key) in enumerate(st[n]["parts"]):
                codes[key] = (e_codes[:, P * j:P * j + P], e_scales[:, P * j:P * j + P])

        def quad_end(n):
            return 0 <= n < n_duos and duos[n][1][-1][0] % 4 == 3

        pv_at = {}
        waiting = [n for n in range(n_duos) if quad_end(n)]
        for k in range(n_duos + 5):
            ready = [n for n in waiting if k >= n + 4 and k >= (V_LOW if duos[n][1][-1][0] < 4 else V_ALL)]
            if ready and (k - SIDE_STEP >= len(side) or side[k - SIDE_STEP] == PAUSE):
                pv_at[k] = ready[0]
                waiting.remove(ready[0])

        def pv_passes(n_last):
            ib, slots = duos[n_last]
            hq = slots[-1][0] // 4
            pv = ps_aux.tile([P, 4, P], F32, name="pv", tag="aux")
            quad[(ib, hq, "pv")] = pv
            for h in range(4 * hq, 4 * hq + 4):
                for g in range(ib // 4 + 1):
                    e_codes, e_scales = codes[e_key(ib, h, g)]
                    part_codes, part_scales = v_part[sharing(ib, g)]
                    nc.tensor.matmul_mx(
                        out=pv[:, h % 4, :],
                        lhsT=e_codes.bitcast(FP8X4),
                        lhsT_scale=e_scales,
                        rhs=part_codes[:, h, g, :].bitcast(FP8X4),
                        rhs_scale=part_scales[:, h, g, :],
                        start=(g == 0), stop=(g == ib // 4),
                    )

        def row_sums(n):
            ib, slots = duos[n]
            hq = slots[-1][0] // 4
            if ib < 4:
                rs = sums_of(ib, hq)
                rsum = small.tile([P, 8], F32, name="rsum", tag="rsum")
                nc.vector.tensor_tensor(out=rsum[:], in0=rs[:, :, 0], in1=rs[:, :, 1], op=ALU.add)
                quad[(ib, hq, "rsum")] = rsum

        def reciprocals(n):
            ib, slots = duos[n]
            hq = slots[-1][0] // 4
            if ib < 4:
                rinv = small.tile([P, 8], F32, name="rinv", tag="rinv", bufs=8)
                nc.vector.reciprocal(out=rinv[:], in_=quad[(ib, hq, "rsum")][:])
                quad[(ib + 4, hq, "rinv")] = rinv[:, 0:4]
                quad[(ib, hq, "rinv")] = rinv[:, 4:8]

        def finish(n):
            ib, slots = duos[n]
            hq = slots[-1][0] // 4
            o_sb = work.tile([P, 512], F32, name="o_sb", tag="o_sb", bufs=3)
            pv, rinv = quad[(ib, hq, "pv")], quad[(ib, hq, "rinv")]
            step = 2 if n == n_duos - 1 else 4
            for j in range(0, 4, step):
                nc.vector.tensor_tensor(
                    out=o_sb[:, P * j:P * (j + step)].rearrange("p (h c) -> p h c", h=step), in0=pv[:, j:j + step, :],
                    in1=rinv[:, j:j + step].unsqueeze(2).to_broadcast([P, step, P]), op=ALU.mult,
                )
                c0 = 512 * hq + P * j
                nc.sync.dma_start(out=o2[P * ib:P * ib + P, c0:c0 + P * step], in_=o_sb[:, P * j:P * (j + step)])

        def run(stage_fn, n, *more):
            if 0 <= n < n_duos:
                stage_fn(n, *more)

        with tc.manual_schedule():
            q_tensor(0, 1, 0, 2)
            q_exit(0, 1, 0, 2)
            for k in range(-2, n_duos + 6):
                run(exps, k, 0)
                run(exps, k, 1)
                run(exits, k - 1)
                run(row_max, k + 1, 0)
                run(row_max, k + 1, 1)
                run(quantise, k - 2)
                if quad_end(k - 1):
                    row_sums(k - 1)
                if quad_end(k - 2):
                    reciprocals(k - 2)
                run(biases, k + 1)
                side_part(k, 1)
                if k - 1 in pv_at:
                    finish(pv_at[k - 1])
                side_part(k, 2)
                if 1 <= k < 5:
                    zero_part(4, 2 * (k - 1), 2 * (k - 1 + 1))
                w_part(k, 1)
                w_part(k, 0)
                run(qk, k + 2, 0)
                run(transposes, k, 0)
                run(qk, k + 2, 1)
                run(transposes, k, 1)
                side_part(k, 0)
                if k in pv_at:
                    pv_passes(pv_at[k])
